import numpy as np
import ml_dtypes


def mxq(x, axis, fmt="e4m3"):
    dtype, down = {"e4m3": (ml_dtypes.float8_e4m3fn, 7), "e5m2": (ml_dtypes.float8_e5m2, 14)}[fmt]
    v = np.moveaxis(np.asarray(x, np.float32).astype(ml_dtypes.bfloat16).astype(np.float64), axis, -1)
    blocks = v.reshape(v.shape[:-1] + (-1, 32))
    amax = np.abs(blocks).max(-1, keepdims=True)
    byte = np.maximum(np.where(amax > 0, np.frexp(amax)[1] - 1 + 127, 0) - down, 1)
    scale = np.exp2(byte - 127.0)
    codes = (blocks / scale).astype(np.float32).astype(dtype).astype(np.float64)
    return np.moveaxis((codes * scale).reshape(v.shape), -1, axis)


WIDE = False


def mx_kscale(k):
    if not WIDE:
        return np.ones(k)
    levels = np.array([18, -18])
    if k % 512:
        return np.exp2(np.random.permutation(np.resize(levels, k // 32))).repeat(32)
    a = np.empty((k // 512, 16))
    for p in range(k // 512):
        a[p, :8] = np.random.permutation(np.resize(levels, 8))
        for g in range(8):
            far = levels[np.abs(levels - a[p, g]) >= 10]
            a[p, g + 8] = far[np.random.randint(len(far))]
    return np.exp2(a.ravel()).repeat(32)


BF16 = ml_dtypes.bfloat16


def bf(x):
    return np.asarray(x, np.float32).astype(BF16)


def f64(x):
    return np.asarray(x).astype(np.float64)


N, C, F, O, DEG = 2048, 512, 512, 40, 16


def draw_adj():
    hit = (np.random.random((N, N)) < 0.5 * DEG / N).astype(np.float64)
    wt = 0.5 + np.random.random((N, N))
    return np.clip(hit + hit.T + np.eye(N), 0.0, 1.0) * (wt + wt.T) * 0.5


def setup_inputs():
    u = mx_kscale(N)
    s = mx_kscale(N)
    v = mx_kscale(F)
    t = np.cbrt(u * u * s)
    h0 = bf(np.maximum(np.random.standard_normal((N, F)) * 3.4, 0.0))
    adj0 = bf(draw_adj())
    w0 = bf(np.random.standard_normal((F, F)) * 0.5 * DEG / np.sqrt(F))
    rw0 = bf(np.random.standard_normal((F, F)) * 0.5 / np.sqrt(F))
    b = bf(np.random.standard_normal(F) * 0.3)
    g = bf(np.random.standard_normal((N, F)) * np.exp2(np.random.randint(-6, 1, (N, 1))) * 4.0 / t[:, None] * v)
    a = f64(adj0)
    dis = np.sum(a, axis=1) ** -0.5
    nnz = np.maximum(np.sum(np.where(a > 0.0, 1.0, 0.0), axis=1), 1.0)
    agg = ((dis[:, None] * a * dis[None, :]) @ f64(h0)) / nnz[:, None]
    y = agg @ f64(w0) + f64(h0) @ f64(rw0) + f64(b)
    return {"h": bf(f64(h0) * t[:, None]),
            "adj": bf(a * t[:, None] / t[None, :]),
            "w": bf(f64(w0) / v),
            "rw": bf(f64(rw0) / v),
            "b": b,
            "y": np.asarray(y, np.float32),
            "dis": np.asarray(dis, np.float32),
            "nnz": np.asarray(nnz, np.float32),
            "grad_out": g}


def reference(h, adj, w, rw, b, y, dis, nnz, grad_out):
    dis, nnz = f64(dis), f64(nnz)
    dy = f64(grad_out) * np.where(f64(y) > 0.0, 1.0, 0.0)
    dz2 = dy * (dis / nnz)[:, None]
    da = mxq(f64(adj), 0, "e4m3").T @ mxq(dz2, 0, "e5m2")
    dp = da * dis[:, None]
    dz1 = np.concatenate([dp, dy], axis=1)
    wr = np.concatenate([f64(w), f64(rw)], axis=1)
    dh = mxq(dz1, 1, "e5m2") @ mxq(wr, 1, "e4m3").T
    dw = mxq(f64(h), 0, "e4m3").T @ mxq(dp, 0, "e5m2")
    return dh, dw

@@ -1,0 +1,320 @@
+from contextlib import ExitStack
+
+import concourse.mybir as mybir
+from concourse.masks import make_identity
+
+F32 = mybir.dt.float32
+BF16 = mybir.dt.bfloat16
+U32 = mybir.dt.uint32
+U8 = mybir.dt.uint8
+E4M3 = mybir.dt.float8_e4m3fn_x4
+E5M2 = mybir.dt.float8_e5m2_x4
+ALU = mybir.AluOpType
+COPY = mybir.ActivationFunctionType.Copy
+
+N, F = 2048, 512
+P, J = 128, 4
+GROUP = P * J
+G = N // GROUP
+HALF = 1024
+
+FLOPS = 2 * N * N * F + 2 * N * 2 * F * F + 2 * N * F * F
+BYTES = 2 * (N * F + N * N + 2 * F * F + N * F) + 4 * (N * F + 2 * N) + 4 * (N * F + F * F)
+
+
+def tile_sage_re_pb_v_kernel(tc, h, adj, w, rw, b, y, dis, nnz, grad_out, out_0, out_1):
+    nc = tc.nc
+    adj_v = adj.rearrange("(g p j) c -> g p j c", p=P, j=J)
+    y_v = y.rearrange("(g p j) o -> g p j o", p=P, j=J)
+    go_v = grad_out.rearrange("(g p j) o -> g p j o", p=P, j=J)
+    h_v = h.rearrange("(g p j) o -> g p j o", p=P, j=J)
+    w_v = [x.rearrange("(b p) o -> p b o", p=P) for x in (w, rw)]
+    out0_v = out_0.rearrange("(g p j) f -> g p j f", p=P, j=J)
+    out1_v = out_1.rearrange("(b p) f -> p b f", p=P)
+
+    with ExitStack() as ctx:
+        keep = ctx.enter_context(tc.tile_pool(name="keep", bufs=1))
+        work = ctx.enter_context(tc.tile_pool(name="work", bufs=2))
+        psum = ctx.enter_context(tc.psum_pool(name="psum", bufs=1))
+        ctx.enter_context(tc.manual_schedule())
+
+        ident = keep.tile([P, P], F32, name="ident")
+        make_identity(nc, ident[:])
+        dis_t = keep.tile([P, G, J], F32, name="dis_t")
+        nnz_t = keep.tile([P, G, J], F32, name="nnz_t")
+        rinv = keep.tile([P, G, J], F32, name="rinv")
+        ratio = keep.tile([P, G, J], F32, name="ratio")
+
+        y_t, go_t, adj_t, h_t, w_t = {}, {}, {}, {}, {}
+        dy, dz = {}, {}
+        dp_t = {}
+        grp = {}
+        codes = {}
+        bank = {}
+
+        def coded(key, bufs=None, tag=None):
+            c = (keep if bufs is None else work).tile([P, GROUP], U32, name="c_%s" % key, tag=tag or "c_%s" % key, align_bytes=256, bufs=bufs or 1)
+            s = (keep if bufs is None else work).tile([P, GROUP], U8, name="s_%s" % key, tag="s_" + (tag or key), align_bytes=256, bufs=bufs or 1)
+            codes[key] = (c, s)
+
+        def new_group(key):
+            grp[key] = work.tile([P, J * GROUP], BF16, name="g_%s" % key, tag="grp", align_bytes=256, bufs=8)
+            return grp[key]
+
+        def new_bank(i):
+            return psum.tile([P, 512], F32, name="bank%d" % i, tag="bank%d" % i)
+
+        def load_y(g, k):
+            t = work.tile([P, 2, F], F32, name="y_%d_%d" % (g, k), tag="y", bufs=4)
+            nc.sync.dma_start(out=t[:], in_=y_v[g][:, 2 * k : 2 * k + 2, :])
+            y_t[g, k] = t
+
+        def load_go(g, k):
+            t = work.tile([P, 2, F], BF16, name="go_%d_%d" % (g, k), tag="go", bufs=4)
+            nc.sync.dma_start(out=t[:], in_=go_v[g][:, 2 * k : 2 * k + 2, :])
+            go_t[g, k] = t
+
+        def load_h(g):
+            t = work.tile([P, J, F], BF16, name="h_%d" % g, tag="rows", bufs=7)
+            nc.sync.dma_start(out=t[:], in_=h_v[g])
+            h_t[g] = t
+
+        def load_w(i):
+            t = work.tile([P, J, F], BF16, name="w_%d" % i, tag="rows", bufs=7)
+            nc.sync.dma_start(out=t[:], in_=w_v[i])
+            w_t[i] = t
+
+        def load_adj(hf, g):
+            t = work.tile([P, J, HALF], BF16, name="adj_%d_%d" % (hf, g), tag="adj", bufs=4)
+            nc.sync.dma_start(out=t[:], in_=adj_v[g][:, :, hf * HALF : (hf + 1) * HALF])
+            for k in range(2):
+                adj_t[2 * hf + k, g] = t[:, :, k * GROUP : (k + 1) * GROUP]
+
+        def load_adj_quarter(q, g):
+            t = work.tile([P, J, GROUP], BF16, name="adjq_%d_%d" % (q, g), tag="rows", bufs=7)
+            nc.sync.dma_start(out=t[:], in_=adj_v[g][:, :, q * GROUP : (q + 1) * GROUP])
+            adj_t[q, g] = t[:]
+
+
+        def mask(g, k):
+            if k == 0:
+                dy[g] = work.tile([P, J, F], BF16, name="dy_%d" % g, tag="dy", bufs=2, align_bytes=64)
+            pair = slice(2 * k, 2 * k + 2)
+            nc.vector.scalar_tensor_tensor(out=dy[g][:, pair, :], in0=y_t[g, k][:], scalar=0.0, in1=go_t[g, k][:], op0=ALU.is_gt, op1=ALU.mult)
+
+        def scale(g, t):
+            if t == 0:
+                dz[g] = work.tile([P, J, F], BF16, name="dz_%d" % g, tag="dz", bufs=2, align_bytes=64)
+            nc.vector.tensor_scalar(out=dz[g][:, t, :], in0=dy[g][:, t, :], scalar1=ratio[:, g, t : t + 1], scalar2=None, op0=ALU.mult)
+
+        def copy_on(engine, out, in_):
+            if engine == "V":
+                nc.vector.tensor_copy(out=out, in_=in_)
+            else:
+                nc.scalar.copy(out=out, in_=in_)
+
+        def group_rows(engine, key, src):
+            copy_on(engine, new_group(key)[:].rearrange("p (c i t) -> p c t i", i=4, t=J), src[:].rearrange("p t (c i) -> p c t i", i=4))
+
+        def group_adj(engine, q, g):
+            src = adj_t[q, g]
+            copy_on(engine, new_group("a%d_%d" % (q, g))[:].rearrange("p (t m j) -> p m j t", t=J, j=J), src.rearrange("p j (m t) -> p m j t", t=J))
+
+        def quant(key, fmt, bufs=None, tag=None):
+            coded(key, bufs, tag)
+            c, s = codes[key]
+            nc.vector.quantize_mx(out=c[:].bitcast(fmt), scales=s[:], in_=grp[key][:])
+
+        def turn(key, k, i, words):
+            bk = new_bank(i)
+            bank[key, k] = bk
+            for s in range(2):
+                for u in range(2):
+                    nc.tensor.transpose(bk[:, (2 * s + u) * P : (2 * s + u + 1) * P], words(2 * k + s, u), ident[:])
+
+        def pair_words(src):
+            words = src[:].bitcast(F32)
+            return lambda t, u: words[:, t, u : 256 : 2]
+
+        def turned(engine, key, k):
+            if k == 0:
+                new_group(key)
+            dst = grp[key][:, k * 1024 : (k + 1) * 1024].bitcast(F32).rearrange("p (s r u) -> p s r u", s=2, u=2)
+            copy_on(engine, dst, bank[key, k][:].rearrange("p (s u r) -> p s r u", s=2, u=2))
+
+        def mm(out, lhs, lfmt, cols, rhs, rfmt, start, stop):
+            nc.tensor.matmul_mx(
+                out=out[:], lhsT=lhs[0][:, cols].bitcast(lfmt), lhsT_scale=lhs[1][:, cols], rhs=rhs[0][:].bitcast(rfmt), rhs_scale=rhs[1][:], start=start, stop=stop
+            )
+
+        def da(q, g, t, i):
+            if g == 0:
+                bank["da", q, t] = new_bank(i)
+            mm(bank["da", q, t], codes["a%d_%d" % (q, g)], E4M3, slice(t * P, (t + 1) * P), codes["dz%d" % g], E5M2, g == 0, g == G - 1)
+
+        def dp_exit(q, t):
+            if t == 0:
+                dp_t[q] = work.tile([P, J, F], BF16, name="dp_%d" % q, tag="dp", bufs=2, align_bytes=64)
+            nc.scalar.activation(out=dp_t[q][:, t, :], in_=bank["da", q, t][:], func=COPY, scale=dis_t[:, q, t : t + 1])
+
+        def dh(q, t, i):
+            bank["dh", q, t] = new_bank(i)
+            cols = slice(t * P, (t + 1) * P)
+            mm(bank["dh", q, t], codes["dyT%d" % q], E5M2, cols, codes["w1"], E4M3, True, False)
+            mm(bank["dh", q, t], codes["dpT%d" % q], E5M2, cols, codes["w0"], E4M3, False, True)
+
+        o0 = {}
+
+        def dh_exit(engine, q, t):
+            if t % 2 == 0:
+                o0[q] = work.tile([P, 2, F], F32, name="o0_%d_%d" % (q, t), tag="o0", bufs=4)
+            copy_on(engine, o0[q][:, t % 2, :], bank["dh", q, t][:])
+            if t % 2 == 1:
+                nc.sync.dma_start(out=out0_v[q][:, t - 1 : t + 1, :], in_=o0[q][:])
+
+        def dw(q, ft, i):
+            if q == 0:
+                bank["dw", ft] = new_bank(i)
+            mm(bank["dw", ft], codes["h%d" % q], E4M3, slice(ft * P, (ft + 1) * P), codes["dpJ%d" % q], E5M2, q == 0, q == G - 1)
+
+        def dw_exit(engine, ft):
+            if ft % 2 == 0:
+                o0["w"] = work.tile([P, 2, F], F32, name="o1_%d" % ft, tag="o0", bufs=4)
+            copy_on(engine, o0["w"][:, ft % 2, :], bank["dw", ft][:])
+            if ft % 2 == 1:
+                nc.sync.dma_start(out=out1_v[:, ft - 1 : ft + 1, :], in_=o0["w"][:])
+
+        nc.scalar.dma_start(out=nnz_t[:], in_=nnz.rearrange("(g p j) -> p g j", p=P, j=J))
+        nc.scalar.dma_start(out=dis_t[:], in_=dis.rearrange("(g p j) -> p g j", p=P, j=J))
+        for g in range(G):
+            for k in range(2):
+                load_y(g, k)
+                load_go(g, k)
+        for g in (0, 1, 2, 3):
+            load_adj_quarter(0, g)
+        for g in (1, 0):
+            load_adj_quarter(1, g)
+        for i in range(2):
+            load_w(i)
+        for g in (2, 3):
+            load_adj_quarter(1, g)
+        for g in range(G):
+            load_adj(1, g)
+        for g in range(G):
+            load_h(g)
+        nc.vector.reciprocal(out=rinv[:], in_=nnz_t[:])
+        nc.vector.tensor_tensor(out=ratio[:], in0=dis_t[:], in1=rinv[:], op=ALU.mult)
+
+        def adj_quant(q, g):
+            quant("a%d_%d" % (q, g), E4M3, 9, "ca")
+
+        def turn_pair(key, i0, src):
+            turn(key, 0, i0, pair_words(src))
+            turn(key, 1, i0 + 1, pair_words(src))
+
+        def turned_pair(engines, key):
+            turned(engines[0], key, 0)
+            turned(engines[1], key, 1)
+
+        for g in range(G + 1):
+            if g < G:
+                mask(g, 0)
+                mask(g, 1)
+                for t in range(J):
+                    scale(g, t)
+                turn_pair("dyT%d" % g, 6, dy[g])
+                group_rows("S", "dz%d" % g, dz[g])
+                turned_pair("SS", "dyT%d" % g)
+            if g > 0:
+                if g == G:
+                    group_adj("V", 0, 0)
+                quant("dz%d" % (g - 1), E5M2)
+                quant("dyT%d" % (g - 1), E5M2)
+        group_adj("S", 0, 1)
+        adj_quant(0, 0)
+        group_adj("V", 0, 2)
+        group_adj("S", 0, 3)
+        adj_quant(0, 1)
+        group_adj("V", 1, 0)
+        adj_quant(0, 2)
+        adj_quant(0, 3)
+        ORDER = (1, 0, 2, 3)
+
+        def da_pass(q, g, order):
+            for t in range(J):
+                if g == order[0]:
+                    bank["da", q, t] = new_bank((0, 1, 4, 5)[t])
+                mm(bank["da", q, t], codes["a%d_%d" % (q, g)], E4M3, slice(t * P, (t + 1) * P), codes["dz%d" % g], E5M2, g == order[0], g == order[-1])
+
+        for g in range(3):
+            da_pass(0, g, (0, 1, 2, 3))
+        da_pass(0, 3, (0, 1, 2, 3))
+        group_adj("S", 1, 1)
+        for q in range(G):
+            n = q + 1
+            if q > 0:
+                dh_exit("S", q - 1, 0)
+                dh_exit("S", q - 1, 1)
+            for t in range(J):
+                dp_exit(q, t)
+            if q > 0:
+                for t in (2, 3):
+                    dh(q - 1, t, t)
+                    dh_exit("S", q - 1, t)
+            turn_pair("dpT%d" % q, 6, dp_t[q])
+            turned_pair("SS", "dpT%d" % q)
+            if q == 0:
+                for i in range(2):
+                    turn_pair("w%d" % i, (2, 6)[i], w_t[i])
+                turned_pair("SS", "w1")
+            if n + 1 < G:
+                group_adj("S", n + 1, 1)
+            if q == 2:
+                group_rows("S", "h0", h_t[0])
+            if n < G:
+                adj_quant(n, 1)
+                da_pass(n, 1, ORDER)
+                if q > 0:
+                    group_adj("V", n, 0)
+                    group_rows("V", "dpJ%d" % (q - 1), dp_t[q - 1])
+                adj_quant(n, 0)
+                da_pass(n, 0, ORDER)
+                group_adj("V", n, 2)
+                if q > 0:
+                    quant("dpJ%d" % (q - 1), E5M2)
+                if q == 0:
+                    turned_pair("VV", "w0")
+                group_adj("V", n, 3)
+                if q == 0:
+                    quant("w0", E4M3)
+                    quant("w1", E4M3)
+                adj_quant(n, 2)
+                quant("dpT%d" % q, E5M2, 2, "cdpT")
+                adj_quant(n, 3)
+                for t in (0, 1):
+                    dh(q, t, 2 + t)
+                da_pass(n, 2, ORDER)
+                da_pass(n, 3, ORDER)
+            else:
+                group_rows("V", "h1", h_t[1])
+                group_rows("V", "dpJ2", dp_t[2])
+                quant("h1", E4M3)
+                quant("h0", E4M3)
+                quant("dpJ2", E5M2)
+                group_rows("V", "h2", h_t[2])
+                group_rows("V", "dpJ3", dp_t[3])
+                quant("h2", E4M3)
+                group_rows("S", "h3", h_t[3])
+        DW = (4, 5, 0, 1)
+        quant("dpT3", E5M2, 2, "cdpT")
+        quant("dpJ3", E5M2)
+        quant("h3", E4M3)
+        for q in range(3):
+            for ft in range(4):
+                dw(q, ft, DW[ft])
+        for t in range(J):
+            dh(3, t, (2, 3)[t % 2])
+            dh_exit("VS"[t % 2], 3, t)
+        for ft in range(4):
+            dw(3, ft, DW[ft])
+            dw_exit("VS"[ft % 2], ft)

@@ -16,7 +16,8 @@ N, F = 2048, 512
 P, J = 128, 4
 GROUP = P * J
 G = N // GROUP
-HALF = 1024
+
+Y_BUFS, GO_BUFS, ROW_BUFS, GRP_BUFS, ADJ_CODES, OUT_BUFS = 4, 3, 7, 8, 6, 3
 
 FLOPS = 2 * N * N * F + 2 * N * 2 * F * F + 2 * N * F * F
 BYTES = 2 * (N * F + N * N + 2 * F * F + N * F) + 4 * (N * F + 2 * N) + 4 * (N * F + F * F)
@@ -45,67 +46,57 @@ def tile_sage_re_pb_v_kernel(tc, h, adj, w, rw, b, y, dis, nnz, grad_out, out_0,
         rinv = keep.tile([P, G, J], F32, name="rinv")
         ratio = keep.tile([P, G, J], F32, name="ratio")
 
-        y_t, go_t, adj_t, h_t, w_t = {}, {}, {}, {}, {}
-        dy, dz = {}, {}
-        dp_t = {}
-        grp = {}
-        codes = {}
-        bank = {}
+        y_t, go_t, dy, rows = {}, {}, {}, {}
+        grp, codes, bank, stage = {}, {}, {}, {}
 
-        def coded(key, bufs=None, tag=None):
-            c = (keep if bufs is None else work).tile([P, GROUP], U32, name="c_%s" % key, tag=tag or "c_%s" % key, align_bytes=256, bufs=bufs or 1)
-            s = (keep if bufs is None else work).tile([P, GROUP], U8, name="s_%s" % key, tag="s_" + (tag or key), align_bytes=256, bufs=bufs or 1)
-            codes[key] = (c, s)
-
-        def new_group(key):
-            grp[key] = work.tile([P, J * GROUP], BF16, name="g_%s" % key, tag="grp", align_bytes=256, bufs=8)
-            return grp[key]
-
-        def new_bank(i):
-            return psum.tile([P, 512], F32, name="bank%d" % i, tag="bank%d" % i)
+        def new_bank(key, i):
+            bank[key] = psum.tile([P, 512], F32, name="bank%d" % i, tag="bank%d" % i)
+            return bank[key]
 
         def load_y(g, k):
-            t = work.tile([P, 2, F], F32, name="y_%d_%d" % (g, k), tag="y", bufs=4)
-            nc.sync.dma_start(out=t[:], in_=y_v[g][:, 2 * k : 2 * k + 2, :])
-            y_t[g, k] = t
+            y_t[g, k] = work.tile([P, 2, F], F32, name="y_%d_%d" % (g, k), tag="y", bufs=Y_BUFS)
+            nc.sync.dma_start(out=y_t[g, k][:], in_=y_v[g][:, 2 * k : 2 * k + 2, :])
 
-        def load_go(g, k):
-            t = work.tile([P, 2, F], BF16, name="go_%d_%d" % (g, k), tag="go", bufs=4)
-            nc.sync.dma_start(out=t[:], in_=go_v[g][:, 2 * k : 2 * k + 2, :])
-            go_t[g, k] = t
+        def load_go(g, k, n):
+            t = work.tile([P, 2 * n, F], BF16, name="go_%d_%d" % (g, k), tag="go", bufs=GO_BUFS)
+            nc.sync.dma_start(out=t[:], in_=go_v[g][:, 2 * k : 2 * (k + n), :])
+            for i in range(n):
+                go_t[g, k + i] = t[:, 2 * i : 2 * i + 2, :]
 
-        def load_h(g):
-            t = work.tile([P, J, F], BF16, name="h_%d" % g, tag="rows", bufs=7)
-            nc.sync.dma_start(out=t[:], in_=h_v[g])
-            h_t[g] = t
+        def load_rows(key, src):
+            t = work.tile([P, J, F], BF16, name="r_" + key, tag="rows", bufs=ROW_BUFS)
+            nc.sync.dma_start(out=t[:], in_=src)
+            rows[key] = t[:]
 
-        def load_w(i):
-            t = work.tile([P, J, F], BF16, name="w_%d" % i, tag="rows", bufs=7)
-            nc.sync.dma_start(out=t[:], in_=w_v[i])
-            w_t[i] = t
+        def load_adj(q, g):
+            load_rows("a%d_%d" % (q, g), adj_v[g][:, :, q * GROUP : (q + 1) * GROUP])
 
-        def load_adj(hf, g):
-            t = work.tile([P, J, HALF], BF16, name="adj_%d_%d" % (hf, g), tag="adj", bufs=4)
-            nc.sync.dma_start(out=t[:], in_=adj_v[g][:, :, hf * HALF : (hf + 1) * HALF])
+        def load_adj_pair(q, g):
+            t = work.tile([P, J, 2 * GROUP], BF16, name="r2_%d_%d" % (q, g), tag="adj2", bufs=G)
+            nc.sync.dma_start(out=t[:], in_=adj_v[g][:, :, q * GROUP : (q + 2) * GROUP])
             for k in range(2):
-                adj_t[2 * hf + k, g] = t[:, :, k * GROUP : (k + 1) * GROUP]
-
-        def load_adj_quarter(q, g):
-            t = work.tile([P, J, GROUP], BF16, name="adjq_%d_%d" % (q, g), tag="rows", bufs=7)
-            nc.sync.dma_start(out=t[:], in_=adj_v[g][:, :, q * GROUP : (q + 1) * GROUP])
-            adj_t[q, g] = t[:]
-
+                rows["a%d_%d" % (q + k, g)] = t[:, :, k * GROUP : (k + 1) * GROUP]
 
         def mask(g, k):
             if k == 0:
-                dy[g] = work.tile([P, J, F], BF16, name="dy_%d" % g, tag="dy", bufs=2, align_bytes=64)
-            pair = slice(2 * k, 2 * k + 2)
-            nc.vector.scalar_tensor_tensor(out=dy[g][:, pair, :], in0=y_t[g, k][:], scalar=0.0, in1=go_t[g, k][:], op0=ALU.is_gt, op1=ALU.mult)
+                dy[g] = work.tile([P, 2, J, F // 2], BF16, name="dy_%d" % g, tag="dy", bufs=2, align_bytes=64)
+            for u in range(2):
+                nc.vector.scalar_tensor_tensor(
+                    out=dy[g][:, u, 2 * k : 2 * k + 2, :].rearrange("p t (w e) -> p (t w) e", e=2),
+                    in0=y_t[g, k][:].rearrange("p t (w u e) -> p (t w) u e", u=2, e=2)[:, :, u, :],
+                    scalar=0.0,
+                    in1=go_t[g, k].rearrange("p t (w u e) -> p (t w) u e", u=2, e=2)[:, :, u, :],
+                    op0=ALU.is_gt,
+                    op1=ALU.mult,
+                )
 
-        def scale(g, t):
-            if t == 0:
-                dz[g] = work.tile([P, J, F], BF16, name="dz_%d" % g, tag="dz", bufs=2, align_bytes=64)
-            nc.vector.tensor_scalar(out=dz[g][:, t, :], in0=dy[g][:, t, :], scalar1=ratio[:, g, t : t + 1], scalar2=None, op0=ALU.mult)
+        def scale(g):
+            dz = work.tile([P, J, F], BF16, name="dz_%d" % g, tag="dz", bufs=2, align_bytes=64)
+            rows["dz%d" % g] = dz[:]
+            for t in range(J):
+                nc.vector.tensor_scalar(
+                    out=dz[:, t, :].rearrange("p (u c) -> p u c", u=2), in0=dy[g][:, :, t, :], scalar1=ratio[:, g, t : t + 1], scalar2=None, op0=ALU.mult
+                )
 
         def copy_on(engine, out, in_):
             if engine == "V":
@@ -113,28 +104,42 @@ def tile_sage_re_pb_v_kernel(tc, h, adj, w, rw, b, y, dis, nnz, grad_out, out_0,
             else:
                 nc.scalar.copy(out=out, in_=in_)
 
-        def group_rows(engine, key, src):
-            copy_on(engine, new_group(key)[:].rearrange("p (c i t) -> p c t i", i=4, t=J), src[:].rearrange("p t (c i) -> p c t i", i=4))
+        def new_group(key):
+            grp[key] = work.tile([P, J * GROUP], BF16, name="g_" + key, tag="grp", align_bytes=64, bufs=GRP_BUFS)
+            return grp[key]
 
-        def group_adj(engine, q, g):
-            src = adj_t[q, g]
-            copy_on(engine, new_group("a%d_%d" % (q, g))[:].rearrange("p (t m j) -> p m j t", t=J, j=J), src.rearrange("p j (m t) -> p m j t", t=J))
+        def weave(engine, key, half=None):
+            if half != 1:
+                new_group(key)
+            if key[0] == "a":
+                dst = grp[key][:].rearrange("p (t m j) -> p m j t", t=J, j=J)
+                src = rows[key].rearrange("p j (m t) -> p m j t", t=J)
+            else:
+                dst = grp[key][:].rearrange("p (c i t) -> p c t i", i=4, t=J)
+                src = rows[key].rearrange("p t (c i) -> p c t i", i=4)
+            part = slice(0, P) if half is None else slice(half * P // 2, (half + 1) * P // 2)
+            copy_on(engine, dst[:, part], src[:, part])
 
-        def quant(key, fmt, bufs=None, tag=None):
-            coded(key, bufs, tag)
-            c, s = codes[key]
+        def quant(key):
+            fmt = E4M3 if key[0] in "ahw" else E5M2
+            tag, bufs = ("ca", ADJ_CODES) if key[0] == "a" else ("cT", 2) if key[:3] == "dpT" else (key, 1)
+            c = work.tile([P, GROUP], U32, name="c_" + key, tag="c_" + tag, align_bytes=64, bufs=bufs)
+            s = work.tile([P, GROUP], U8, name="s_" + key, tag="s_" + tag, align_bytes=64, bufs=bufs)
+            codes[key] = (c, s, fmt)
             nc.vector.quantize_mx(out=c[:].bitcast(fmt), scales=s[:], in_=grp[key][:])
 
-        def turn(key, k, i, words):
-            bk = new_bank(i)
-            bank[key, k] = bk
+        def words(key, t, u):
+            if key[0] == "w":
+                return rows[key].bitcast(F32)[:, t, u : 2 * P : 2]
+            if key[:2] == "dy":
+                return dy[int(key[3])][:, u, t, :].bitcast(F32)
+            return rows["dp" + key[3]][:, t, u * 2 * P : (u + 1) * 2 * P].bitcast(F32)
+
+        def turn(key, k, i):
+            bk = new_bank((key, k), i)
             for s in range(2):
                 for u in range(2):
-                    nc.tensor.transpose(bk[:, (2 * s + u) * P : (2 * s + u + 1) * P], words(2 * k + s, u), ident[:])
-
-        def pair_words(src):
-            words = src[:].bitcast(F32)
-            return lambda t, u: words[:, t, u : 256 : 2]
+                    nc.tensor.transpose(bk[:, (2 * s + u) * P : (2 * s + u + 1) * P], words(key, 2 * k + s, u), ident[:])
 
         def turned(engine, key, k):
             if k == 0:
@@ -142,179 +147,190 @@ def tile_sage_re_pb_v_kernel(tc, h, adj, w, rw, b, y, dis, nnz, grad_out, out_0,
             dst = grp[key][:, k * 1024 : (k + 1) * 1024].bitcast(F32).rearrange("p (s r u) -> p s r u", s=2, u=2)
             copy_on(engine, dst, bank[key, k][:].rearrange("p (s u r) -> p s r u", s=2, u=2))
 
-        def mm(out, lhs, lfmt, cols, rhs, rfmt, start, stop):
-            nc.tensor.matmul_mx(
-                out=out[:], lhsT=lhs[0][:, cols].bitcast(lfmt), lhsT_scale=lhs[1][:, cols], rhs=rhs[0][:].bitcast(rfmt), rhs_scale=rhs[1][:], start=start, stop=stop
-            )
+        def mm(out, lhs, t, rhs, start, stop):
+            cols = slice(t * P, (t + 1) * P)
+            lc, ls, lf = codes[lhs]
+            rc, rs, rf = codes[rhs]
+            nc.tensor.matmul_mx(out=out[:], lhsT=lc[:, cols].bitcast(lf), lhsT_scale=ls[:, cols], rhs=rc[:].bitcast(rf), rhs_scale=rs[:], start=start, stop=stop)
 
-        def da(q, g, t, i):
-            if g == 0:
-                bank["da", q, t] = new_bank(i)
-            mm(bank["da", q, t], codes["a%d_%d" % (q, g)], E4M3, slice(t * P, (t + 1) * P), codes["dz%d" % g], E5M2, g == 0, g == G - 1)
+        def da(q, g, first, last):
+            for t in range(J):
+                if first:
+                    new_bank(("da", q, t), t)
+                mm(bank["da", q, t], "a%d_%d" % (q, g), t, "dz%d" % g, first, last)
 
-        def dp_exit(q, t):
+        def dp_exit(engine, q, t):
             if t == 0:
-                dp_t[q] = work.tile([P, J, F], BF16, name="dp_%d" % q, tag="dp", bufs=2, align_bytes=64)
-            nc.scalar.activation(out=dp_t[q][:, t, :], in_=bank["da", q, t][:], func=COPY, scale=dis_t[:, q, t : t + 1])
+                rows["dp%d" % q] = work.tile([P, J, F], BF16, name="dp_%d" % q, tag="dp", bufs=3, align_bytes=64)[:]
+            out = rows["dp%d" % q][:, t, :]
+            if engine == "V":
+                nc.vector.tensor_scalar(out=out, in0=bank["da", q, t][:], scalar1=dis_t[:, q, t : t + 1], scalar2=None, op0=ALU.mult)
+            else:
+                nc.scalar.activation(out=out, in_=bank["da", q, t][:], func=COPY, scale=dis_t[:, q, t : t + 1])
 
         def dh(q, t, i):
-            bank["dh", q, t] = new_bank(i)
-            cols = slice(t * P, (t + 1) * P)
-            mm(bank["dh", q, t], codes["dyT%d" % q], E5M2, cols, codes["w1"], E4M3, True, False)
-            mm(bank["dh", q, t], codes["dpT%d" % q], E5M2, cols, codes["w0"], E4M3, False, True)
-
-        o0 = {}
+            new_bank(("dh", q, t), i)
+            mm(bank["dh", q, t], "dyT%d" % q, t, "w1", True, False)
+            mm(bank["dh", q, t], "dpT%d" % q, t, "w0", False, True)
 
         def dh_exit(engine, q, t):
             if t % 2 == 0:
-                o0[q] = work.tile([P, 2, F], F32, name="o0_%d_%d" % (q, t), tag="o0", bufs=4)
-            copy_on(engine, o0[q][:, t % 2, :], bank["dh", q, t][:])
+                stage[q] = work.tile([P, 2, F], F32, name="o0_%d_%d" % (q, t), tag="out", bufs=OUT_BUFS)
+            copy_on(engine, stage[q][:, t % 2, :], bank["dh", q, t][:])
             if t % 2 == 1:
-                nc.sync.dma_start(out=out0_v[q][:, t - 1 : t + 1, :], in_=o0[q][:])
+                nc.sync.dma_start(out=out0_v[q][:, t - 1 : t + 1, :], in_=stage[q][:])
 
         def dw(q, ft, i):
             if q == 0:
-                bank["dw", ft] = new_bank(i)
-            mm(bank["dw", ft], codes["h%d" % q], E4M3, slice(ft * P, (ft + 1) * P), codes["dpJ%d" % q], E5M2, q == 0, q == G - 1)
+                new_bank(("dw", ft), i)
+            mm(bank["dw", ft], "h%d" % q, ft, "dp%d" % q, q == 0, q == G - 1)
 
         def dw_exit(engine, ft):
-            if ft % 2 == 0:
-                o0["w"] = work.tile([P, 2, F], F32, name="o1_%d" % ft, tag="o0", bufs=4)
-            copy_on(engine, o0["w"][:, ft % 2, :], bank["dw", ft][:])
-            if ft % 2 == 1:
-                nc.sync.dma_start(out=out1_v[:, ft - 1 : ft + 1, :], in_=o0["w"][:])
+            t = work.tile([P, F], F32, name="o1_%d" % ft, tag="out1", bufs=4)
+            copy_on(engine, t[:].rearrange("p (w u e) -> p w u e", u=2, e=2), bank["dw", ft][:].rearrange("p (u w e) -> p w u e", u=2, e=2))
+            nc.sync.dma_start(out=out1_v[:, ft, :], in_=t[:])
+
+        def turn2(key, i):
+            turn(key, 0, i)
+            turn(key, 1, i + 1)
+
+        def turned2(engine, key):
+            turned(engine, key, 0)
+            turned(engine, key, 1)
+
+        def adj_key(q, g):
+            return "a%d_%d" % (q, g)
 
         nc.scalar.dma_start(out=nnz_t[:], in_=nnz.rearrange("(g p j) -> p g j", p=P, j=J))
         nc.scalar.dma_start(out=dis_t[:], in_=dis.rearrange("(g p j) -> p g j", p=P, j=J))
+        load_y(0, 0)
+        load_go(0, 0, 1)
+        load_adj(0, 0)
+        load_y(0, 1)
+        load_go(0, 1, 1)
+        for g in range(1, G):
+            load_y(g, 0)
+            load_go(g, 0, 2)
+            load_y(g, 1)
+            load_adj(0, g)
+        load_adj(1, 0)
+        load_adj(1, 3)
+        load_rows("w1", w_v[1])
+        load_adj(1, 1)
+        load_rows("w0", w_v[0])
+        load_adj(1, 2)
+        for g in (3, 0, 1, 2):
+            load_adj_pair(2, g)
         for g in range(G):
-            for k in range(2):
-                load_y(g, k)
-                load_go(g, k)
-        for g in (0, 1, 2, 3):
-            load_adj_quarter(0, g)
-        for g in (1, 0):
-            load_adj_quarter(1, g)
-        for i in range(2):
-            load_w(i)
-        for g in (2, 3):
-            load_adj_quarter(1, g)
+            load_rows("h%d" % g, h_v[g])
+
+        weave("S", adj_key(0, 0))
         for g in range(G):
-            load_adj(1, g)
-        for g in range(G):
-            load_h(g)
-        nc.vector.reciprocal(out=rinv[:], in_=nnz_t[:])
-        nc.vector.tensor_tensor(out=ratio[:], in0=dis_t[:], in1=rinv[:], op=ALU.mult)
-
-        def adj_quant(q, g):
-            quant("a%d_%d" % (q, g), E4M3, 9, "ca")
-
-        def turn_pair(key, i0, src):
-            turn(key, 0, i0, pair_words(src))
-            turn(key, 1, i0 + 1, pair_words(src))
-
-        def turned_pair(engines, key):
-            turned(engines[0], key, 0)
-            turned(engines[1], key, 1)
-
-        for g in range(G + 1):
-            if g < G:
-                mask(g, 0)
-                mask(g, 1)
-                for t in range(J):
-                    scale(g, t)
-                turn_pair("dyT%d" % g, 6, dy[g])
-                group_rows("S", "dz%d" % g, dz[g])
-                turned_pair("SS", "dyT%d" % g)
+            mask(g, 0)
+            if g == 0:
+                nc.vector.reciprocal(out=rinv[:], in_=nnz_t[:])
+            mask(g, 1)
+            if g == 0:
+                nc.vector.tensor_tensor(out=ratio[:], in0=dis_t[:], in1=rinv[:], op=ALU.mult)
+            turn2("dyT%d" % g, 4)
             if g > 0:
-                if g == G:
-                    group_adj("V", 0, 0)
-                quant("dz%d" % (g - 1), E5M2)
-                quant("dyT%d" % (g - 1), E5M2)
-        group_adj("S", 0, 1)
-        adj_quant(0, 0)
-        group_adj("V", 0, 2)
-        group_adj("S", 0, 3)
-        adj_quant(0, 1)
-        group_adj("V", 1, 0)
-        adj_quant(0, 2)
-        adj_quant(0, 3)
-        ORDER = (1, 0, 2, 3)
+                quant("dyT%d" % (g - 1))
+            scale(g)
+            if g == G - 1:
+                weave("V", adj_key(0, g))
+            if g > 0:
+                quant(adj_key(0, g - 1))
+                quant("dz%d" % (g - 1))
+                da(0, g - 1, g == 1, False)
+            if g in (1, 2):
+                weave("S", adj_key(0, g))
+            turned2("S", "dyT%d" % g)
+            weave("S", "dz%d" % g)
+        quant(adj_key(0, 3))
+        weave("V", adj_key(1, 0))
+        quant("dz3")
+        turn2("w1", 6)
+        da(0, 3, False, True)
+        quant("dyT3")
+        weave("S", adj_key(1, 3))
 
-        def da_pass(q, g, order):
+        for q in range(1, G):
+            p = q - 1
             for t in range(J):
-                if g == order[0]:
-                    bank["da", q, t] = new_bank((0, 1, 4, 5)[t])
-                mm(bank["da", q, t], codes["a%d_%d" % (q, g)], E4M3, slice(t * P, (t + 1) * P), codes["dz%d" % g], E5M2, g == order[0], g == order[-1])
-
-        for g in range(3):
-            da_pass(0, g, (0, 1, 2, 3))
-        da_pass(0, 3, (0, 1, 2, 3))
-        group_adj("S", 1, 1)
-        for q in range(G):
-            n = q + 1
-            if q > 0:
-                dh_exit("S", q - 1, 0)
-                dh_exit("S", q - 1, 1)
-            for t in range(J):
-                dp_exit(q, t)
-            if q > 0:
-                for t in (2, 3):
-                    dh(q - 1, t, t)
-                    dh_exit("S", q - 1, t)
-            turn_pair("dpT%d" % q, 6, dp_t[q])
-            turned_pair("SS", "dpT%d" % q)
-            if q == 0:
-                for i in range(2):
-                    turn_pair("w%d" % i, (2, 6)[i], w_t[i])
-                turned_pair("SS", "w1")
-            if n + 1 < G:
-                group_adj("S", n + 1, 1)
-            if q == 2:
-                group_rows("S", "h0", h_t[0])
-            if n < G:
-                adj_quant(n, 1)
-                da_pass(n, 1, ORDER)
-                if q > 0:
-                    group_adj("V", n, 0)
-                    group_rows("V", "dpJ%d" % (q - 1), dp_t[q - 1])
-                adj_quant(n, 0)
-                da_pass(n, 0, ORDER)
-                group_adj("V", n, 2)
-                if q > 0:
-                    quant("dpJ%d" % (q - 1), E5M2)
-                if q == 0:
-                    turned_pair("VV", "w0")
-                group_adj("V", n, 3)
-                if q == 0:
-                    quant("w0", E4M3)
-                    quant("w1", E4M3)
-                adj_quant(n, 2)
-                quant("dpT%d" % q, E5M2, 2, "cdpT")
-                adj_quant(n, 3)
-                for t in (0, 1):
-                    dh(q, t, 2 + t)
-                da_pass(n, 2, ORDER)
-                da_pass(n, 3, ORDER)
+                dp_exit("S", p, t)
+            weave("V", adj_key(q, 1))
+            quant(adj_key(q, 0))
+            da(q, 0, True, False)
+            turn2("dpT%d" % p, 4)
+            if p > 0:
+                dh_exit("S", p - 1, 0)
+                dh_exit("S", p - 1, 1)
             else:
-                group_rows("V", "h1", h_t[1])
-                group_rows("V", "dpJ2", dp_t[2])
-                quant("h1", E4M3)
-                quant("h0", E4M3)
-                quant("dpJ2", E5M2)
-                group_rows("V", "h2", h_t[2])
-                group_rows("V", "dpJ3", dp_t[3])
-                quant("h2", E4M3)
-                group_rows("S", "h3", h_t[3])
-        DW = (4, 5, 0, 1)
-        quant("dpT3", E5M2, 2, "cdpT")
-        quant("dpJ3", E5M2)
-        quant("h3", E4M3)
-        for q in range(3):
-            for ft in range(4):
-                dw(q, ft, DW[ft])
+                turned2("S", "w1")
+                turn2("w0", 6)
+            turned2("S", "dpT%d" % p)
+            weave("V", adj_key(q, 2))
+            quant(adj_key(q, 1))
+            da(q, 1, False, False)
+            if p == 0:
+                turned2("S", "w0")
+            weave("S", adj_key(q + 1, 3) if q < G - 1 else "h1")
+            if p > 0:
+                dh(p - 1, 2, 6)
+                dh(p - 1, 3, 7)
+                dh_exit("S", p - 1, 2)
+                dh_exit("S", p - 1, 3)
+            quant(adj_key(q, 3))
+            da(q, 3, False, False)
+            quant(adj_key(q, 2))
+            da(q, 2, False, True)
+            if p > 0:
+                weave("V", "dp%d" % (p - 1))
+            else:
+                quant("w1")
+            quant("dpT%d" % p)
+            weave("V", adj_key(q + 1, 0) if q < G - 1 else "h0")
+            if p > 0:
+                quant("dp%d" % (p - 1))
+            else:
+                quant("w0")
+            dh(p, 0, 6)
+            dh(p, 1, 7)
+
         for t in range(J):
-            dh(3, t, (2, 3)[t % 2])
-            dh_exit("VS"[t % 2], 3, t)
+            dp_exit("S", 3, t)
+        quant("h1")
+        quant("h0")
+        weave("V", "dp2")
+        weave("V", "h2")
+        turn2("dpT3", 4)
+        dh_exit("S", 2, 0)
+        turned2("S", "dpT3")
+        dh_exit("S", 2, 1)
         for ft in range(4):
-            dw(3, ft, DW[ft])
-            dw_exit("VS"[ft % 2], ft)
+            dw(0, ft, ft)
+        dh(2, 2, 6)
+        for ft in range(4):
+            dw(1, ft, ft)
+        dh(2, 3, 7)
+        quant("dp2")
+        quant("dpT3")
+        weave("V", "h3", 0)
+        weave("S", "h3", 1)
+        weave("V", "dp3")
+        quant("h2")
+        dh_exit("S", 2, 2)
+        dh_exit("S", 2, 3)
+        dh(3, 0, 4)
+        dh(3, 1, 5)
+        dh(3, 2, 6)
+        dh(3, 3, 7)
+        quant("h3")
+        quant("dp3")
+        for k in (2, 3):
+            for ft in range(4):
+                dw(k, ft, ft)
+        for t in range(J):
+            dh_exit("S", 3, t)
+        for ft in range(4):
+            dw_exit("VVVS"[ft], ft)

@@ -46,7 +46,7 @@ def tile_sage_re_pb_v_kernel(tc, h, adj, w, rw, b, y, dis, nnz, grad_out, out_0,
         rinv = keep.tile([P, G, J], F32, name="rinv")
         ratio = keep.tile([P, G, J], F32, name="ratio")
 
-        y_t, go_t, dy, rows = {}, {}, {}, {}
+        y_t, go_t, rows = {}, {}, {}
         grp, codes, bank, stage = {}, {}, {}, {}
 
         def new_bank(key, i):
@@ -79,24 +79,16 @@ def tile_sage_re_pb_v_kernel(tc, h, adj, w, rw, b, y, dis, nnz, grad_out, out_0,
 
         def mask(g, k):
             if k == 0:
-                dy[g] = work.tile([P, 2, J, F // 2], BF16, name="dy_%d" % g, tag="dy", bufs=2, align_bytes=64)
-            for u in range(2):
-                nc.vector.scalar_tensor_tensor(
-                    out=dy[g][:, u, 2 * k : 2 * k + 2, :].rearrange("p t (w e) -> p (t w) e", e=2),
-                    in0=y_t[g, k][:].rearrange("p t (w u e) -> p (t w) u e", u=2, e=2)[:, :, u, :],
-                    scalar=0.0,
-                    in1=go_t[g, k].rearrange("p t (w u e) -> p (t w) u e", u=2, e=2)[:, :, u, :],
-                    op0=ALU.is_gt,
-                    op1=ALU.mult,
-                )
+                rows["dy%d" % g] = work.tile([P, J, F], BF16, name="dy_%d" % g, tag="dy", bufs=2, align_bytes=64)[:]
+            nc.vector.scalar_tensor_tensor(
+                out=rows["dy%d" % g][:, 2 * k : 2 * k + 2, :], in0=y_t[g, k][:], scalar=0.0, in1=go_t[g, k], op0=ALU.is_gt, op1=ALU.mult
+            )
 
         def scale(g):
             dz = work.tile([P, J, F], BF16, name="dz_%d" % g, tag="dz", bufs=2, align_bytes=64)
             rows["dz%d" % g] = dz[:]
             for t in range(J):
-                nc.vector.tensor_scalar(
-                    out=dz[:, t, :].rearrange("p (u c) -> p u c", u=2), in0=dy[g][:, :, t, :], scalar1=ratio[:, g, t : t + 1], scalar2=None, op0=ALU.mult
-                )
+                nc.vector.tensor_scalar(out=dz[:, t, :], in0=rows["dy%d" % g][:, t, :], scalar1=ratio[:, g, t : t + 1], scalar2=None, op0=ALU.mult)
 
         def copy_on(engine, out, in_):
             if engine == "V":
@@ -114,6 +106,9 @@ def tile_sage_re_pb_v_kernel(tc, h, adj, w, rw, b, y, dis, nnz, grad_out, out_0,
             if key[0] == "a":
                 dst = grp[key][:].rearrange("p (t m j) -> p m j t", t=J, j=J)
                 src = rows[key].rearrange("p j (m t) -> p m j t", t=J)
+            elif key[:2] == "dz":
+                dst = grp[key][:].rearrange("p (u w e t) -> p w t u e", u=2, e=2, t=J)
+                src = rows[key].rearrange("p t (w u e) -> p w t u e", u=2, e=2)
             else:
                 dst = grp[key][:].rearrange("p (c i t) -> p c t i", i=4, t=J)
                 src = rows[key].rearrange("p t (c i) -> p c t i", i=4)
@@ -129,11 +124,8 @@ def tile_sage_re_pb_v_kernel(tc, h, adj, w, rw, b, y, dis, nnz, grad_out, out_0,
             nc.vector.quantize_mx(out=c[:].bitcast(fmt), scales=s[:], in_=grp[key][:])
 
         def words(key, t, u):
-            if key[0] == "w":
-                return rows[key].bitcast(F32)[:, t, u : 2 * P : 2]
-            if key[:2] == "dy":
-                return dy[int(key[3])][:, u, t, :].bitcast(F32)
-            return rows["dp" + key[3]][:, t, u * 2 * P : (u + 1) * 2 * P].bitcast(F32)
+            row = rows[key.replace("T", "")].bitcast(F32)[:, t, :]
+            return row[:, u * P : (u + 1) * P] if key[:2] == "dp" else row[:, u : 2 * P : 2]
 
         def turn(key, k, i):
             bk = new_bank((key, k), i)
@@ -153,11 +145,12 @@ def tile_sage_re_pb_v_kernel(tc, h, adj, w, rw, b, y, dis, nnz, grad_out, out_0,
             rc, rs, rf = codes[rhs]
             nc.tensor.matmul_mx(out=out[:], lhsT=lc[:, cols].bitcast(lf), lhsT_scale=ls[:, cols], rhs=rc[:].bitcast(rf), rhs_scale=rs[:], start=start, stop=stop)
 
-        def da(q, g, first, last):
+        def da(q, gs, first, last):
             for t in range(J):
                 if first:
                     new_bank(("da", q, t), t)
-                mm(bank["da", q, t], "a%d_%d" % (q, g), t, "dz%d" % g, first, last)
+                for g in gs:
+                    mm(bank["da", q, t], "a%d_%d" % (q, g), t, "dz%d" % g, first and g == gs[0], last and g == gs[-1])
 
         def dp_exit(engine, q, t):
             if t == 0:
@@ -241,7 +234,7 @@ def tile_sage_re_pb_v_kernel(tc, h, adj, w, rw, b, y, dis, nnz, grad_out, out_0,
             if g > 0:
                 quant(adj_key(0, g - 1))
                 quant("dz%d" % (g - 1))
-                da(0, g - 1, g == 1, False)
+                da(0, [g - 1], g == 1, False)
             if g in (1, 2):
                 weave("S", adj_key(0, g))
             turned2("S", "dyT%d" % g)
@@ -250,7 +243,7 @@ def tile_sage_re_pb_v_kernel(tc, h, adj, w, rw, b, y, dis, nnz, grad_out, out_0,
         weave("V", adj_key(1, 0))
         quant("dz3")
         turn2("w1", 6)
-        da(0, 3, False, True)
+        da(0, [3], False, True)
         quant("dyT3")
         weave("S", adj_key(1, 3))
 
@@ -260,7 +253,7 @@ def tile_sage_re_pb_v_kernel(tc, h, adj, w, rw, b, y, dis, nnz, grad_out, out_0,
                 dp_exit("S", p, t)
             weave("V", adj_key(q, 1))
             quant(adj_key(q, 0))
-            da(q, 0, True, False)
+            da(q, [0], True, False)
             turn2("dpT%d" % p, 4)
             if p > 0:
                 dh_exit("S", p - 1, 0)
@@ -271,7 +264,7 @@ def tile_sage_re_pb_v_kernel(tc, h, adj, w, rw, b, y, dis, nnz, grad_out, out_0,
             turned2("S", "dpT%d" % p)
             weave("V", adj_key(q, 2))
             quant(adj_key(q, 1))
-            da(q, 1, False, False)
+            da(q, [1], False, False)
             if p == 0:
                 turned2("S", "w0")
             weave("S", adj_key(q + 1, 3) if q < G - 1 else "h1")
@@ -281,9 +274,9 @@ def tile_sage_re_pb_v_kernel(tc, h, adj, w, rw, b, y, dis, nnz, grad_out, out_0,
                 dh_exit("S", p - 1, 2)
                 dh_exit("S", p - 1, 3)
             quant(adj_key(q, 3))
-            da(q, 3, False, False)
+            da(q, [3], False, False)
             quant(adj_key(q, 2))
-            da(q, 2, False, True)
+            da(q, [2], False, True)
             if p > 0:
                 weave("V", "dp%d" % (p - 1))
             else:

@@ -17,7 +17,7 @@ P, J = 128, 4
 GROUP = P * J
 G = N // GROUP
 
-Y_BUFS, GO_BUFS, ROW_BUFS, GRP_BUFS, ADJ_CODES, OUT_BUFS = 4, 3, 7, 8, 6, 3
+Y_BUFS, GO_BUFS, ROW_BUFS, GRP_BUFS, ADJ_CODES, OUT_BUFS = 4, 3, 12, 8, 7, 4
 
 FLOPS = 2 * N * N * F + 2 * N * 2 * F * F + 2 * N * F * F
 BYTES = 2 * (N * F + N * N + 2 * F * F + N * F) + 4 * (N * F + 2 * N) + 4 * (N * F + F * F)
@@ -29,7 +29,7 @@ def tile_sage_re_pb_v_kernel(tc, h, adj, w, rw, b, y, dis, nnz, grad_out, out_0,
     y_v = y.rearrange("(g p j) o -> g p j o", p=P, j=J)
     go_v = grad_out.rearrange("(g p j) o -> g p j o", p=P, j=J)
     h_v = h.rearrange("(g p j) o -> g p j o", p=P, j=J)
-    w_v = [x.rearrange("(b p) o -> p b o", p=P) for x in (w, rw)]
+    w_v = [x.rearrange("(p b) o -> p b o", p=P) for x in (w, rw)]
     out0_v = out_0.rearrange("(g p j) f -> g p j f", p=P, j=J)
     out1_v = out_1.rearrange("(b p) f -> p b f", p=P)
 
@@ -70,12 +70,6 @@ def tile_sage_re_pb_v_kernel(tc, h, adj, w, rw, b, y, dis, nnz, grad_out, out_0,
 
         def load_adj(q, g):
             load_rows("a%d_%d" % (q, g), adj_v[g][:, :, q * GROUP : (q + 1) * GROUP])
-
-        def load_adj_pair(q, g):
-            t = work.tile([P, J, 2 * GROUP], BF16, name="r2_%d_%d" % (q, g), tag="adj2", bufs=G)
-            nc.sync.dma_start(out=t[:], in_=adj_v[g][:, :, q * GROUP : (q + 2) * GROUP])
-            for k in range(2):
-                rows["a%d_%d" % (q + k, g)] = t[:, :, k * GROUP : (k + 1) * GROUP]
 
         def mask(g, k):
             if k == 0:
@@ -145,8 +139,8 @@ def tile_sage_re_pb_v_kernel(tc, h, adj, w, rw, b, y, dis, nnz, grad_out, out_0,
             rc, rs, rf = codes[rhs]
             nc.tensor.matmul_mx(out=out[:], lhsT=lc[:, cols].bitcast(lf), lhsT_scale=ls[:, cols], rhs=rc[:].bitcast(rf), rhs_scale=rs[:], start=start, stop=stop)
 
-        def da(q, gs, first, last):
-            for t in range(J):
+        def da(q, gs, first, last, tiles=range(J)):
+            for t in tiles:
                 if first:
                     new_bank(("da", q, t), t)
                 for g in gs:
@@ -169,7 +163,7 @@ def tile_sage_re_pb_v_kernel(tc, h, adj, w, rw, b, y, dis, nnz, grad_out, out_0,
         def dh_exit(engine, q, t):
             if t % 2 == 0:
                 stage[q] = work.tile([P, 2, F], F32, name="o0_%d_%d" % (q, t), tag="out", bufs=OUT_BUFS)
-            copy_on(engine, stage[q][:, t % 2, :], bank["dh", q, t][:])
+            copy_on(engine, stage[q][:, t % 2, :].rearrange("p (r s) -> p r s", s=J), bank["dh", q, t][:].rearrange("p (s r) -> p r s", s=J))
             if t % 2 == 1:
                 nc.sync.dma_start(out=out0_v[q][:, t - 1 : t + 1, :], in_=stage[q][:])
 
@@ -206,14 +200,15 @@ def tile_sage_re_pb_v_kernel(tc, h, adj, w, rw, b, y, dis, nnz, grad_out, out_0,
             load_go(g, 0, 2)
             load_y(g, 1)
             load_adj(0, g)
+        load_rows("w1", w_v[1])
         load_adj(1, 0)
         load_adj(1, 3)
-        load_rows("w1", w_v[1])
-        load_adj(1, 1)
         load_rows("w0", w_v[0])
+        load_adj(1, 1)
         load_adj(1, 2)
-        for g in (3, 0, 1, 2):
-            load_adj_pair(2, g)
+        for q in (2, 3):
+            for g in (0, 3, 1, 2):
+                load_adj(q, g)
         for g in range(G):
             load_rows("h%d" % g, h_v[g])
 
@@ -226,104 +221,96 @@ def tile_sage_re_pb_v_kernel(tc, h, adj, w, rw, b, y, dis, nnz, grad_out, out_0,
             if g == 0:
                 nc.vector.tensor_tensor(out=ratio[:], in0=dis_t[:], in1=rinv[:], op=ALU.mult)
             turn2("dyT%d" % g, 4)
+            scale(g)
             if g > 0:
                 quant("dyT%d" % (g - 1))
-            scale(g)
             if g == G - 1:
                 weave("V", adj_key(0, g))
             if g > 0:
                 quant(adj_key(0, g - 1))
                 quant("dz%d" % (g - 1))
+                if g == G - 1:
+                    turn2("w1", 6)
                 da(0, [g - 1], g == 1, False)
             if g in (1, 2):
                 weave("S", adj_key(0, g))
-            turned2("S", "dyT%d" % g)
+            if g < G - 1:
+                turned2("S", "dyT%d" % g)
             weave("S", "dz%d" % g)
+        turned2("S", "dyT3")
+        turned2("S", "w1")
         quant(adj_key(0, 3))
         weave("V", adj_key(1, 0))
         quant("dz3")
-        turn2("w1", 6)
         da(0, [3], False, True)
+        turn2("w0", 6)
         quant("dyT3")
+        quant(adj_key(1, 0))
+        weave("V", adj_key(1, 1))
+        quant("w1")
         weave("S", adj_key(1, 3))
+        quant(adj_key(1, 1))
 
+        ring = [4, 5, 6, 7] * 8
         for q in range(1, G):
             p = q - 1
+            last = q == G - 1
             for t in range(J):
                 dp_exit("S", p, t)
-            weave("V", adj_key(q, 1))
-            quant(adj_key(q, 0))
-            da(q, [0], True, False)
-            turn2("dpT%d" % p, 4)
+                if t % 2 == 1:
+                    turn("dpT%d" % p, t // 2, ring[6 * p + t // 2])
+                da(q, [0, 1], True, False, [t])
             if p > 0:
-                dh_exit("S", p - 1, 0)
-                dh_exit("S", p - 1, 1)
-            else:
-                turned2("S", "w1")
-                turn2("w0", 6)
-            turned2("S", "dpT%d" % p)
-            weave("V", adj_key(q, 2))
-            quant(adj_key(q, 1))
-            da(q, [1], False, False)
-            if p == 0:
-                turned2("S", "w0")
-            weave("S", adj_key(q + 1, 3) if q < G - 1 else "h1")
-            if p > 0:
-                dh(p - 1, 2, 6)
-                dh(p - 1, 3, 7)
                 dh_exit("S", p - 1, 2)
                 dh_exit("S", p - 1, 3)
+            else:
+                turned2("S", "w0")
+            turned2("S", "dpT%d" % p)
+            weave("V", adj_key(q, 2))
             quant(adj_key(q, 3))
             da(q, [3], False, False)
-            quant(adj_key(q, 2))
-            da(q, [2], False, True)
             if p > 0:
                 weave("V", "dp%d" % (p - 1))
-            else:
-                quant("w1")
+            weave("S", adj_key(q + 1, 3) if not last else "h1")
+            quant(adj_key(q, 2))
+            da(q, [2], False, True)
+            weave("V", adj_key(q + 1, 0) if not last else "h0")
             quant("dpT%d" % p)
-            weave("V", adj_key(q + 1, 0) if q < G - 1 else "h0")
-            if p > 0:
-                quant("dp%d" % (p - 1))
-            else:
-                quant("w0")
-            dh(p, 0, 6)
-            dh(p, 1, 7)
+            quant("dp%d" % (p - 1) if p > 0 else "w0")
+            for t in range(J):
+                dh(p, t, ring[6 * p + 2 + t])
+            weave("V", adj_key(q + 1, 1) if not last else "dp2")
+            quant(adj_key(q + 1, 0) if not last else "h0")
+            quant(adj_key(q + 1, 1) if not last else "h1")
+            dh_exit("S", p, 0)
+            dh_exit("S", p, 1)
 
         for t in range(J):
-            dp_exit("S", 3, t)
-        quant("h1")
-        quant("h0")
-        weave("V", "dp2")
-        weave("V", "h2")
-        turn2("dpT3", 4)
-        dh_exit("S", 2, 0)
-        turned2("S", "dpT3")
-        dh_exit("S", 2, 1)
-        for ft in range(4):
+            dp_exit("SV"[t % 2], 3, t)
+        dw(0, 0, 0)
+        turn2("dpT3", ring[18])
+        for ft in range(1, 4):
             dw(0, ft, ft)
-        dh(2, 2, 6)
         for ft in range(4):
             dw(1, ft, ft)
-        dh(2, 3, 7)
-        quant("dp2")
+        dh_exit("S", 2, 2)
+        turned2("S", "dpT3")
+        dh_exit("S", 2, 3)
+        weave("V", "h2")
         quant("dpT3")
-        weave("V", "h3", 0)
-        weave("S", "h3", 1)
+        quant("dp2")
+        for t in range(J):
+            dh(3, t, ring[20 + t])
         weave("V", "dp3")
         quant("h2")
-        dh_exit("S", 2, 2)
-        dh_exit("S", 2, 3)
-        dh(3, 0, 4)
-        dh(3, 1, 5)
-        dh(3, 2, 6)
-        dh(3, 3, 7)
-        quant("h3")
+        weave("S", "h3", 0)
+        weave("V", "h3", 1)
         quant("dp3")
+        quant("h3")
         for k in (2, 3):
             for ft in range(4):
                 dw(k, ft, ft)
         for t in range(J):
             dh_exit("S", 3, t)
         for ft in range(4):
-            dw_exit("VVVS"[ft], ft)
+            dw_exit("VS"[ft % 2], ft)

@@ -17,7 +17,7 @@ P, J = 128, 4
 GROUP = P * J
 G = N // GROUP
 
-Y_BUFS, GO_BUFS, ROW_BUFS, GRP_BUFS, ADJ_CODES, OUT_BUFS = 4, 3, 12, 8, 7, 4
+Y_BUFS, GO_BUFS, ROW_BUFS, GRP_BUFS, ADJ_CODES, OUT_BUFS, ALIGN = 4, 3, 11, 8, 7, (8, 3), 64
 
 FLOPS = 2 * N * N * F + 2 * N * 2 * F * F + 2 * N * F * F
 BYTES = 2 * (N * F + N * N + 2 * F * F + N * F) + 4 * (N * F + 2 * N) + 4 * (N * F + F * F)
@@ -29,7 +29,7 @@ def tile_sage_re_pb_v_kernel(tc, h, adj, w, rw, b, y, dis, nnz, grad_out, out_0,
     y_v = y.rearrange("(g p j) o -> g p j o", p=P, j=J)
     go_v = grad_out.rearrange("(g p j) o -> g p j o", p=P, j=J)
     h_v = h.rearrange("(g p j) o -> g p j o", p=P, j=J)
-    w_v = [x.rearrange("(p b) o -> p b o", p=P) for x in (w, rw)]
+    w_v = [x.rearrange("(b p) o -> p b o", p=P) for x in (w, rw)]
     out0_v = out_0.rearrange("(g p j) f -> g p j f", p=P, j=J)
     out1_v = out_1.rearrange("(b p) f -> p b f", p=P)
 
@@ -42,7 +42,7 @@ def tile_sage_re_pb_v_kernel(tc, h, adj, w, rw, b, y, dis, nnz, grad_out, out_0,
         ident = keep.tile([P, P], F32, name="ident")
         make_identity(nc, ident[:])
         dis_t = keep.tile([P, G, J], F32, name="dis_t")
-        nnz_t = keep.tile([P, G, J], F32, name="nnz_t")
+        flat = keep.tile([P, GROUP], F32, name="flat")
         rinv = keep.tile([P, G, J], F32, name="rinv")
         ratio = keep.tile([P, G, J], F32, name="ratio")
 
@@ -52,6 +52,14 @@ def tile_sage_re_pb_v_kernel(tc, h, adj, w, rw, b, y, dis, nnz, grad_out, out_0,
         def new_bank(key, i):
             bank[key] = psum.tile([P, 512], F32, name="bank%d" % i, tag="bank%d" % i)
             return bank[key]
+
+        def node_factors():
+            bk = new_bank("nodes", 7)
+            for j in range(J):
+                nc.tensor.transpose(bk[:, j * P : (j + 1) * P], flat[:, j:GROUP:J], ident[:])
+            cols = bk[:].rearrange("p (j r) -> p r j", j=J)
+            nc.vector.reciprocal(out=rinv[:], in_=cols[:, G : 2 * G, :])
+            nc.vector.tensor_copy(out=dis_t[:], in_=cols[:, 0:G, :])
 
         def load_y(g, k):
             y_t[g, k] = work.tile([P, 2, F], F32, name="y_%d_%d" % (g, k), tag="y", bufs=Y_BUFS)
@@ -91,31 +99,45 @@ def tile_sage_re_pb_v_kernel(tc, h, adj, w, rw, b, y, dis, nnz, grad_out, out_0,
                 nc.scalar.copy(out=out, in_=in_)
 
         def new_group(key):
-            grp[key] = work.tile([P, J * GROUP], BF16, name="g_" + key, tag="grp", align_bytes=64, bufs=GRP_BUFS)
-            return grp[key]
+            grp[key] = work.tile([P, J * GROUP], BF16, name="g_" + key, tag="grp", align_bytes=64, bufs=GRP_BUFS)[:]
 
         def weave(engine, key, half=None):
             if half != 1:
                 new_group(key)
             if key[0] == "a":
-                dst = grp[key][:].rearrange("p (t m j) -> p m j t", t=J, j=J)
-                src = rows[key].rearrange("p j (m t) -> p m j t", t=J)
+                dst = grp[key].rearrange("p (t a b j) -> p a t j b", t=J, b=2, j=J)
+                src = rows[key].rearrange("p j (a b t) -> p a t j b", b=2, t=J)
             elif key[:2] == "dz":
-                dst = grp[key][:].rearrange("p (u w e t) -> p w t u e", u=2, e=2, t=J)
-                src = rows[key].rearrange("p t (w u e) -> p w t u e", u=2, e=2)
+                dst = grp[key].rearrange("p (u w e t) -> p w u t e", u=2, e=2, t=J)
+                src = rows[key].rearrange("p t (w u e) -> p w u t e", u=2, e=2)
             else:
-                dst = grp[key][:].rearrange("p (c i t) -> p c t i", i=4, t=J)
-                src = rows[key].rearrange("p t (c i) -> p c t i", i=4)
-            part = slice(0, P) if half is None else slice(half * P // 2, (half + 1) * P // 2)
+                dst = grp[key].rearrange("p (c i t) -> p c t i", i=2, t=J)
+                src = rows[key].rearrange("p t (c i) -> p c t i", i=2)
+            n = dst.shape[1]
+            part = slice(0, n) if half is None else slice(half * n // 2, (half + 1) * n // 2)
             copy_on(engine, dst[:, part], src[:, part])
 
-        def quant(key):
-            fmt = E4M3 if key[0] in "ahw" else E5M2
-            tag, bufs = ("ca", ADJ_CODES) if key[0] == "a" else ("cT", 2) if key[:3] == "dpT" else (key, 1)
-            c = work.tile([P, GROUP], U32, name="c_" + key, tag="c_" + tag, align_bytes=64, bufs=bufs)
-            s = work.tile([P, GROUP], U8, name="s_" + key, tag="s_" + tag, align_bytes=64, bufs=bufs)
-            codes[key] = (c, s, fmt)
-            nc.vector.quantize_mx(out=c[:].bitcast(fmt), scales=s[:], in_=grp[key][:])
+        def weave_both(key):
+            weave("V", key, 0)
+            weave("S", key, 1)
+
+        def quant(*keys):
+            for key in keys:
+                fmt = E4M3 if key[0] in "ahw" else E5M2
+                tag, bufs = ("a", ADJ_CODES) if key[0] == "a" else ("T", 2) if key[:3] == "dpT" else (key, 1)
+                c = work.tile([P, GROUP], U32, name="c_" + key, tag="c_" + tag, align_bytes=ALIGN, bufs=bufs)
+                s = work.tile([P, GROUP], U8, name="s_" + key, tag="s_" + tag, align_bytes=ALIGN, bufs=bufs)
+                codes[key] = (c[:], s[:], fmt)
+                nc.vector.quantize_mx(out=c[:].bitcast(fmt), scales=s[:], in_=grp[key])
+
+        def quant_half(key, half):
+            if half == 0:
+                c = work.tile([P, GROUP], U32, name="c_" + key, tag="c_" + key, align_bytes=ALIGN, bufs=1)
+                s = work.tile([P, GROUP], U8, name="s_" + key, tag="s_" + key, align_bytes=ALIGN, bufs=1)
+                codes[key] = (c[:], s[:], E4M3)
+            c, s, fmt = codes[key]
+            cols = slice(half * GROUP // 2, (half + 1) * GROUP // 2)
+            nc.vector.quantize_mx(out=c[:, cols].bitcast(fmt), scales=s[:, cols], in_=grp[key][:, half * 2 * GROUP : (half + 1) * 2 * GROUP])
 
         def words(key, t, u):
             row = rows[key.replace("T", "")].bitcast(F32)[:, t, :]
@@ -137,7 +159,7 @@ def tile_sage_re_pb_v_kernel(tc, h, adj, w, rw, b, y, dis, nnz, grad_out, out_0,
             cols = slice(t * P, (t + 1) * P)
             lc, ls, lf = codes[lhs]
             rc, rs, rf = codes[rhs]
-            nc.tensor.matmul_mx(out=out[:], lhsT=lc[:, cols].bitcast(lf), lhsT_scale=ls[:, cols], rhs=rc[:].bitcast(rf), rhs_scale=rs[:], start=start, stop=stop)
+            nc.tensor.matmul_mx(out=out[:], lhsT=lc[:, cols].bitcast(lf), lhsT_scale=ls[:, cols], rhs=rc.bitcast(rf), rhs_scale=rs, start=start, stop=stop)
 
         def da(q, gs, first, last, tiles=range(J)):
             for t in tiles:
@@ -161,11 +183,12 @@ def tile_sage_re_pb_v_kernel(tc, h, adj, w, rw, b, y, dis, nnz, grad_out, out_0,
             mm(bank["dh", q, t], "dpT%d" % q, t, "w0", False, True)
 
         def dh_exit(engine, q, t):
-            if t % 2 == 0:
-                stage[q] = work.tile([P, 2, F], F32, name="o0_%d_%d" % (q, t), tag="out", bufs=OUT_BUFS)
-            copy_on(engine, stage[q][:, t % 2, :].rearrange("p (r s) -> p r s", s=J), bank["dh", q, t][:].rearrange("p (s r) -> p r s", s=J))
-            if t % 2 == 1:
-                nc.sync.dma_start(out=out0_v[q][:, t - 1 : t + 1, :], in_=stage[q][:])
+            n = 2 if q < G - 1 else 1
+            if t % n == 0:
+                stage[q] = work.tile([P, n, F], F32, name="o0_%d_%d" % (q, t), tag="out%d" % n, bufs=OUT_BUFS[n - 1])
+            copy_on(engine, stage[q][:, t % n, :], bank["dh", q, t][:])
+            if t % n == n - 1:
+                nc.sync.dma_start(out=out0_v[q][:, t - n + 1 : t + 1, :], in_=stage[q][:])
 
         def dw(q, ft, i):
             if q == 0:
@@ -173,7 +196,7 @@ def tile_sage_re_pb_v_kernel(tc, h, adj, w, rw, b, y, dis, nnz, grad_out, out_0,
             mm(bank["dw", ft], "h%d" % q, ft, "dp%d" % q, q == 0, q == G - 1)
 
         def dw_exit(engine, ft):
-            t = work.tile([P, F], F32, name="o1_%d" % ft, tag="out1", bufs=4)
+            t = work.tile([P, F], F32, name="o1_%d" % ft, tag="out1", bufs=OUT_BUFS[0])
             copy_on(engine, t[:].rearrange("p (w u e) -> p w u e", u=2, e=2), bank["dw", ft][:].rearrange("p (u w e) -> p w u e", u=2, e=2))
             nc.sync.dma_start(out=out1_v[:, ft, :], in_=t[:])
 
@@ -188,23 +211,24 @@ def tile_sage_re_pb_v_kernel(tc, h, adj, w, rw, b, y, dis, nnz, grad_out, out_0,
         def adj_key(q, g):
             return "a%d_%d" % (q, g)
 
-        nc.scalar.dma_start(out=nnz_t[:], in_=nnz.rearrange("(g p j) -> p g j", p=P, j=J))
-        nc.scalar.dma_start(out=dis_t[:], in_=dis.rearrange("(g p j) -> p g j", p=P, j=J))
+        nc.vector.memset(flat[:], 0.0)
         load_y(0, 0)
         load_go(0, 0, 1)
-        load_adj(0, 0)
+        nc.sync.dma_start(out=flat[0:G, :], in_=dis.rearrange("(g c) -> g c", g=G))
+        nc.sync.dma_start(out=flat[G : 2 * G, :], in_=nnz.rearrange("(g c) -> g c", g=G))
         load_y(0, 1)
         load_go(0, 1, 1)
         for g in range(1, G):
             load_y(g, 0)
             load_go(g, 0, 2)
             load_y(g, 1)
+        for g in range(0, G):
             load_adj(0, g)
-        load_rows("w1", w_v[1])
         load_adj(1, 0)
-        load_adj(1, 3)
-        load_rows("w0", w_v[0])
         load_adj(1, 1)
+        load_adj(1, 3)
+        load_rows("w1", w_v[1])
+        load_rows("w0", w_v[0])
         load_adj(1, 2)
         for q in (2, 3):
             for g in (0, 3, 1, 2):
@@ -212,43 +236,37 @@ def tile_sage_re_pb_v_kernel(tc, h, adj, w, rw, b, y, dis, nnz, grad_out, out_0,
         for g in range(G):
             load_rows("h%d" % g, h_v[g])
 
-        weave("S", adj_key(0, 0))
         for g in range(G):
             mask(g, 0)
             if g == 0:
-                nc.vector.reciprocal(out=rinv[:], in_=nnz_t[:])
+                node_factors()
             mask(g, 1)
             if g == 0:
                 nc.vector.tensor_tensor(out=ratio[:], in0=dis_t[:], in1=rinv[:], op=ALU.mult)
-            turn2("dyT%d" % g, 4)
+            turn2("dyT%d" % g, 4 + 2 * (g % 2))
             scale(g)
-            if g > 0:
-                quant("dyT%d" % (g - 1))
-            if g == G - 1:
-                weave("V", adj_key(0, g))
-            if g > 0:
-                quant(adj_key(0, g - 1))
-                quant("dz%d" % (g - 1))
-                if g == G - 1:
-                    turn2("w1", 6)
-                da(0, [g - 1], g == 1, False)
             if g in (1, 2):
-                weave("S", adj_key(0, g))
-            if g < G - 1:
-                turned2("S", "dyT%d" % g)
+                quant("dz%d" % (g - 1), "dyT%d" % (g - 1))
+            turned("S", "dyT%d" % g, 0)
             weave("S", "dz%d" % g)
-        turned2("S", "dyT3")
-        turned2("S", "w1")
-        quant(adj_key(0, 3))
-        weave("V", adj_key(1, 0))
-        quant("dz3")
+            turned("S", "dyT%d" % g, 1)
+        weave("V", adj_key(0, 0))
+        quant("dz2", adj_key(0, 0))
+        da(0, [0], True, False)
+        weave("V", adj_key(0, 1))
+        weave("S", adj_key(0, 2))
+        quant("dyT2", adj_key(0, 1))
+        da(0, [1], False, False)
+        weave("V", adj_key(0, 3))
+        quant("dz3", adj_key(0, 2))
+        da(0, [2], False, False)
+        quant(adj_key(0, 3), "dyT3")
         da(0, [3], False, True)
-        turn2("w0", 6)
-        quant("dyT3")
+        weave("S", adj_key(1, 0))
+        weave("S", adj_key(1, 1))
+        turn2("w1", 6)
         quant(adj_key(1, 0))
-        weave("V", adj_key(1, 1))
-        quant("w1")
-        weave("S", adj_key(1, 3))
+        weave("V", adj_key(1, 3))
         quant(adj_key(1, 1))
 
         ring = [4, 5, 6, 7] * 8
@@ -264,13 +282,18 @@ def tile_sage_re_pb_v_kernel(tc, h, adj, w, rw, b, y, dis, nnz, grad_out, out_0,
                 dh_exit("S", p - 1, 2)
                 dh_exit("S", p - 1, 3)
             else:
-                turned2("S", "w0")
+                turned2("S", "w1")
+                turn2("w0", 6)
             turned2("S", "dpT%d" % p)
+            if p == 0:
+                turned2("S", "w0")
             weave("V", adj_key(q, 2))
             quant(adj_key(q, 3))
             da(q, [3], False, False)
             if p > 0:
                 weave("V", "dp%d" % (p - 1))
+            else:
+                quant("w1")
             weave("S", adj_key(q + 1, 3) if not last else "h1")
             quant(adj_key(q, 2))
             da(q, [2], False, True)
@@ -279,38 +302,44 @@ def tile_sage_re_pb_v_kernel(tc, h, adj, w, rw, b, y, dis, nnz, grad_out, out_0,
             quant("dp%d" % (p - 1) if p > 0 else "w0")
             for t in range(J):
                 dh(p, t, ring[6 * p + 2 + t])
-            weave("V", adj_key(q + 1, 1) if not last else "dp2")
-            quant(adj_key(q + 1, 0) if not last else "h0")
-            quant(adj_key(q + 1, 1) if not last else "h1")
-            dh_exit("S", p, 0)
-            dh_exit("S", p, 1)
+            if not last:
+                weave("V", adj_key(q + 1, 1))
+                quant(adj_key(q + 1, 0), adj_key(q + 1, 1))
+                dh_exit("S", p, 0)
+                dh_exit("S", p, 1)
 
         for t in range(J):
-            dp_exit("SV"[t % 2], 3, t)
-        dw(0, 0, 0)
-        turn2("dpT3", ring[18])
-        for ft in range(1, 4):
-            dw(0, ft, ft)
-        for ft in range(4):
-            dw(1, ft, ft)
-        dh_exit("S", 2, 2)
+            dp_exit("VSVS"[t], 3, t)
+        turn2("dpT3", 0)
+        weave("V", "dp2")
+        quant("h0", "h1")
+        dh_exit("S", 2, 0)
+        dh_exit("S", 2, 1)
         turned2("S", "dpT3")
+        dh_exit("S", 2, 2)
         dh_exit("S", 2, 3)
+        for k in range(2):
+            for ft in range(4):
+                dw(k, ft, (2, 3, 6, 7)[ft])
         weave("V", "h2")
         quant("dpT3")
-        quant("dp2")
         for t in range(J):
-            dh(3, t, ring[20 + t])
+            dh(3, t, (0, 1, 4, 5)[t])
+        quant("dp2")
         weave("V", "dp3")
         quant("h2")
         weave("S", "h3", 0)
+        dh_exit("S", 3, 0)
+        dh_exit("S", 3, 1)
+        dh_exit("S", 3, 2)
         weave("V", "h3", 1)
         quant("dp3")
-        quant("h3")
-        for k in (2, 3):
-            for ft in range(4):
-                dw(k, ft, ft)
-        for t in range(J):
-            dh_exit("S", 3, t)
+        for ft in range(4):
+            dw(2, ft, None)
+        for half in range(2):
+            quant_half("h3", half)
+            dw(3, 2 * half, None)
+            dw(3, 2 * half + 1, None)
+        dh_exit("S", 3, 3)
         for ft in range(4):
             dw_exit("VS"[ft % 2], ft)

@@ -17,7 +17,8 @@ P, J = 128, 4
 GROUP = P * J
 G = N // GROUP
 
-Y_BUFS, GO_BUFS, ROW_BUFS, GRP_BUFS, ADJ_CODES, OUT_BUFS, ALIGN = 4, 3, 11, 8, 7, (8, 3), 64
+Y_BUFS, GO_BUFS, ROW_BUFS, GRP_BUFS, ADJ_CODES, OUT_BUFS, ALIGN = 4, 3, 10, 7, 7, (8, 3), 64
+LATE = ("dyT2", "dyT3")
 
 FLOPS = 2 * N * N * F + 2 * N * 2 * F * F + 2 * N * F * F
 BYTES = 2 * (N * F + N * N + 2 * F * F + N * F) + 4 * (N * F + 2 * N) + 4 * (N * F + F * F)
@@ -99,7 +100,7 @@ def tile_sage_re_pb_v_kernel(tc, h, adj, w, rw, b, y, dis, nnz, grad_out, out_0,
                 nc.scalar.copy(out=out, in_=in_)
 
         def new_group(key):
-            grp[key] = work.tile([P, J * GROUP], BF16, name="g_" + key, tag="grp", align_bytes=64, bufs=GRP_BUFS)[:]
+            grp[key] = work.tile([P, J * GROUP], BF16, name="g_" + key, tag="late" if key in LATE else "grp", align_bytes=64, bufs=len(LATE) if key in LATE else GRP_BUFS)[:]
 
         def weave(engine, key, half=None):
             if half != 1:
@@ -224,11 +225,11 @@ def tile_sage_re_pb_v_kernel(tc, h, adj, w, rw, b, y, dis, nnz, grad_out, out_0,
             load_y(g, 1)
         for g in range(0, G):
             load_adj(0, g)
+        load_rows("w1", w_v[1])
         load_adj(1, 0)
         load_adj(1, 1)
-        load_adj(1, 3)
-        load_rows("w1", w_v[1])
         load_rows("w0", w_v[0])
+        load_adj(1, 3)
         load_adj(1, 2)
         for q in (2, 3):
             for g in (0, 3, 1, 2):
@@ -249,25 +250,31 @@ def tile_sage_re_pb_v_kernel(tc, h, adj, w, rw, b, y, dis, nnz, grad_out, out_0,
                 quant("dz%d" % (g - 1), "dyT%d" % (g - 1))
             turned("S", "dyT%d" % g, 0)
             weave("S", "dz%d" % g)
-            turned("S", "dyT%d" % g, 1)
+            if g < G - 1:
+                turned("S", "dyT%d" % g, 1)
         weave("V", adj_key(0, 0))
         quant("dz2", adj_key(0, 0))
         da(0, [0], True, False)
         weave("V", adj_key(0, 1))
         weave("S", adj_key(0, 2))
-        quant("dyT2", adj_key(0, 1))
+        turned("S", "dyT3", 1)
+        quant("dz3", adj_key(0, 1))
         da(0, [1], False, False)
+        turn2("w1", 4)
         weave("V", adj_key(0, 3))
-        quant("dz3", adj_key(0, 2))
+        quant(adj_key(0, 2))
         da(0, [2], False, False)
-        quant(adj_key(0, 3), "dyT3")
-        da(0, [3], False, True)
         weave("S", adj_key(1, 0))
-        weave("S", adj_key(1, 1))
-        turn2("w1", 6)
+        weave("V", adj_key(1, 1), 0)
+        quant(adj_key(0, 3))
+        da(0, [3], False, True)
+        turned2("S", "w1")
+        turn2("w0", 6)
+        weave("V", adj_key(1, 1), 1)
         quant(adj_key(1, 0))
-        weave("V", adj_key(1, 3))
+        weave("V", adj_key(1, 3), 0)
         quant(adj_key(1, 1))
+        weave("V", adj_key(1, 3), 1)
 
         ring = [4, 5, 6, 7] * 8
         for q in range(1, G):
@@ -275,31 +282,36 @@ def tile_sage_re_pb_v_kernel(tc, h, adj, w, rw, b, y, dis, nnz, grad_out, out_0,
             last = q == G - 1
             for t in range(J):
                 dp_exit("S", p, t)
-                if t % 2 == 1:
-                    turn("dpT%d" % p, t // 2, ring[6 * p + t // 2])
+                if t == J - 1:
+                    turn2("dpT%d" % p, ring[6 * p])
                 da(q, [0, 1], True, False, [t])
             if p > 0:
                 dh_exit("S", p - 1, 2)
                 dh_exit("S", p - 1, 3)
             else:
-                turned2("S", "w1")
-                turn2("w0", 6)
-            turned2("S", "dpT%d" % p)
-            if p == 0:
                 turned2("S", "w0")
-            weave("V", adj_key(q, 2))
+            weave("V", adj_key(q, 2), 0 if p == 0 else None)
+            if p == 0:
+                weave("S", adj_key(q, 2), 1)
+            turned2("S", "dpT%d" % p)
             quant(adj_key(q, 3))
             da(q, [3], False, False)
+            if p == 0:
+                weave("V", adj_key(2, 0))
             if p > 0:
                 weave("V", "dp%d" % (p - 1))
+                if last:
+                    quant("dyT2")
             else:
                 quant("w1")
             weave("S", adj_key(q + 1, 3) if not last else "h1")
             quant(adj_key(q, 2))
             da(q, [2], False, True)
-            weave("V", adj_key(q + 1, 0) if not last else "h0")
-            quant("dpT%d" % p)
-            quant("dp%d" % (p - 1) if p > 0 else "w0")
+            if p == 0:
+                quant("dpT0", "w0")
+            if p > 0:
+                weave("V", adj_key(q + 1, 0) if not last else "h0")
+                quant("dpT%d" % p, "dp%d" % (p - 1))
             for t in range(J):
                 dh(p, t, ring[6 * p + 2 + t])
             if not last:
@@ -309,10 +321,10 @@ def tile_sage_re_pb_v_kernel(tc, h, adj, w, rw, b, y, dis, nnz, grad_out, out_0,
                 dh_exit("S", p, 1)
 
         for t in range(J):
-            dp_exit("VSVS"[t], 3, t)
+            dp_exit("SSSS"[t], 3, t)
         turn2("dpT3", 0)
-        weave("V", "dp2")
         quant("h0", "h1")
+        weave("V", "dp2")
         dh_exit("S", 2, 0)
         dh_exit("S", 2, 1)
         turned2("S", "dpT3")
@@ -322,24 +334,26 @@ def tile_sage_re_pb_v_kernel(tc, h, adj, w, rw, b, y, dis, nnz, grad_out, out_0,
             for ft in range(4):
                 dw(k, ft, (2, 3, 6, 7)[ft])
         weave("V", "h2")
-        quant("dpT3")
+        quant("dyT3", "dpT3")
         for t in range(J):
             dh(3, t, (0, 1, 4, 5)[t])
         quant("dp2")
         weave("V", "dp3")
         quant("h2")
         weave("S", "h3", 0)
-        dh_exit("S", 3, 0)
-        dh_exit("S", 3, 1)
-        dh_exit("S", 3, 2)
-        weave("V", "h3", 1)
+        for t in range(4):
+            dh_exit("S", 3, t)
         quant("dp3")
-        for ft in range(4):
+        quant_half("h3", 0)
+        weave("V", "h3", 1)
+        for ft in range(2):
             dw(2, ft, None)
-        for half in range(2):
-            quant_half("h3", half)
-            dw(3, 2 * half, None)
-            dw(3, 2 * half + 1, None)
-        dh_exit("S", 3, 3)
-        for ft in range(4):
-            dw_exit("VS"[ft % 2], ft)
+            dw(3, ft, None)
+        for ft in (2, 3):
+            dw(2, ft, None)
+        dw_exit("S", 0)
+        quant_half("h3", 1)
+        for ft in (2, 3):
+            dw(3, ft, None)
+        for ft in (1, 2, 3):
+            dw_exit("SVS"[ft - 1], ft)

@@ -17,7 +17,7 @@ P, J = 128, 4
 GROUP = P * J
 G = N // GROUP
 
-Y_BUFS, GO_BUFS, ROW_BUFS, GRP_BUFS, ADJ_CODES, OUT_BUFS, ALIGN = 4, 3, 10, 7, 7, (8, 3), 64
+Y_BUFS, GO_BUFS, ROW_BUFS, GRP_BUFS, ADJ_CODES, OUT_BUFS, ALIGN = 4, 3, 10, 7, 7, (8, 3), 256
 LATE = ("dyT2", "dyT3")
 
 FLOPS = 2 * N * N * F + 2 * N * 2 * F * F + 2 * N * F * F

@@ -17,7 +17,7 @@ P, J = 128, 4
 GROUP = P * J
 G = N // GROUP
 
-Y_BUFS, GO_BUFS, ROW_BUFS, GRP_BUFS, ADJ_CODES, OUT_BUFS, ALIGN = 4, 3, 10, 7, 7, (8, 3), 256
+Y_BUFS, GO_BUFS, ROW_BUFS, GRP_BUFS, ADJ_CODES, OUT_BUFS, ALIGN = 4, 3, 10, 7, 7, (8, 3), 64
 LATE = ("dyT2", "dyT3")
 
 FLOPS = 2 * N * N * F + 2 * N * 2 * F * F + 2 * N * F * F
@@ -42,6 +42,8 @@ def tile_sage_re_pb_v_kernel(tc, h, adj, w, rw, b, y, dis, nnz, grad_out, out_0,
 
         ident = keep.tile([P, P], F32, name="ident")
         make_identity(nc, ident[:])
+        ident16 = keep.tile([P, P], BF16, name="ident16")
+        make_identity(nc, ident16[:])
         dis_t = keep.tile([P, G, J], F32, name="dis_t")
         flat = keep.tile([P, GROUP], F32, name="flat")
         rinv = keep.tile([P, G, J], F32, name="rinv")
@@ -87,11 +89,31 @@ def tile_sage_re_pb_v_kernel(tc, h, adj, w, rw, b, y, dis, nnz, grad_out, out_0,
                 out=rows["dy%d" % g][:, 2 * k : 2 * k + 2, :], in0=y_t[g, k][:], scalar=0.0, in1=go_t[g, k], op0=ALU.is_gt, op1=ALU.mult
             )
 
-        def scale(g):
-            dz = work.tile([P, J, F], BF16, name="dz_%d" % g, tag="dz", bufs=2, align_bytes=64)
-            rows["dz%d" % g] = dz[:]
-            for t in range(J):
-                nc.vector.tensor_scalar(out=dz[:, t, :], in0=rows["dy%d" % g][:, t, :], scalar1=ratio[:, g, t : t + 1], scalar2=None, op0=ALU.mult)
+        def scale(g, k):
+            if k == 0:
+                rows["dz%d" % g] = work.tile([P, J, F], BF16, name="dz_%d" % g, tag="dz", bufs=2, align_bytes=64)[:]
+            for t in (2 * k, 2 * k + 1):
+                nc.vector.tensor_scalar(out=rows["dz%d" % g][:, t, :], in0=rows["dy%d" % g][:, t, :], scalar1=ratio[:, g, t : t + 1], scalar2=None, op0=ALU.mult)
+
+        def spread(key, k, i):
+            for half in range(2):
+                if k == 0:
+                    bank[key, half] = psum.tile([P, 2 * GROUP], BF16, name="bank%d" % (i + half), tag="bank%d" % (i + half))
+                slots = bank[key, half][:].rearrange("p (c t) -> p t c", t=J)
+                cols = slice(half * GROUP // 2, (half + 1) * GROUP // 2)
+                nc.tensor.matmul(slots[:, 2 * k : 2 * k + 2, :], lhsT=ident16[:], rhs=rows[key][:, 2 * k : 2 * k + 2, cols], start=True, stop=True)
+
+        def spread_exit(key):
+            new_group(key)
+            for half in range(2):
+                part = slice(half * P // 2, (half + 1) * P // 2)
+                if key[0] == "a":
+                    dst = grp[key].rearrange("p (t m j) -> p t m j", t=J, j=J)[:, :, part, :]
+                    src = bank[key, half][:].rearrange("p (m t j) -> p t m j", t=J, j=J)
+                else:
+                    dst = grp[key].rearrange("p (u w x) -> p u w x", u=2, x=2 * J)[:, :, part, :]
+                    src = bank[key, half][:].rearrange("p (w u x) -> p u w x", u=2, x=2 * J)
+                nc.scalar.copy(out=dst, in_=src)
 
         def copy_on(engine, out, in_):
             if engine == "V":
@@ -219,17 +241,17 @@ def tile_sage_re_pb_v_kernel(tc, h, adj, w, rw, b, y, dis, nnz, grad_out, out_0,
         nc.sync.dma_start(out=flat[G : 2 * G, :], in_=nnz.rearrange("(g c) -> g c", g=G))
         load_y(0, 1)
         load_go(0, 1, 1)
+        load_adj(0, 0)
         for g in range(1, G):
             load_y(g, 0)
             load_go(g, 0, 2)
             load_y(g, 1)
-        for g in range(0, G):
             load_adj(0, g)
         load_rows("w1", w_v[1])
         load_adj(1, 0)
         load_adj(1, 1)
-        load_rows("w0", w_v[0])
         load_adj(1, 3)
+        load_rows("w0", w_v[0])
         load_adj(1, 2)
         for q in (2, 3):
             for g in (0, 3, 1, 2):
@@ -241,40 +263,38 @@ def tile_sage_re_pb_v_kernel(tc, h, adj, w, rw, b, y, dis, nnz, grad_out, out_0,
             mask(g, 0)
             if g == 0:
                 node_factors()
+            else:
+                quant(adj_key(0, g - 1))
+            turn("dyT%d" % g, 0, 4)
             mask(g, 1)
             if g == 0:
                 nc.vector.tensor_tensor(out=ratio[:], in0=dis_t[:], in1=rinv[:], op=ALU.mult)
-            turn2("dyT%d" % g, 4 + 2 * (g % 2))
-            scale(g)
-            if g in (1, 2):
-                quant("dz%d" % (g - 1), "dyT%d" % (g - 1))
+            turn("dyT%d" % g, 1, 5)
+            scale(g, 0)
+            scale(g, 1)
+            if g == G - 1:
+                break
+            spread("dz%d" % g, 0, 6)
+            spread("dz%d" % g, 1, 6)
             turned("S", "dyT%d" % g, 0)
-            weave("S", "dz%d" % g)
-            if g < G - 1:
-                turned("S", "dyT%d" % g, 1)
-        weave("V", adj_key(0, 0))
-        quant("dz2", adj_key(0, 0))
-        da(0, [0], True, False)
-        weave("V", adj_key(0, 1))
-        weave("S", adj_key(0, 2))
-        turned("S", "dyT3", 1)
-        quant("dz3", adj_key(0, 1))
-        da(0, [1], False, False)
-        turn2("w1", 4)
-        weave("V", adj_key(0, 3))
-        quant(adj_key(0, 2))
+            weave("V" if g == 0 else "S", adj_key(0, g))
+            turned("S", "dyT%d" % g, 1)
+            spread_exit("dz%d" % g)
+            if g > 0:
+                quant("dz%d" % (g - 1), "dyT%d" % (g - 1))
+                da(0, [g - 1], g == 1, False)
+        quant("dz2")
         da(0, [2], False, False)
-        weave("S", adj_key(1, 0))
-        weave("V", adj_key(1, 1), 0)
-        quant(adj_key(0, 3))
+        turned("S", "dyT3", 0)
+        weave("S", adj_key(0, 3))
+        weave("V", "dz3")
+        turn2("w1", 6)
+        quant(adj_key(0, 3), "dz3")
         da(0, [3], False, True)
-        turned2("S", "w1")
-        turn2("w0", 6)
-        weave("V", adj_key(1, 1), 1)
-        quant(adj_key(1, 0))
-        weave("V", adj_key(1, 3), 0)
-        quant(adj_key(1, 1))
-        weave("V", adj_key(1, 3), 1)
+        weave("S", adj_key(1, 0))
+        weave("V", adj_key(1, 1))
+        quant(adj_key(1, 0), adj_key(1, 1))
+        weave("V", adj_key(1, 3))
 
         ring = [4, 5, 6, 7] * 8
         for q in range(1, G):
@@ -283,21 +303,22 @@ def tile_sage_re_pb_v_kernel(tc, h, adj, w, rw, b, y, dis, nnz, grad_out, out_0,
             for t in range(J):
                 dp_exit("S", p, t)
                 if t == J - 1:
+                    if p == 0:
+                        turned("S", "dyT3", 1)
                     turn2("dpT%d" % p, ring[6 * p])
                 da(q, [0, 1], True, False, [t])
             if p > 0:
                 dh_exit("S", p - 1, 2)
                 dh_exit("S", p - 1, 3)
             else:
-                turned2("S", "w0")
-            weave("V", adj_key(q, 2), 0 if p == 0 else None)
-            if p == 0:
-                weave("S", adj_key(q, 2), 1)
+                turned2("S", "w1")
+                turn2("w0", 6)
+            weave("V", adj_key(q, 2))
             turned2("S", "dpT%d" % p)
+            if p == 0:
+                turned2("S", "w0")
             quant(adj_key(q, 3))
             da(q, [3], False, False)
-            if p == 0:
-                weave("V", adj_key(2, 0))
             if p > 0:
                 weave("V", "dp%d" % (p - 1))
                 if last:
@@ -309,8 +330,8 @@ def tile_sage_re_pb_v_kernel(tc, h, adj, w, rw, b, y, dis, nnz, grad_out, out_0,
             da(q, [2], False, True)
             if p == 0:
                 quant("dpT0", "w0")
+            weave("V", adj_key(q + 1, 0) if not last else "h0")
             if p > 0:
-                weave("V", adj_key(q + 1, 0) if not last else "h0")
                 quant("dpT%d" % p, "dp%d" % (p - 1))
             for t in range(J):
                 dh(p, t, ring[6 * p + 2 + t])

@@ -206,7 +206,7 @@ def tile_sage_re_pb_v_kernel(tc, h, adj, w, rw, b, y, dis, nnz, grad_out, out_0,
             mm(bank["dh", q, t], "dpT%d" % q, t, "w0", False, True)
 
         def dh_exit(engine, q, t):
-            n = 2 if q < G - 1 else 1
+            n = 2 if q < G - 2 else 1
             if t % n == 0:
                 stage[q] = work.tile([P, n, F], F32, name="o0_%d_%d" % (q, t), tag="out%d" % n, bufs=OUT_BUFS[n - 1])
             copy_on(engine, stage[q][:, t % n, :], bank["dh", q, t][:])
@@ -243,16 +243,16 @@ def tile_sage_re_pb_v_kernel(tc, h, adj, w, rw, b, y, dis, nnz, grad_out, out_0,
         load_go(0, 1, 1)
         load_adj(0, 0)
         for g in range(1, G):
+            load_adj(0, g)
             load_y(g, 0)
             load_go(g, 0, 2)
             load_y(g, 1)
-            load_adj(0, g)
-        load_rows("w1", w_v[1])
         load_adj(1, 0)
         load_adj(1, 1)
         load_adj(1, 3)
-        load_rows("w0", w_v[0])
+        load_rows("w1", w_v[1])
         load_adj(1, 2)
+        load_rows("w0", w_v[0])
         for q in (2, 3):
             for g in (0, 3, 1, 2):
                 load_adj(q, g)
@@ -263,8 +263,6 @@ def tile_sage_re_pb_v_kernel(tc, h, adj, w, rw, b, y, dis, nnz, grad_out, out_0,
             mask(g, 0)
             if g == 0:
                 node_factors()
-            else:
-                quant(adj_key(0, g - 1))
             turn("dyT%d" % g, 0, 4)
             mask(g, 1)
             if g == 0:
@@ -276,25 +274,32 @@ def tile_sage_re_pb_v_kernel(tc, h, adj, w, rw, b, y, dis, nnz, grad_out, out_0,
                 break
             spread("dz%d" % g, 0, 6)
             spread("dz%d" % g, 1, 6)
-            turned("S", "dyT%d" % g, 0)
-            weave("V" if g == 0 else "S", adj_key(0, g))
-            turned("S", "dyT%d" % g, 1)
-            spread_exit("dz%d" % g)
-            if g > 0:
-                quant("dz%d" % (g - 1), "dyT%d" % (g - 1))
+            if g == 0:
+                turned2("S", "dyT0")
+                weave("V", adj_key(0, 0))
+                weave("S", adj_key(0, 1))
+                quant("dyT0", adj_key(0, 0))
+            else:
+                weave("S", adj_key(0, g + 1))
+                turned2("S", "dyT%d" % g)
+                quant(adj_key(0, g), "dz%d" % (g - 1))
                 da(0, [g - 1], g == 1, False)
+            spread_exit("dz%d" % g)
+            if g == 2:
+                quant("dyT1", adj_key(0, 3))
         quant("dz2")
         da(0, [2], False, False)
         turned("S", "dyT3", 0)
-        weave("S", adj_key(0, 3))
-        weave("V", "dz3")
-        turn2("w1", 6)
-        quant(adj_key(0, 3), "dz3")
-        da(0, [3], False, True)
+        weave_both("dz3")
         weave("S", adj_key(1, 0))
-        weave("V", adj_key(1, 1))
+        weave("V", adj_key(1, 1), 0)
+        quant("dz3")
+        da(0, [3], False, True)
+        weave("V", adj_key(1, 1), 1)
+        turn2("w1", 6)
+        weave("V", adj_key(1, 3), 0)
         quant(adj_key(1, 0), adj_key(1, 1))
-        weave("V", adj_key(1, 3))
+        weave("V", adj_key(1, 3), 1)
 
         ring = [4, 5, 6, 7] * 8
         for q in range(1, G):
@@ -329,8 +334,10 @@ def tile_sage_re_pb_v_kernel(tc, h, adj, w, rw, b, y, dis, nnz, grad_out, out_0,
             quant(adj_key(q, 2))
             da(q, [2], False, True)
             if p == 0:
-                quant("dpT0", "w0")
+                quant("dpT0")
             weave("V", adj_key(q + 1, 0) if not last else "h0")
+            if p == 0:
+                quant("w0")
             if p > 0:
                 quant("dpT%d" % p, "dp%d" % (p - 1))
             for t in range(J):

@@ -17,7 +17,7 @@ P, J = 128, 4
 GROUP = P * J
 G = N // GROUP
 
-Y_BUFS, GO_BUFS, ROW_BUFS, GRP_BUFS, ADJ_CODES, OUT_BUFS, ALIGN = 4, 3, 10, 7, 7, (8, 3), 64
+Y_BUFS, GO_BUFS, ROW_BUFS, GRP_BUFS, ADJ_CODES, OUT_BUFS, ALIGN = 4, 3, 10, 7, 7, 14, 64
 LATE = ("dyT2", "dyT3")
 
 FLOPS = 2 * N * N * F + 2 * N * 2 * F * F + 2 * N * F * F
@@ -50,7 +50,7 @@ def tile_sage_re_pb_v_kernel(tc, h, adj, w, rw, b, y, dis, nnz, grad_out, out_0,
         ratio = keep.tile([P, G, J], F32, name="ratio")
 
         y_t, go_t, rows = {}, {}, {}
-        grp, codes, bank, stage = {}, {}, {}, {}
+        grp, codes, bank = {}, {}, {}
 
         def new_bank(key, i):
             bank[key] = psum.tile([P, 512], F32, name="bank%d" % i, tag="bank%d" % i)
@@ -206,12 +206,9 @@ def tile_sage_re_pb_v_kernel(tc, h, adj, w, rw, b, y, dis, nnz, grad_out, out_0,
             mm(bank["dh", q, t], "dpT%d" % q, t, "w0", False, True)
 
         def dh_exit(engine, q, t):
-            n = 2 if q < G - 2 else 1
-            if t % n == 0:
-                stage[q] = work.tile([P, n, F], F32, name="o0_%d_%d" % (q, t), tag="out%d" % n, bufs=OUT_BUFS[n - 1])
-            copy_on(engine, stage[q][:, t % n, :], bank["dh", q, t][:])
-            if t % n == n - 1:
-                nc.sync.dma_start(out=out0_v[q][:, t - n + 1 : t + 1, :], in_=stage[q][:])
+            tile = work.tile([P, F], F32, name="o0_%d_%d" % (q, t), tag="out", bufs=OUT_BUFS)
+            copy_on(engine, tile[:], bank["dh", q, t][:])
+            nc.sync.dma_start(out=out0_v[q][:, t, :], in_=tile[:])
 
         def dw(q, ft, i):
             if q == 0:
@@ -219,7 +216,7 @@ def tile_sage_re_pb_v_kernel(tc, h, adj, w, rw, b, y, dis, nnz, grad_out, out_0,
             mm(bank["dw", ft], "h%d" % q, ft, "dp%d" % q, q == 0, q == G - 1)
 
         def dw_exit(engine, ft):
-            t = work.tile([P, F], F32, name="o1_%d" % ft, tag="out1", bufs=OUT_BUFS[0])
+            t = work.tile([P, F], F32, name="o1_%d" % ft, tag="out", bufs=OUT_BUFS)
             copy_on(engine, t[:].rearrange("p (w u e) -> p w u e", u=2, e=2), bank["dw", ft][:].rearrange("p (u w e) -> p w u e", u=2, e=2))
             nc.sync.dma_start(out=out1_v[:, ft, :], in_=t[:])
 
@@ -264,6 +261,8 @@ def tile_sage_re_pb_v_kernel(tc, h, adj, w, rw, b, y, dis, nnz, grad_out, out_0,
             if g == 0:
                 node_factors()
             turn("dyT%d" % g, 0, 4)
+            if g > 1:
+                da(0, [g - 2], g == 2, False)
             mask(g, 1)
             if g == 0:
                 nc.vector.tensor_tensor(out=ratio[:], in0=dis_t[:], in1=rinv[:], op=ALU.mult)
@@ -280,26 +279,26 @@ def tile_sage_re_pb_v_kernel(tc, h, adj, w, rw, b, y, dis, nnz, grad_out, out_0,
                 weave("S", adj_key(0, 1))
                 quant("dyT0", adj_key(0, 0))
             else:
+                if g == 1:
+                    turned2("S", "dyT1")
                 weave("S", adj_key(0, g + 1))
-                turned2("S", "dyT%d" % g)
+                if g == 2:
+                    turned2("S", "dyT2")
                 quant(adj_key(0, g), "dz%d" % (g - 1))
-                da(0, [g - 1], g == 1, False)
+                if g == 1:
+                    quant("dyT1")
             spread_exit("dz%d" % g)
-            if g == 2:
-                quant("dyT1", adj_key(0, 3))
         quant("dz2")
         da(0, [2], False, False)
         turned("S", "dyT3", 0)
         weave_both("dz3")
         weave("S", adj_key(1, 0))
-        weave("V", adj_key(1, 1), 0)
-        quant("dz3")
+        quant(adj_key(0, 3), "dz3")
         da(0, [3], False, True)
-        weave("V", adj_key(1, 1), 1)
+        weave("V", adj_key(1, 1))
         turn2("w1", 6)
-        weave("V", adj_key(1, 3), 0)
         quant(adj_key(1, 0), adj_key(1, 1))
-        weave("V", adj_key(1, 3), 1)
+        weave("V", adj_key(1, 3))
 
         ring = [4, 5, 6, 7] * 8
         for q in range(1, G):

@@ -17,8 +17,7 @@ P, J = 128, 4
 GROUP = P * J
 G = N // GROUP
 
-Y_BUFS, GO_BUFS, ROW_BUFS, GRP_BUFS, ADJ_CODES, OUT_BUFS, ALIGN = 4, 3, 10, 7, 7, 14, 64
-LATE = ("dyT2", "dyT3")
+RAW_BUFS, MADE_BUFS, ADJ_CODES, OUT_BUFS, ALIGN = 18, 17, 7, 10, 64
 
 FLOPS = 2 * N * N * F + 2 * N * 2 * F * F + 2 * N * F * F
 BYTES = 2 * (N * F + N * N + 2 * F * F + N * F) + 4 * (N * F + 2 * N) + 4 * (N * F + F * F)
@@ -30,7 +29,7 @@ def tile_sage_re_pb_v_kernel(tc, h, adj, w, rw, b, y, dis, nnz, grad_out, out_0,
     y_v = y.rearrange("(g p j) o -> g p j o", p=P, j=J)
     go_v = grad_out.rearrange("(g p j) o -> g p j o", p=P, j=J)
     h_v = h.rearrange("(g p j) o -> g p j o", p=P, j=J)
-    w_v = [x.rearrange("(b p) o -> p b o", p=P) for x in (w, rw)]
+    w_v = [x.rearrange("(p b) o -> p b o", p=P) for x in (w, rw)]
     out0_v = out_0.rearrange("(g p j) f -> g p j f", p=P, j=J)
     out1_v = out_1.rearrange("(b p) f -> p b f", p=P)
 
@@ -40,17 +39,37 @@ def tile_sage_re_pb_v_kernel(tc, h, adj, w, rw, b, y, dis, nnz, grad_out, out_0,
         psum = ctx.enter_context(tc.psum_pool(name="psum", bufs=1))
         ctx.enter_context(tc.manual_schedule())
 
+        dis_t = keep.tile([P, G, J], F32, name="dis_t")
+        flat = keep.tile([P, GROUP], F32, name="flat")
+        rinv = keep.tile([P, G, J], F32, name="rinv")
+        nc.gpsimd.memset(flat[:], 0.0)
+        ratio = keep.tile([P, G, J], F32, name="ratio")
         ident = keep.tile([P, P], F32, name="ident")
         make_identity(nc, ident[:])
         ident16 = keep.tile([P, P], BF16, name="ident16")
         make_identity(nc, ident16[:])
-        dis_t = keep.tile([P, G, J], F32, name="dis_t")
-        flat = keep.tile([P, GROUP], F32, name="flat")
-        rinv = keep.tile([P, G, J], F32, name="rinv")
-        ratio = keep.tile([P, G, J], F32, name="ratio")
 
         y_t, go_t, rows = {}, {}, {}
         grp, codes, bank = {}, {}, {}
+        free = {"raw": list(range(RAW_BUFS)), "made": list(range(RAW_BUFS, RAW_BUFS + MADE_BUFS))}
+        held, users, waiting = {}, {}, []
+
+        def take(kind, name, shape, dtype, n_users):
+            i = free[kind].pop(0)
+            held[name] = (kind, i)
+            users[name] = n_users
+            return work.tile(shape, dtype, name=name, tag="buf%d" % i, bufs=1, align_bytes=ALIGN)
+
+        def used(name):
+            users[name] = users[name] - 1
+            if users[name] == 0:
+                kind, i = held[name]
+                free[kind].append(i)
+                issue_loads()
+
+        def issue_loads():
+            while waiting and free["raw"]:
+                waiting.pop(0)()
 
         def new_bank(key, i):
             bank[key] = psum.tile([P, 512], F32, name="bank%d" % i, tag="bank%d" % i)
@@ -62,50 +81,68 @@ def tile_sage_re_pb_v_kernel(tc, h, adj, w, rw, b, y, dis, nnz, grad_out, out_0,
                 nc.tensor.transpose(bk[:, j * P : (j + 1) * P], flat[:, j:GROUP:J], ident[:])
             cols = bk[:].rearrange("p (j r) -> p r j", j=J)
             nc.vector.reciprocal(out=rinv[:], in_=cols[:, G : 2 * G, :])
-            nc.vector.tensor_copy(out=dis_t[:], in_=cols[:, 0:G, :])
+            nc.vector.tensor_tensor(out=ratio[:], in0=cols[:, 0:G, :], in1=rinv[:], op=ALU.mult)
+            nc.scalar.copy(out=dis_t[:], in_=cols[:, 0:G, :])
 
-        def load_y(g, k):
-            y_t[g, k] = work.tile([P, 2, F], F32, name="y_%d_%d" % (g, k), tag="y", bufs=Y_BUFS)
-            nc.sync.dma_start(out=y_t[g, k][:], in_=y_v[g][:, 2 * k : 2 * k + 2, :])
+        def load_y(g, t0, n):
+            name = "y_%d_%d" % (g, t0)
+            t = take("raw", name, [P, n, F], F32, n)
+            nc.sync.dma_start(out=t[:], in_=y_v[g][:, t0 : t0 + n, :])
+            y_t[g, t0] = (t[:], name)
 
-        def load_go(g, k, n):
-            t = work.tile([P, 2 * n, F], BF16, name="go_%d_%d" % (g, k), tag="go", bufs=GO_BUFS)
-            nc.sync.dma_start(out=t[:], in_=go_v[g][:, 2 * k : 2 * (k + n), :])
+        def load_go(g, t0, n):
+            name = "go_%d_%d" % (g, t0)
+            t = take("raw", name, [P, n, F], BF16, n)
+            nc.sync.dma_start(out=t[:], in_=go_v[g][:, t0 : t0 + n, :])
             for i in range(n):
-                go_t[g, k + i] = t[:, 2 * i : 2 * i + 2, :]
+                go_t[g, t0 + i] = (t, i, name)
 
         def load_rows(key, src):
-            t = work.tile([P, J, F], BF16, name="r_" + key, tag="rows", bufs=ROW_BUFS)
+            t = take("raw", "r_" + key, [P, J, F], BF16, 2)
             nc.sync.dma_start(out=t[:], in_=src)
             rows[key] = t[:]
 
         def load_adj(q, g):
             load_rows("a%d_%d" % (q, g), adj_v[g][:, :, q * GROUP : (q + 1) * GROUP])
 
-        def mask(g, k):
-            if k == 0:
-                rows["dy%d" % g] = work.tile([P, J, F], BF16, name="dy_%d" % g, tag="dy", bufs=2, align_bytes=64)[:]
+        def mask(g, t0, n):
+            if t0 == 0:
+                rows["dy%d" % g] = take("made", "r_dy%d" % g, [P, J, F], BF16, 6)[:]
+            yt, yname = y_t[g, t0]
+            gt, i, gname = go_t[g, t0]
             nc.vector.scalar_tensor_tensor(
-                out=rows["dy%d" % g][:, 2 * k : 2 * k + 2, :], in0=y_t[g, k][:], scalar=0.0, in1=go_t[g, k], op0=ALU.is_gt, op1=ALU.mult
+                out=rows["dy%d" % g][:, t0 : t0 + n, :], in0=yt, scalar=0.0, in1=gt[:, i : i + n, :], op0=ALU.is_gt, op1=ALU.mult
             )
+            for t in range(n):
+                used(yname)
+                used(gname)
 
-        def scale(g, k):
-            if k == 0:
-                rows["dz%d" % g] = work.tile([P, J, F], BF16, name="dz_%d" % g, tag="dz", bufs=2, align_bytes=64)[:]
-            for t in (2 * k, 2 * k + 1):
+        def scale(g, *ts):
+            for t in ts:
+                if t == 0:
+                    rows["dz%d" % g] = take("made", "r_dz%d" % g, [P, J, F], BF16, 2)[:]
                 nc.vector.tensor_scalar(out=rows["dz%d" % g][:, t, :], in0=rows["dy%d" % g][:, t, :], scalar1=ratio[:, g, t : t + 1], scalar2=None, op0=ALU.mult)
+                used("r_dy%d" % g)
 
-        def spread(key, k, i):
-            for half in range(2):
+        def spread(key, k, i, halves=(0, 1)):
+            for half in halves:
                 if k == 0:
                     bank[key, half] = psum.tile([P, 2 * GROUP], BF16, name="bank%d" % (i + half), tag="bank%d" % (i + half))
                 slots = bank[key, half][:].rearrange("p (c t) -> p t c", t=J)
                 cols = slice(half * GROUP // 2, (half + 1) * GROUP // 2)
                 nc.tensor.matmul(slots[:, 2 * k : 2 * k + 2, :], lhsT=ident16[:], rhs=rows[key][:, 2 * k : 2 * k + 2, cols], start=True, stop=True)
+            if 1 in halves:
+                used("r_" + key)
 
-        def spread_exit(key):
-            new_group(key)
+        def spread4(key, i):
             for half in range(2):
+                spread(key, 0, i, [half])
+                spread(key, 1, i, [half])
+
+        def spread_exit(key, engines="SS", halves=(0, 1)):
+            if key not in grp:
+                new_group(key)
+            for half in halves:
                 part = slice(half * P // 2, (half + 1) * P // 2)
                 if key[0] == "a":
                     dst = grp[key].rearrange("p (t m j) -> p t m j", t=J, j=J)[:, :, part, :]
@@ -113,7 +150,7 @@ def tile_sage_re_pb_v_kernel(tc, h, adj, w, rw, b, y, dis, nnz, grad_out, out_0,
                 else:
                     dst = grp[key].rearrange("p (u w x) -> p u w x", u=2, x=2 * J)[:, :, part, :]
                     src = bank[key, half][:].rearrange("p (w u x) -> p u w x", u=2, x=2 * J)
-                nc.scalar.copy(out=dst, in_=src)
+                copy_on(engines[half], dst, src)
 
         def copy_on(engine, out, in_):
             if engine == "V":
@@ -122,10 +159,10 @@ def tile_sage_re_pb_v_kernel(tc, h, adj, w, rw, b, y, dis, nnz, grad_out, out_0,
                 nc.scalar.copy(out=out, in_=in_)
 
         def new_group(key):
-            grp[key] = work.tile([P, J * GROUP], BF16, name="g_" + key, tag="late" if key in LATE else "grp", align_bytes=64, bufs=len(LATE) if key in LATE else GRP_BUFS)[:]
+            grp[key] = take("made", "g_" + key, [P, J * GROUP], BF16, 2)[:]
 
-        def weave(engine, key, half=None):
-            if half != 1:
+        def weave(engine, key, lo=0, hi=8):
+            if key not in grp:
                 new_group(key)
             if key[0] == "a":
                 dst = grp[key].rearrange("p (t a b j) -> p a t j b", t=J, b=2, j=J)
@@ -137,12 +174,11 @@ def tile_sage_re_pb_v_kernel(tc, h, adj, w, rw, b, y, dis, nnz, grad_out, out_0,
                 dst = grp[key].rearrange("p (c i t) -> p c t i", i=2, t=J)
                 src = rows[key].rearrange("p t (c i) -> p c t i", i=2)
             n = dst.shape[1]
-            part = slice(0, n) if half is None else slice(half * n // 2, (half + 1) * n // 2)
-            copy_on(engine, dst[:, part], src[:, part])
-
-        def weave_both(key):
-            weave("V", key, 0)
-            weave("S", key, 1)
+            copy_on(engine, dst[:, lo * n // 8 : hi * n // 8], src[:, lo * n // 8 : hi * n // 8])
+            if lo == 0:
+                used("r_" + key)
+            if hi == 8:
+                used("r_" + key)
 
         def quant(*keys):
             for key in keys:
@@ -152,15 +188,21 @@ def tile_sage_re_pb_v_kernel(tc, h, adj, w, rw, b, y, dis, nnz, grad_out, out_0,
                 s = work.tile([P, GROUP], U8, name="s_" + key, tag="s_" + tag, align_bytes=ALIGN, bufs=bufs)
                 codes[key] = (c[:], s[:], fmt)
                 nc.vector.quantize_mx(out=c[:].bitcast(fmt), scales=s[:], in_=grp[key])
+                used("g_" + key)
+                used("g_" + key)
 
-        def quant_half(key, half):
-            if half == 0:
+        def quant_part(key, lo, hi):
+            if key not in codes:
                 c = work.tile([P, GROUP], U32, name="c_" + key, tag="c_" + key, align_bytes=ALIGN, bufs=1)
                 s = work.tile([P, GROUP], U8, name="s_" + key, tag="s_" + key, align_bytes=ALIGN, bufs=1)
-                codes[key] = (c[:], s[:], E4M3)
+                codes[key] = (c[:], s[:], E4M3 if key[0] in "ahw" else E5M2)
             c, s, fmt = codes[key]
-            cols = slice(half * GROUP // 2, (half + 1) * GROUP // 2)
-            nc.vector.quantize_mx(out=c[:, cols].bitcast(fmt), scales=s[:, cols], in_=grp[key][:, half * 2 * GROUP : (half + 1) * 2 * GROUP])
+            cols = slice(lo * P, hi * P)
+            nc.vector.quantize_mx(out=c[:, cols].bitcast(fmt), scales=s[:, cols], in_=grp[key][:, lo * GROUP : hi * GROUP])
+            if lo == 0:
+                used("g_" + key)
+            if hi == J:
+                used("g_" + key)
 
         def words(key, t, u):
             row = rows[key.replace("T", "")].bitcast(F32)[:, t, :]
@@ -171,12 +213,17 @@ def tile_sage_re_pb_v_kernel(tc, h, adj, w, rw, b, y, dis, nnz, grad_out, out_0,
             for s in range(2):
                 for u in range(2):
                     nc.tensor.transpose(bk[:, (2 * s + u) * P : (2 * s + u + 1) * P], words(key, 2 * k + s, u), ident[:])
+            used("r_" + key.replace("T", ""))
 
         def turned(engine, key, k):
             if k == 0:
                 new_group(key)
-            dst = grp[key][:, k * 1024 : (k + 1) * 1024].bitcast(F32).rearrange("p (s r u) -> p s r u", s=2, u=2)
-            copy_on(engine, dst, bank[key, k][:].rearrange("p (s u r) -> p s r u", s=2, u=2))
+            if key[0] == "w":
+                dst = grp[key].bitcast(F32).rearrange("p (r b u) -> p r b u", b=J, u=2)[:, :, 2 * k : 2 * k + 2, :]
+                copy_on(engine, dst, bank[key, k][:].rearrange("p (s u r) -> p r s u", s=2, u=2))
+            else:
+                dst = grp[key][:, k * 1024 : (k + 1) * 1024].bitcast(F32).rearrange("p (s r u) -> p s r u", s=2, u=2)
+                copy_on(engine, dst, bank[key, k][:].rearrange("p (s u r) -> p s r u", s=2, u=2))
 
         def mm(out, lhs, t, rhs, start, stop):
             cols = slice(t * P, (t + 1) * P)
@@ -193,7 +240,7 @@ def tile_sage_re_pb_v_kernel(tc, h, adj, w, rw, b, y, dis, nnz, grad_out, out_0,
 
         def dp_exit(engine, q, t):
             if t == 0:
-                rows["dp%d" % q] = work.tile([P, J, F], BF16, name="dp_%d" % q, tag="dp", bufs=3, align_bytes=64)[:]
+                rows["dp%d" % q] = take("made", "r_dp%d" % q, [P, J, F], BF16, 4)[:]
             out = rows["dp%d" % q][:, t, :]
             if engine == "V":
                 nc.vector.tensor_scalar(out=out, in0=bank["da", q, t][:], scalar1=dis_t[:, q, t : t + 1], scalar2=None, op0=ALU.mult)
@@ -205,15 +252,22 @@ def tile_sage_re_pb_v_kernel(tc, h, adj, w, rw, b, y, dis, nnz, grad_out, out_0,
             mm(bank["dh", q, t], "dyT%d" % q, t, "w1", True, False)
             mm(bank["dh", q, t], "dpT%d" % q, t, "w0", False, True)
 
+        def dh4(q, i):
+            for t in range(J):
+                new_bank(("dh", q, t), i + t)
+                mm(bank["dh", q, t], "dyT%d" % q, t, "w1", True, False)
+            for t in range(J):
+                mm(bank["dh", q, t], "dpT%d" % q, t, "w0", False, True)
+
         def dh_exit(engine, q, t):
             tile = work.tile([P, F], F32, name="o0_%d_%d" % (q, t), tag="out", bufs=OUT_BUFS)
             copy_on(engine, tile[:], bank["dh", q, t][:])
             nc.sync.dma_start(out=out0_v[q][:, t, :], in_=tile[:])
 
-        def dw(q, ft, i):
+        def dw(q, ft, i, last=False):
             if q == 0:
                 new_bank(("dw", ft), i)
-            mm(bank["dw", ft], "h%d" % q, ft, "dp%d" % q, q == 0, q == G - 1)
+            mm(bank["dw", ft], "h%d" % q, ft, "dp%d" % q, q == 0, last)
 
         def dw_exit(engine, ft):
             t = work.tile([P, F], F32, name="o1_%d" % ft, tag="out", bufs=OUT_BUFS)
@@ -231,156 +285,199 @@ def tile_sage_re_pb_v_kernel(tc, h, adj, w, rw, b, y, dis, nnz, grad_out, out_0,
         def adj_key(q, g):
             return "a%d_%d" % (q, g)
 
-        nc.vector.memset(flat[:], 0.0)
-        load_y(0, 0)
-        load_go(0, 0, 1)
-        nc.sync.dma_start(out=flat[0:G, :], in_=dis.rearrange("(g c) -> g c", g=G))
-        nc.sync.dma_start(out=flat[G : 2 * G, :], in_=nnz.rearrange("(g c) -> g c", g=G))
-        load_y(0, 1)
-        load_go(0, 1, 1)
-        load_adj(0, 0)
-        for g in range(1, G):
-            load_adj(0, g)
-            load_y(g, 0)
-            load_go(g, 0, 2)
-            load_y(g, 1)
-        load_adj(1, 0)
-        load_adj(1, 1)
-        load_adj(1, 3)
-        load_rows("w1", w_v[1])
-        load_adj(1, 2)
-        load_rows("w0", w_v[0])
+        def small_loads():
+            nc.sync.dma_start(out=flat[0:G, :], in_=dis.rearrange("(g c) -> g c", g=G))
+            nc.sync.dma_start(out=flat[G : 2 * G, :], in_=nnz.rearrange("(g c) -> g c", g=G))
+
+        def later(fn, *args):
+            waiting.append(lambda: fn(*args))
+
+        later(load_y, 0, 0, 1)
+        later(load_go, 0, 0, 2)
+        later(small_loads)
+        later(load_y, 0, 1, 1)
+        later(load_y, 0, 2, 2)
+        later(load_go, 0, 2, 2)
+        for g in (1, 2):
+            later(load_y, g, 0, 2)
+            later(load_go, g, 0, 4)
+            later(load_y, g, 2, 2)
+            later(load_adj, 0, g - 1)
+        later(load_y, 3, 0, 2)
+        later(load_go, 3, 0, 4)
+        later(load_adj, 0, 2)
+        later(load_y, 3, 2, 2)
+        later(load_adj, 0, 3)
+        later(load_adj, 1, 0)
+        later(load_rows, "w1", w_v[1])
+        later(load_rows, "w0", w_v[0])
+        later(load_adj, 1, 1)
+        later(load_adj, 1, 2)
+        later(load_adj, 1, 3)
         for q in (2, 3):
-            for g in (0, 3, 1, 2):
-                load_adj(q, g)
+            for g in range(G):
+                later(load_adj, q, g)
         for g in range(G):
-            load_rows("h%d" % g, h_v[g])
+            later(load_rows, "h%d" % g, h_v[g])
+        issue_loads()
 
-        for g in range(G):
-            mask(g, 0)
-            if g == 0:
-                node_factors()
+        mask(0, 0, 1)
+        mask(0, 1, 1)
+        node_factors()
+        turn("dyT0", 0, 4)
+        scale(0, 0, 1)
+        turned("S", "dyT0", 0)
+        mask(0, 2, 2)
+        turn("dyT0", 1, 5)
+        scale(0, 2, 3)
+        turned("S", "dyT0", 1)
+        weave("S", "dz0")
+        for g in (1, 2):
+            mask(g, 0, 2)
             turn("dyT%d" % g, 0, 4)
-            if g > 1:
-                da(0, [g - 2], g == 2, False)
-            mask(g, 1)
-            if g == 0:
-                nc.vector.tensor_tensor(out=ratio[:], in0=dis_t[:], in1=rinv[:], op=ALU.mult)
-            turn("dyT%d" % g, 1, 5)
-            scale(g, 0)
-            scale(g, 1)
-            if g == G - 1:
-                break
+            quant("dyT0" if g == 1 else "a0_0")
+            scale(g, 0, 1)
             spread("dz%d" % g, 0, 6)
+            turned("S", "dyT%d" % g, 0)
+            mask(g, 2, 2)
+            turn("dyT%d" % g, 1, 5)
+            quant("dz%d" % (g - 1))
+            scale(g, 2, 3)
             spread("dz%d" % g, 1, 6)
-            if g == 0:
-                turned2("S", "dyT0")
-                weave("V", adj_key(0, 0))
-                weave("S", adj_key(0, 1))
-                quant("dyT0", adj_key(0, 0))
-            else:
-                if g == 1:
-                    turned2("S", "dyT1")
-                weave("S", adj_key(0, g + 1))
-                if g == 2:
-                    turned2("S", "dyT2")
-                quant(adj_key(0, g), "dz%d" % (g - 1))
-                if g == 1:
-                    quant("dyT1")
+            weave("S", adj_key(0, g - 1))
+            if g == 2:
+                quant("dyT1")
+                da(0, [0], True, False)
+            turned("V", "dyT%d" % g, 1)
             spread_exit("dz%d" % g)
+        mask(3, 0, 2)
+        turn("dyT3", 0, 4)
+        quant("a0_1")
+        da(0, [1], False, False)
+        scale(3, 0, 1)
+        spread("dz3", 0, 6)
+        weave("S", "a0_2")
         quant("dz2")
-        da(0, [2], False, False)
+        mask(3, 2, 2)
+        scale(3, 2, 3)
+        spread("dz3", 1, 6)
+        turn("dyT3", 1, 5)
         turned("S", "dyT3", 0)
-        weave_both("dz3")
-        weave("S", adj_key(1, 0))
-        quant(adj_key(0, 3), "dz3")
+        weave("S", "a0_3", 0, 4)
+        quant("a0_2")
+        da(0, [2], False, False)
+        weave("V", "a0_3", 4, 8)
+        spread_exit("dz3")
+        weave("V", "a1_0", 0, 2)
+        quant("a0_3")
+        weave("V", "a1_0", 2, 4)
+        quant("dz3")
         da(0, [3], False, True)
-        weave("V", adj_key(1, 1))
-        turn2("w1", 6)
-        quant(adj_key(1, 0), adj_key(1, 1))
-        weave("V", adj_key(1, 3))
 
-        ring = [4, 5, 6, 7] * 8
+        weave("S", "a1_0", 4, 8)
+        turned("S", "dyT3", 1)
+        quant("dyT2", "a1_0", "dyT3")
+        weave("V", "a1_1")
+        turn2("w1", 6)
         for q in range(1, G):
             p = q - 1
             last = q == G - 1
+            if p > 0:
+                dh4(p - 1, 4)
             for t in range(J):
                 dp_exit("S", p, t)
-                if t == J - 1:
-                    if p == 0:
-                        turned("S", "dyT3", 1)
-                    turn2("dpT%d" % p, ring[6 * p])
-                da(q, [0, 1], True, False, [t])
-            if p > 0:
+                da(q, [0], True, False, [t])
+                if p == 0 and t == 1:
+                    turn2("w0", 4)
+            if p == 0:
+                weave("V", "a1_2", 0, 4)
+            quant(adj_key(q, 1))
+            weave("V", adj_key(q, 2), 4 if p == 0 else 0, 8)
+            if p == 0:
+                turned2("S", "w1")
+            else:
                 dh_exit("S", p - 1, 2)
                 dh_exit("S", p - 1, 3)
-            else:
-                turned2("S", "w1")
-                turn2("w0", 6)
-            weave("V", adj_key(q, 2))
-            turned2("S", "dpT%d" % p)
+            da(q, [1], False, False)
+            turn2("dpT%d" % p, 6)
             if p == 0:
                 turned2("S", "w0")
-            quant(adj_key(q, 3))
-            da(q, [3], False, False)
-            if p > 0:
-                weave("V", "dp%d" % (p - 1))
-                if last:
-                    quant("dyT2")
             else:
-                quant("w1")
-            weave("S", adj_key(q + 1, 3) if not last else "h1")
+                dh_exit("S", p - 1, 0)
+                dh_exit("S", p - 1, 1)
+            weave("V", adj_key(q, 3), 0, 4)
             quant(adj_key(q, 2))
-            da(q, [2], False, True)
             if p == 0:
-                quant("dpT0")
-            weave("V", adj_key(q + 1, 0) if not last else "h0")
-            if p == 0:
+                weave("S", "a1_3", 4, 8)
                 quant("w0")
+                turned2("S", "dpT0")
+                weave("S", "a2_1", 0, 4)
+            else:
+                weave("V", adj_key(q, 3), 4, 8)
+                weave("S", adj_key(q + 1, 1) if not last else "h0", 0, 4)
+                turned2("S", "dpT%d" % p)
+            da(q, [2], False, False)
+            if p == 0:
+                quant("w1")
+            else:
+                weave("V", adj_key(q + 1, 0) if not last else "h0", *((0, 4) if not last else (4, 8)))
+            quant(adj_key(q, 3))
+            da(q, [3], False, True)
             if p > 0:
-                quant("dpT%d" % p, "dp%d" % (p - 1))
-            for t in range(J):
-                dh(p, t, ring[6 * p + 2 + t])
+                weave("S", "dp0", 3 * p - 3, 3 * p)
             if not last:
-                weave("V", adj_key(q + 1, 1))
-                quant(adj_key(q + 1, 0), adj_key(q + 1, 1))
-                dh_exit("S", p, 0)
-                dh_exit("S", p, 1)
+                weave("V", adj_key(q + 1, 0), 0 if p == 0 else 4, 8)
+                quant("dpT%d" % p)
+                weave("V", adj_key(q + 1, 1), 4, 8)
+                quant(adj_key(q + 1, 0))
 
+        weave("V", "dp0", 6, 8)
+        quant("h0")
+        weave("V", "h1", 0, 4)
+        quant("dpT2")
+        dh4(2, 4)
         for t in range(J):
-            dp_exit("SSSS"[t], 3, t)
+            dp_exit("S", 3, t)
         turn2("dpT3", 0)
-        quant("h0", "h1")
-        weave("V", "dp2")
-        dh_exit("S", 2, 0)
-        dh_exit("S", 2, 1)
+        weave("V", "h1", 4, 8)
+        quant("dp0")
+        weave("V", "dp1")
+        for t in range(3):
+            dh_exit("S", 2, t)
+        for ft in range(J):
+            dw(0, ft, 2 + ft)
+        quant("h1")
+        weave("V", "dp2", 0, 4)
+        quant("dp1")
+        for ft in range(J):
+            dw(1, ft, None)
         turned2("S", "dpT3")
-        dh_exit("S", 2, 2)
         dh_exit("S", 2, 3)
-        for k in range(2):
-            for ft in range(4):
-                dw(k, ft, (2, 3, 6, 7)[ft])
-        weave("V", "h2")
-        quant("dyT3", "dpT3")
+        weave("V", "dp2", 4, 8)
+        quant("dpT3")
         for t in range(J):
-            dh(3, t, (0, 1, 4, 5)[t])
-        quant("dp2")
+            dh(3, t, (6, 0, 1, 7)[t])
+        weave("S", "h2", 0, 4)
         weave("V", "dp3")
-        quant("h2")
-        weave("S", "h3", 0)
-        for t in range(4):
+        quant("dp2")
+        for t in range(J):
             dh_exit("S", 3, t)
+        weave("V", "h3", 0, 4)
+        quant_part("h2", 0, 2)
+        dw(2, 0, None)
+        dw(2, 1, None)
         quant("dp3")
-        quant_half("h3", 0)
-        weave("V", "h3", 1)
-        for ft in range(2):
-            dw(2, ft, None)
-            dw(3, ft, None)
-        for ft in (2, 3):
-            dw(2, ft, None)
+        quant_part("h3", 0, 2)
+        dw(3, 0, None, True)
+        dw(3, 1, None, True)
+        weave("V", "h2", 4, 8)
+        weave("S", "h3", 4, 8)
         dw_exit("S", 0)
-        quant_half("h3", 1)
-        for ft in (2, 3):
-            dw(3, ft, None)
-        for ft in (1, 2, 3):
-            dw_exit("SVS"[ft - 1], ft)
+        quant_part("h2", 2, 4)
+        quant_part("h3", 2, 4)
+        for q in (2, 3):
+            for ft in (2, 3):
+                dw(q, ft, None, q == 3)
+        dw_exit("V", 1)
+        dw_exit("S", 2)
+        dw_exit("V", 3)

@@ -17,7 +17,17 @@ P, J = 128, 4
 GROUP = P * J
 G = N // GROUP
 
-RAW_BUFS, MADE_BUFS, ADJ_CODES, OUT_BUFS, ALIGN = 18, 17, 7, 10, 64
+RAW_BUFS, WIDE_BUFS, CODE_BUFS, OUT_BUFS, ALIGN = 14, 10, 10, 10, 64
+
+WIDTH = J * GROUP
+SHARED = [("r_dy%d" % g, "r_dz%d" % g) for g in range(G)] + [("g_dz%d" % g, "g_a0_%d" % g) for g in range(G)]
+SHARED = SHARED + [("r_dp0", "r_dp1"), ("r_dp2", "r_dp3")]
+CODED = [("dyT0", "dyT1"), ("dyT2", "dyT3"), ("w0", "w1"), ("dpT0", "dpT1"), ("dpT2", "dpT3"), ("dp0", "dp1"), ("dp2", "dp3"), ("h0", "h1"), ("h2", "h3")]
+CODED = CODED + [("a%d_%d" % (q, g), "a%d_%d" % (q, g + 1)) for q in range(1, G) for g in (0, 2)]
+SHARED = SHARED + [("g_" + x, "g_" + z) for x, z in CODED]
+CODED = CODED + [("dz0", "dz1"), ("dz2", "dz3"), ("a0_0", "a0_1"), ("a0_2", "a0_3")]
+PLACE = {key: ("_".join(pair), i) for pair in SHARED for i, key in enumerate(pair)}
+CODE_PLACE = {key: ("k_" + "_".join(pair), i) for pair in CODED for i, key in enumerate(pair)}
 
 FLOPS = 2 * N * N * F + 2 * N * 2 * F * F + 2 * N * F * F
 BYTES = 2 * (N * F + N * N + 2 * F * F + N * F) + 4 * (N * F + 2 * N) + 4 * (N * F + F * F)
@@ -49,23 +59,51 @@ def tile_sage_re_pb_v_kernel(tc, h, adj, w, rw, b, y, dis, nnz, grad_out, out_0,
         ident16 = keep.tile([P, P], BF16, name="ident16")
         make_identity(nc, ident16[:])
 
+        h_all = keep.tile([P, G, J, F], BF16, name="h_all")
         y_t, go_t, rows = {}, {}, {}
         grp, codes, bank = {}, {}, {}
-        free = {"raw": list(range(RAW_BUFS)), "made": list(range(RAW_BUFS, RAW_BUFS + MADE_BUFS))}
-        held, users, waiting = {}, {}, []
+        free = {"raw": list(range(RAW_BUFS)), "wide": list(range(WIDE_BUFS)), "code": list(range(CODE_BUFS))}
+        held, users, waiting, wide, pairs = {}, {}, [], {}, {}
 
-        def take(kind, name, shape, dtype, n_users):
+        def take(kind, name, n_users):
             i = free[kind].pop(0)
             held[name] = (kind, i)
             users[name] = n_users
-            return work.tile(shape, dtype, name=name, tag="buf%d" % i, bufs=1, align_bytes=ALIGN)
+            return "%s%d" % (kind, i)
+
+        def take_raw(name, shape, dtype, n_users):
+            return work.tile(shape, dtype, name=name, tag=take("raw", name, n_users), bufs=1, align_bytes=ALIGN)
+
+        def half_of(key, n_users):
+            name, i = PLACE[key]
+            if name not in wide:
+                wide[name] = work.tile([P, 2 * WIDTH], BF16, name=name, tag=take("wide", name, 2), bufs=1, align_bytes=ALIGN)
+            users[key] = n_users
+            return wide[name][:, i * WIDTH : (i + 1) * WIDTH]
+
+        def code_pair(key):
+            name, i = CODE_PLACE[key]
+            if name not in pairs:
+                tag = take("code", name, 2)
+                c = work.tile([P, 2 * GROUP], U32, name=name, tag=tag, bufs=1, align_bytes=ALIGN)
+                s = work.tile([P, 2 * GROUP], U8, name=name + "s", tag=tag + "s", bufs=1, align_bytes=ALIGN)
+                pairs[name] = (c, s)
+            if key not in codes:
+                cols = slice(i * GROUP, (i + 1) * GROUP)
+                codes[key] = (pairs[name][0][:, cols], pairs[name][1][:, cols], E4M3 if key[0] in "ahw" else E5M2)
+                users["c_" + key] = J * G if key[:2] == "dz" or key[0] == "w" else J
+            return pairs[name]
 
         def used(name):
             users[name] = users[name] - 1
-            if users[name] == 0:
+            if users[name] > 0:
+                return
+            if name in held:
                 kind, i = held[name]
                 free[kind].append(i)
                 issue_loads()
+            else:
+                used(CODE_PLACE[name[2:]][0] if name[:2] == "c_" else PLACE[name][0])
 
         def issue_loads():
             while waiting and free["raw"]:
@@ -86,28 +124,31 @@ def tile_sage_re_pb_v_kernel(tc, h, adj, w, rw, b, y, dis, nnz, grad_out, out_0,
 
         def load_y(g, t0, n):
             name = "y_%d_%d" % (g, t0)
-            t = take("raw", name, [P, n, F], F32, n)
+            t = take_raw(name, [P, n, F], F32, n)
             nc.sync.dma_start(out=t[:], in_=y_v[g][:, t0 : t0 + n, :])
             y_t[g, t0] = (t[:], name)
 
         def load_go(g, t0, n):
             name = "go_%d_%d" % (g, t0)
-            t = take("raw", name, [P, n, F], BF16, n)
+            t = take_raw(name, [P, n, F], BF16, n)
             nc.sync.dma_start(out=t[:], in_=go_v[g][:, t0 : t0 + n, :])
             for i in range(n):
                 go_t[g, t0 + i] = (t, i, name)
 
         def load_rows(key, src):
-            t = take("raw", "r_" + key, [P, J, F], BF16, 2)
+            t = take_raw("r_" + key, [P, J, F], BF16, 2 if key[0] == "w" else 8)
             nc.sync.dma_start(out=t[:], in_=src)
             rows[key] = t[:]
+
+        def load_h(g):
+            nc.sync.dma_start(out=h_all[:, g], in_=h_v[g])
 
         def load_adj(q, g):
             load_rows("a%d_%d" % (q, g), adj_v[g][:, :, q * GROUP : (q + 1) * GROUP])
 
         def mask(g, t0, n):
             if t0 == 0:
-                rows["dy%d" % g] = take("made", "r_dy%d" % g, [P, J, F], BF16, 6)[:]
+                rows["dy%d" % g] = half_of("r_dy%d" % g, 6).rearrange("p (j f) -> p j f", j=J)
             yt, yname = y_t[g, t0]
             gt, i, gname = go_t[g, t0]
             nc.vector.scalar_tensor_tensor(
@@ -120,7 +161,7 @@ def tile_sage_re_pb_v_kernel(tc, h, adj, w, rw, b, y, dis, nnz, grad_out, out_0,
         def scale(g, *ts):
             for t in ts:
                 if t == 0:
-                    rows["dz%d" % g] = take("made", "r_dz%d" % g, [P, J, F], BF16, 2)[:]
+                    rows["dz%d" % g] = half_of("r_dz%d" % g, 8).rearrange("p (j f) -> p j f", j=J)
                 nc.vector.tensor_scalar(out=rows["dz%d" % g][:, t, :], in0=rows["dy%d" % g][:, t, :], scalar1=ratio[:, g, t : t + 1], scalar2=None, op0=ALU.mult)
                 used("r_dy%d" % g)
 
@@ -131,7 +172,7 @@ def tile_sage_re_pb_v_kernel(tc, h, adj, w, rw, b, y, dis, nnz, grad_out, out_0,
                 slots = bank[key, half][:].rearrange("p (c t) -> p t c", t=J)
                 cols = slice(half * GROUP // 2, (half + 1) * GROUP // 2)
                 nc.tensor.matmul(slots[:, 2 * k : 2 * k + 2, :], lhsT=ident16[:], rhs=rows[key][:, 2 * k : 2 * k + 2, cols], start=True, stop=True)
-            if 1 in halves:
+            for i in range(2 * len(halves)):
                 used("r_" + key)
 
         def spread4(key, i):
@@ -159,7 +200,7 @@ def tile_sage_re_pb_v_kernel(tc, h, adj, w, rw, b, y, dis, nnz, grad_out, out_0,
                 nc.scalar.copy(out=out, in_=in_)
 
         def new_group(key):
-            grp[key] = take("made", "g_" + key, [P, J * GROUP], BF16, 2)[:]
+            grp[key] = half_of("g_" + key, 1)
 
         def weave(engine, key, lo=0, hi=8):
             if key not in grp:
@@ -175,34 +216,37 @@ def tile_sage_re_pb_v_kernel(tc, h, adj, w, rw, b, y, dis, nnz, grad_out, out_0,
                 src = rows[key].rearrange("p t (c i) -> p c t i", i=2)
             n = dst.shape[1]
             copy_on(engine, dst[:, lo * n // 8 : hi * n // 8], src[:, lo * n // 8 : hi * n // 8])
-            if lo == 0:
+            for i in range(lo, hi):
                 used("r_" + key)
-            if hi == 8:
-                used("r_" + key)
+
+        def weave_h(engine, ft, lo=0, hi=G):
+            key = "h%d" % ft
+            if key not in grp:
+                new_group(key)
+            dst = grp[key].rearrange("p (g c i t) -> p g c t i", g=G, i=2, t=J)
+            src = h_all[:, :, :, ft * P : (ft + 1) * P].rearrange("p g t (c i) -> p g c t i", i=2)
+            copy_on(engine, dst[:, lo:hi], src[:, lo:hi])
+
+        def quant_part(key, lo, hi):
+            code_pair(key)
+            c, s, fmt = codes[key]
+            nc.vector.quantize_mx(out=c[:, lo * P : hi * P].bitcast(fmt), scales=s[:, lo * P : hi * P], in_=grp[key][:, lo * GROUP : hi * GROUP])
+            if hi == J:
+                used("g_" + key)
 
         def quant(*keys):
             for key in keys:
-                fmt = E4M3 if key[0] in "ahw" else E5M2
-                tag, bufs = ("a", ADJ_CODES) if key[0] == "a" else ("T", 2) if key[:3] == "dpT" else (key, 1)
-                c = work.tile([P, GROUP], U32, name="c_" + key, tag="c_" + tag, align_bytes=ALIGN, bufs=bufs)
-                s = work.tile([P, GROUP], U8, name="s_" + key, tag="s_" + tag, align_bytes=ALIGN, bufs=bufs)
-                codes[key] = (c[:], s[:], fmt)
-                nc.vector.quantize_mx(out=c[:].bitcast(fmt), scales=s[:], in_=grp[key])
-                used("g_" + key)
+                code_pair(key)
+                c, s, fmt = codes[key]
+                nc.vector.quantize_mx(out=c.bitcast(fmt), scales=s, in_=grp[key])
                 used("g_" + key)
 
-        def quant_part(key, lo, hi):
-            if key not in codes:
-                c = work.tile([P, GROUP], U32, name="c_" + key, tag="c_" + key, align_bytes=ALIGN, bufs=1)
-                s = work.tile([P, GROUP], U8, name="s_" + key, tag="s_" + key, align_bytes=ALIGN, bufs=1)
-                codes[key] = (c[:], s[:], E4M3 if key[0] in "ahw" else E5M2)
-            c, s, fmt = codes[key]
-            cols = slice(lo * P, hi * P)
-            nc.vector.quantize_mx(out=c[:, cols].bitcast(fmt), scales=s[:, cols], in_=grp[key][:, lo * GROUP : hi * GROUP])
-            if lo == 0:
-                used("g_" + key)
-            if hi == J:
-                used("g_" + key)
+        def quant2(key0, key1):
+            code_pair(key0)
+            c, s = code_pair(key1)
+            nc.vector.quantize_mx(out=c[:].bitcast(codes[key0][2]), scales=s[:], in_=wide[PLACE["g_" + key0][0]][:])
+            used("g_" + key0)
+            used("g_" + key1)
 
         def words(key, t, u):
             row = rows[key.replace("T", "")].bitcast(F32)[:, t, :]
@@ -230,6 +274,8 @@ def tile_sage_re_pb_v_kernel(tc, h, adj, w, rw, b, y, dis, nnz, grad_out, out_0,
             lc, ls, lf = codes[lhs]
             rc, rs, rf = codes[rhs]
             nc.tensor.matmul_mx(out=out[:], lhsT=lc[:, cols].bitcast(lf), lhsT_scale=ls[:, cols], rhs=rc.bitcast(rf), rhs_scale=rs, start=start, stop=stop)
+            used("c_" + lhs)
+            used("c_" + rhs)
 
         def da(q, gs, first, last, tiles=range(J)):
             for t in tiles:
@@ -240,7 +286,7 @@ def tile_sage_re_pb_v_kernel(tc, h, adj, w, rw, b, y, dis, nnz, grad_out, out_0,
 
         def dp_exit(engine, q, t):
             if t == 0:
-                rows["dp%d" % q] = take("made", "r_dp%d" % q, [P, J, F], BF16, 4)[:]
+                rows["dp%d" % q] = half_of("r_dp%d" % q, 10).rearrange("p (j f) -> p j f", j=J)
             out = rows["dp%d" % q][:, t, :]
             if engine == "V":
                 nc.vector.tensor_scalar(out=out, in0=bank["da", q, t][:], scalar1=dis_t[:, q, t : t + 1], scalar2=None, op0=ALU.mult)
@@ -254,7 +300,7 @@ def tile_sage_re_pb_v_kernel(tc, h, adj, w, rw, b, y, dis, nnz, grad_out, out_0,
 
         def dh4(q, i):
             for t in range(J):
-                new_bank(("dh", q, t), i + t)
+                new_bank(("dh", q, t), i[t])
                 mm(bank["dh", q, t], "dyT%d" % q, t, "w1", True, False)
             for t in range(J):
                 mm(bank["dh", q, t], "dpT%d" % q, t, "w0", False, True)
@@ -264,10 +310,11 @@ def tile_sage_re_pb_v_kernel(tc, h, adj, w, rw, b, y, dis, nnz, grad_out, out_0,
             copy_on(engine, tile[:], bank["dh", q, t][:])
             nc.sync.dma_start(out=out0_v[q][:, t, :], in_=tile[:])
 
-        def dw(q, ft, i, last=False):
-            if q == 0:
-                new_bank(("dw", ft), i)
-            mm(bank["dw", ft], "h%d" % q, ft, "dp%d" % q, q == 0, last)
+        def dw(ft, qs, i):
+            for q in qs:
+                if q == 0:
+                    new_bank(("dw", ft), i)
+                mm(bank["dw", ft], "h%d" % ft, q, "dp%d" % q, q == 0, q == G - 1)
 
         def dw_exit(engine, ft):
             t = work.tile([P, F], F32, name="o1_%d" % ft, tag="out", bufs=OUT_BUFS)
@@ -315,10 +362,10 @@ def tile_sage_re_pb_v_kernel(tc, h, adj, w, rw, b, y, dis, nnz, grad_out, out_0,
         later(load_adj, 1, 2)
         later(load_adj, 1, 3)
         for q in (2, 3):
-            for g in range(G):
+            for g in (0, 3, 1, 2):
                 later(load_adj, q, g)
         for g in range(G):
-            later(load_rows, "h%d" % g, h_v[g])
+            later(load_h, g)
         issue_loads()
 
         mask(0, 0, 1)
@@ -357,8 +404,8 @@ def tile_sage_re_pb_v_kernel(tc, h, adj, w, rw, b, y, dis, nnz, grad_out, out_0,
         scale(3, 0, 1)
         spread("dz3", 0, 6)
         weave("S", "a0_2")
-        quant("dz2")
         mask(3, 2, 2)
+        quant("dz2")
         scale(3, 2, 3)
         spread("dz3", 1, 6)
         turn("dyT3", 1, 5)
@@ -374,26 +421,28 @@ def tile_sage_re_pb_v_kernel(tc, h, adj, w, rw, b, y, dis, nnz, grad_out, out_0,
         quant("dz3")
         da(0, [3], False, True)
 
-        weave("S", "a1_0", 4, 8)
         turned("S", "dyT3", 1)
-        quant("dyT2", "a1_0", "dyT3")
+        weave("S", "a1_0", 4, 8)
+        quant2("dyT2", "dyT3")
+        quant("a1_0")
         weave("V", "a1_1")
         turn2("w1", 6)
         for q in range(1, G):
             p = q - 1
             last = q == G - 1
+            nxt = (adj_key(q + 1, 0), adj_key(q + 1, 1), adj_key(q + 1, 3)) if not last else ("dp0", "dp1", "dp2")
             if p > 0:
-                dh4(p - 1, 4)
+                dh4(p - 1, (4, 5, 6, 7))
             for t in range(J):
                 dp_exit("S", p, t)
                 da(q, [0], True, False, [t])
                 if p == 0 and t == 1:
                     turn2("w0", 4)
+            if p > 0:
+                weave("V", adj_key(q, 3), 7, 8)
+            weave("V", adj_key(q, 2))
             if p == 0:
-                weave("V", "a1_2", 0, 4)
-            quant(adj_key(q, 1))
-            weave("V", adj_key(q, 2), 4 if p == 0 else 0, 8)
-            if p == 0:
+                quant("a1_1")
                 turned2("S", "w1")
             else:
                 dh_exit("S", p - 1, 2)
@@ -402,82 +451,71 @@ def tile_sage_re_pb_v_kernel(tc, h, adj, w, rw, b, y, dis, nnz, grad_out, out_0,
             turn2("dpT%d" % p, 6)
             if p == 0:
                 turned2("S", "w0")
+                weave("V", "a1_3", 0, 4)
+                quant("a1_2")
+                weave("S", "a1_3", 4, 8)
+                weave("V", nxt[0])
+                quant("a1_3")
+                quant2("w0", "w1")
             else:
                 dh_exit("S", p - 1, 0)
                 dh_exit("S", p - 1, 1)
-            weave("V", adj_key(q, 3), 0, 4)
-            quant(adj_key(q, 2))
-            if p == 0:
-                weave("S", "a1_3", 4, 8)
-                quant("w0")
-                turned2("S", "dpT0")
-                weave("S", "a2_1", 0, 4)
-            else:
-                weave("V", adj_key(q, 3), 4, 8)
-                weave("S", adj_key(q + 1, 1) if not last else "h0", 0, 4)
-                turned2("S", "dpT%d" % p)
-            da(q, [2], False, False)
-            if p == 0:
-                quant("w1")
-            else:
-                weave("V", adj_key(q + 1, 0) if not last else "h0", *((0, 4) if not last else (4, 8)))
-            quant(adj_key(q, 3))
-            da(q, [3], False, True)
+                quant(adj_key(q, 3), adj_key(q, 2))
+                weave("V", nxt[0], 0 if last else 0, 8)
+                weave("V", nxt[1])
+            weave("S", nxt[2], 0, 4 if p > 0 else 2)
+            turned2("S", "dpT%d" % p)
+            weave("S", nxt[2], 4 if p > 0 else 2, 7)
+            da(q, [2 if p == 0 else 3], False, False)
+            da(q, [3 if p == 0 else 2], False, True)
+            if last:
+                weave_h("V", 0, 0, 4)
+            elif p > 0:
+                pass
             if p > 0:
-                weave("S", "dp0", 3 * p - 3, 3 * p)
-            if not last:
-                weave("V", adj_key(q + 1, 0), 0 if p == 0 else 4, 8)
-                quant("dpT%d" % p)
-                weave("V", adj_key(q + 1, 1), 4, 8)
-                quant(adj_key(q + 1, 0))
+                pass
+            quant("dpT%d" % p)
+            if p == 0:
+                weave("V", nxt[1])
+                quant(nxt[0], nxt[1])
+            else:
+                quant2(nxt[0], nxt[1])
 
-        weave("V", "dp0", 6, 8)
-        quant("h0")
-        weave("V", "h1", 0, 4)
-        quant("dpT2")
-        dh4(2, 4)
+        dh4(2, (4, 5, 6, 7))
         for t in range(J):
             dp_exit("S", 3, t)
         turn2("dpT3", 0)
-        weave("V", "h1", 4, 8)
-        quant("dp0")
-        weave("V", "dp1")
-        for t in range(3):
-            dh_exit("S", 2, t)
-        for ft in range(J):
-            dw(0, ft, 2 + ft)
-        quant("h1")
-        weave("V", "dp2", 0, 4)
-        quant("dp1")
-        for ft in range(J):
-            dw(1, ft, None)
+        weave("V", "dp2", 7, 8)
+
+        quant("h0", "dp2")
+        dw(0, [0, 1, 2], 2)
+        dh_exit("S", 2, 0)
         turned2("S", "dpT3")
-        dh_exit("S", 2, 3)
-        weave("V", "dp2", 4, 8)
+        for t in (1, 2, 3):
+            dh_exit("S", 2, t)
+        weave_h("V", 1)
         quant("dpT3")
-        for t in range(J):
-            dh(3, t, (6, 0, 1, 7)[t])
-        weave("S", "h2", 0, 4)
+        dh4(3, (3, 4, 0, 1))
+        quant("h1")
+        dw(1, [0, 1, 2], 5)
+        weave_h("S", 2, 2, 4)
         weave("V", "dp3")
-        quant("dp2")
+        weave_h("V", 2, 0, 2)
+        quant("dp3")
+        dw(0, [3], 2)
+        dw(1, [3], 5)
+        quant("h2")
+        dw(2, range(G), 6)
         for t in range(J):
             dh_exit("S", 3, t)
-        weave("V", "h3", 0, 4)
-        quant_part("h2", 0, 2)
-        dw(2, 0, None)
-        dw(2, 1, None)
-        quant("dp3")
-        quant_part("h3", 0, 2)
-        dw(3, 0, None, True)
-        dw(3, 1, None, True)
-        weave("V", "h2", 4, 8)
-        weave("S", "h3", 4, 8)
+        weave_h("V", 3, 0, 2)
+
         dw_exit("S", 0)
-        quant_part("h2", 2, 4)
+        weave_h("V", 3, 2, 4)
+        quant_part("h3", 0, 2)
+        dw(3, [0, 1], 7)
         quant_part("h3", 2, 4)
-        for q in (2, 3):
-            for ft in (2, 3):
-                dw(q, ft, None, q == 3)
-        dw_exit("V", 1)
+        dw(3, [2, 3], 7)
+        dw_exit("S", 1)
         dw_exit("S", 2)
         dw_exit("V", 3)

@@ -17,7 +17,7 @@ P, J = 128, 4
 GROUP = P * J
 G = N // GROUP
 
-RAW_BUFS, WIDE_BUFS, CODE_BUFS, OUT_BUFS, ALIGN = 14, 10, 10, 10, 64
+RAW_BUFS, WIDE_BUFS, CODE_BUFS, OUT_BUFS, ALIGN = 15, 10, 10, 8, 64
 
 WIDTH = J * GROUP
 SHARED = [("r_dy%d" % g, "r_dz%d" % g) for g in range(G)] + [("g_dz%d" % g, "g_a0_%d" % g) for g in range(G)]
@@ -59,11 +59,12 @@ def tile_sage_re_pb_v_kernel(tc, h, adj, w, rw, b, y, dis, nnz, grad_out, out_0,
         ident16 = keep.tile([P, P], BF16, name="ident16")
         make_identity(nc, ident16[:])
 
-        h_all = keep.tile([P, G, J, F], BF16, name="h_all")
+        y_mid = work.tile([P, 2, J, F], F32, name="y_mid", tag="big", bufs=1)
+        late = {}
         y_t, go_t, rows = {}, {}, {}
         grp, codes, bank = {}, {}, {}
         free = {"raw": list(range(RAW_BUFS)), "wide": list(range(WIDE_BUFS)), "code": list(range(CODE_BUFS))}
-        held, users, waiting, wide, pairs = {}, {}, [], {}, {}
+        held, users, waiting, wide, pairs = {}, {"y_mid": 99}, [], {}, {}
 
         def take(kind, name, n_users):
             i = free[kind].pop(0)
@@ -140,8 +141,14 @@ def tile_sage_re_pb_v_kernel(tc, h, adj, w, rw, b, y, dis, nnz, grad_out, out_0,
             nc.sync.dma_start(out=t[:], in_=src)
             rows[key] = t[:]
 
+        def load_y_whole(g):
+            nc.sync.dma_start(out=y_mid[:, g - 1], in_=y_v[g])
+            y_t[g, 0] = (y_mid[:, g - 1], "y_mid")
+
         def load_h(g):
-            nc.sync.dma_start(out=h_all[:, g], in_=h_v[g])
+            if g == 0:
+                late["h"] = work.tile([P, G, J, F], BF16, name="h_all", tag="big", bufs=1)
+            nc.sync.dma_start(out=late["h"][:, g], in_=h_v[g])
 
         def load_adj(q, g):
             load_rows("a%d_%d" % (q, g), adj_v[g][:, :, q * GROUP : (q + 1) * GROUP])
@@ -188,6 +195,9 @@ def tile_sage_re_pb_v_kernel(tc, h, adj, w, rw, b, y, dis, nnz, grad_out, out_0,
                 if key[0] == "a":
                     dst = grp[key].rearrange("p (t m j) -> p t m j", t=J, j=J)[:, :, part, :]
                     src = bank[key, half][:].rearrange("p (m t j) -> p t m j", t=J, j=J)
+                elif key[:2] == "dp":
+                    dst = grp[key][:, half * WIDTH // 2 : (half + 1) * WIDTH // 2]
+                    src = bank[key, half][:]
                 else:
                     dst = grp[key].rearrange("p (u w x) -> p u w x", u=2, x=2 * J)[:, :, part, :]
                     src = bank[key, half][:].rearrange("p (w u x) -> p u w x", u=2, x=2 * J)
@@ -224,7 +234,7 @@ def tile_sage_re_pb_v_kernel(tc, h, adj, w, rw, b, y, dis, nnz, grad_out, out_0,
             if key not in grp:
                 new_group(key)
             dst = grp[key].rearrange("p (g c i t) -> p g c t i", g=G, i=2, t=J)
-            src = h_all[:, :, :, ft * P : (ft + 1) * P].rearrange("p g t (c i) -> p g c t i", i=2)
+            src = late["h"][:, :, :, ft * P : (ft + 1) * P].rearrange("p g t (c i) -> p g c t i", i=2)
             copy_on(engine, dst[:, lo:hi], src[:, lo:hi])
 
         def quant_part(key, lo, hi):
@@ -305,10 +315,21 @@ def tile_sage_re_pb_v_kernel(tc, h, adj, w, rw, b, y, dis, nnz, grad_out, out_0,
             for t in range(J):
                 mm(bank["dh", q, t], "dpT%d" % q, t, "w0", False, True)
 
+        def out_tile(name, early):
+            if early:
+                return work.tile([P, F], F32, name=name, tag="out", bufs=OUT_BUFS)
+            return take_raw(name, [P, F], F32, 1)
+
         def dh_exit(engine, q, t):
-            tile = work.tile([P, F], F32, name="o0_%d_%d" % (q, t), tag="out", bufs=OUT_BUFS)
+            tile = out_tile("o0_%d_%d" % (q, t), q < 2)
             copy_on(engine, tile[:], bank["dh", q, t][:])
             nc.sync.dma_start(out=out0_v[q][:, t, :], in_=tile[:])
+
+        def dh_exit2(engine, q, t):
+            tile = take_raw("o0_%d_%d" % (q, t), [P, 2, F], F32, 1)
+            for i in range(2):
+                copy_on(engine, tile[:, i, :], bank["dh", q, t + i][:])
+            nc.sync.dma_start(out=out0_v[q][:, t : t + 2, :], in_=tile[:])
 
         def dw(ft, qs, i):
             for q in qs:
@@ -316,10 +337,13 @@ def tile_sage_re_pb_v_kernel(tc, h, adj, w, rw, b, y, dis, nnz, grad_out, out_0,
                     new_bank(("dw", ft), i)
                 mm(bank["dw", ft], "h%d" % ft, q, "dp%d" % q, q == 0, q == G - 1)
 
-        def dw_exit(engine, ft):
-            t = work.tile([P, F], F32, name="o1_%d" % ft, tag="out", bufs=OUT_BUFS)
-            copy_on(engine, t[:].rearrange("p (w u e) -> p w u e", u=2, e=2), bank["dw", ft][:].rearrange("p (u w e) -> p w u e", u=2, e=2))
-            nc.sync.dma_start(out=out1_v[:, ft, :], in_=t[:])
+        def dw_exit(engine, ft, parts=1):
+            t = out_tile("o1_%d" % ft, False)
+            dst = t[:].rearrange("p (w u e) -> p w u e", u=2, e=2)
+            src = bank["dw", ft][:].rearrange("p (u w e) -> p w u e", u=2, e=2)
+            for i in range(parts):
+                copy_on(engine, dst[:, i * P // parts : (i + 1) * P // parts], src[:, i * P // parts : (i + 1) * P // parts])
+                nc.sync.dma_start(out=out1_v[:, ft, i * F // parts : (i + 1) * F // parts], in_=t[:, i * F // parts : (i + 1) * F // parts])
 
         def turn2(key, i):
             turn(key, 0, i)
@@ -339,12 +363,10 @@ def tile_sage_re_pb_v_kernel(tc, h, adj, w, rw, b, y, dis, nnz, grad_out, out_0,
         def later(fn, *args):
             waiting.append(lambda: fn(*args))
 
-        later(load_y, 0, 0, 1)
-        later(load_go, 0, 0, 2)
+        later(load_y, 0, 0, 2)
+        later(load_go, 0, 0, 4)
         later(small_loads)
-        later(load_y, 0, 1, 1)
         later(load_y, 0, 2, 2)
-        later(load_go, 0, 2, 2)
         for g in (1, 2):
             later(load_y, g, 0, 2)
             later(load_go, g, 0, 4)
@@ -368,15 +390,16 @@ def tile_sage_re_pb_v_kernel(tc, h, adj, w, rw, b, y, dis, nnz, grad_out, out_0,
             later(load_h, g)
         issue_loads()
 
-        mask(0, 0, 1)
-        mask(0, 1, 1)
+        mask(0, 0, 2)
         node_factors()
         turn("dyT0", 0, 4)
-        scale(0, 0, 1)
-        turned("S", "dyT0", 0)
         mask(0, 2, 2)
+        scale(0, 0, 1)
+
+        turned("S", "dyT0", 0)
         turn("dyT0", 1, 5)
         scale(0, 2, 3)
+
         turned("S", "dyT0", 1)
         weave("S", "dz0")
         for g in (1, 2):
@@ -408,11 +431,12 @@ def tile_sage_re_pb_v_kernel(tc, h, adj, w, rw, b, y, dis, nnz, grad_out, out_0,
         quant("dz2")
         scale(3, 2, 3)
         spread("dz3", 1, 6)
-        turn("dyT3", 1, 5)
         turned("S", "dyT3", 0)
         weave("S", "a0_3", 0, 4)
         quant("a0_2")
         da(0, [2], False, False)
+        turn("w1", 0, 5)
+        turn("w1", 1, 4)
         weave("V", "a0_3", 4, 8)
         spread_exit("dz3")
         weave("V", "a1_0", 0, 2)
@@ -421,12 +445,13 @@ def tile_sage_re_pb_v_kernel(tc, h, adj, w, rw, b, y, dis, nnz, grad_out, out_0,
         quant("dz3")
         da(0, [3], False, True)
 
-        turned("S", "dyT3", 1)
         weave("S", "a1_0", 4, 8)
-        quant2("dyT2", "dyT3")
-        quant("a1_0")
+
+        quant("dyT2", "a1_0")
+        turn2("w0", 6)
+        turned2("S", "w1")
+        turn("dyT3", 1, 5)
         weave("V", "a1_1")
-        turn2("w1", 6)
         for q in range(1, G):
             p = q - 1
             last = q == G - 1
@@ -436,21 +461,19 @@ def tile_sage_re_pb_v_kernel(tc, h, adj, w, rw, b, y, dis, nnz, grad_out, out_0,
             for t in range(J):
                 dp_exit("S", p, t)
                 da(q, [0], True, False, [t])
-                if p == 0 and t == 1:
-                    turn2("w0", 4)
             if p > 0:
                 weave("V", adj_key(q, 3), 7, 8)
             weave("V", adj_key(q, 2))
             if p == 0:
                 quant("a1_1")
-                turned2("S", "w1")
-            else:
-                dh_exit("S", p - 1, 2)
-                dh_exit("S", p - 1, 3)
-            da(q, [1], False, False)
-            turn2("dpT%d" % p, 6)
-            if p == 0:
+                turned("S", "dyT3", 1)
                 turned2("S", "w0")
+            else:
+                dh_exit("S", p - 1, 0)
+                dh_exit("S", p - 1, 1)
+            da(q, [1], False, False)
+            turn2("dpT%d" % p, 4)
+            if p == 0:
                 weave("V", "a1_3", 0, 4)
                 quant("a1_2")
                 weave("S", "a1_3", 4, 8)
@@ -458,10 +481,10 @@ def tile_sage_re_pb_v_kernel(tc, h, adj, w, rw, b, y, dis, nnz, grad_out, out_0,
                 quant("a1_3")
                 quant2("w0", "w1")
             else:
-                dh_exit("S", p - 1, 0)
-                dh_exit("S", p - 1, 1)
+                dh_exit("S", p - 1, 2)
+                dh_exit("S", p - 1, 3)
                 quant(adj_key(q, 3), adj_key(q, 2))
-                weave("V", nxt[0], 0 if last else 0, 8)
+                weave("V", nxt[0])
                 weave("V", nxt[1])
             weave("S", nxt[2], 0, 4 if p > 0 else 2)
             turned2("S", "dpT%d" % p)
@@ -469,11 +492,9 @@ def tile_sage_re_pb_v_kernel(tc, h, adj, w, rw, b, y, dis, nnz, grad_out, out_0,
             da(q, [2 if p == 0 else 3], False, False)
             da(q, [3 if p == 0 else 2], False, True)
             if last:
-                weave_h("V", 0, 0, 4)
+                weave_h("V", 0, 0, 2)
             elif p > 0:
-                pass
-            if p > 0:
-                pass
+                quant("dyT3")
             quant("dpT%d" % p)
             if p == 0:
                 weave("V", nxt[1])
@@ -486,27 +507,29 @@ def tile_sage_re_pb_v_kernel(tc, h, adj, w, rw, b, y, dis, nnz, grad_out, out_0,
             dp_exit("S", 3, t)
         turn2("dpT3", 0)
         weave("V", "dp2", 7, 8)
-
-        quant("h0", "dp2")
+        weave_h("V", 0, 2, 4)
+        quant("dp2", "h0")
         dw(0, [0, 1, 2], 2)
-        dh_exit("S", 2, 0)
+        for t in range(2):
+            dh_exit("S", 2, t)
         turned2("S", "dpT3")
-        for t in (1, 2, 3):
+        for t in range(2, J):
             dh_exit("S", 2, t)
         weave_h("V", 1)
         quant("dpT3")
         dh4(3, (3, 4, 0, 1))
         quant("h1")
         dw(1, [0, 1, 2], 5)
-        weave_h("S", 2, 2, 4)
+        weave_h("S", 2, 1, 4)
         weave("V", "dp3")
-        weave_h("V", 2, 0, 2)
+        weave_h("V", 2, 0, 1)
         quant("dp3")
         dw(0, [3], 2)
         dw(1, [3], 5)
+
         quant("h2")
         dw(2, range(G), 6)
-        for t in range(J):
+        for t in range(0, J):
             dh_exit("S", 3, t)
         weave_h("V", 3, 0, 2)
 
@@ -517,5 +540,5 @@ def tile_sage_re_pb_v_kernel(tc, h, adj, w, rw, b, y, dis, nnz, grad_out, out_0,
         quant_part("h3", 2, 4)
         dw(3, [2, 3], 7)
         dw_exit("S", 1)
-        dw_exit("S", 2)
-        dw_exit("V", 3)
+        dw_exit("V", 2)
+        dw_exit("S", 3)

@@ -377,8 +377,8 @@ def tile_sage_re_pb_v_kernel(tc, h, adj, w, rw, b, y, dis, nnz, grad_out, out_0,
         later(load_adj, 0, 2)
         later(load_y, 3, 2, 2)
         later(load_adj, 0, 3)
-        later(load_adj, 1, 0)
         later(load_rows, "w1", w_v[1])
+        later(load_adj, 1, 0)
         later(load_rows, "w0", w_v[0])
         later(load_adj, 1, 1)
         later(load_adj, 1, 2)
@@ -425,33 +425,31 @@ def tile_sage_re_pb_v_kernel(tc, h, adj, w, rw, b, y, dis, nnz, grad_out, out_0,
         quant("a0_1")
         da(0, [1], False, False)
         scale(3, 0, 1)
-        spread("dz3", 0, 6)
         weave("S", "a0_2")
         mask(3, 2, 2)
+        turn("dyT3", 1, 5)
         quant("dz2")
         scale(3, 2, 3)
-        spread("dz3", 1, 6)
         turned("S", "dyT3", 0)
-        weave("S", "a0_3", 0, 4)
+        weave("S", "a0_3", 0, 7)
         quant("a0_2")
         da(0, [2], False, False)
-        turn("w1", 0, 5)
-        turn("w1", 1, 4)
-        weave("V", "a0_3", 4, 8)
-        spread_exit("dz3")
-        weave("V", "a1_0", 0, 2)
-        quant("a0_3")
-        weave("V", "a1_0", 2, 4)
-        quant("dz3")
+        turn2("w1", 6)
+        weave("V", "dz3")
+        weave("V", "a0_3", 7, 8)
+        quant("dz3", "a0_3")
         da(0, [3], False, True)
 
-        weave("S", "a1_0", 4, 8)
 
-        quant("dyT2", "a1_0")
-        turn2("w0", 6)
+        turned("S", "dyT3", 1)
+        turn2("w0", 4)
+        weave("S", "a1_0", 4, 8)
         turned2("S", "w1")
-        turn("dyT3", 1, 5)
-        weave("V", "a1_1")
+        weave("V", "a1_0", 0, 4)
+        weave("V", "a1_1", 0, 4)
+        quant("a1_0")
+        weave("V", "a1_1", 4, 8)
+        quant("dyT2", "a1_1")
         for q in range(1, G):
             p = q - 1
             last = q == G - 1
@@ -465,18 +463,16 @@ def tile_sage_re_pb_v_kernel(tc, h, adj, w, rw, b, y, dis, nnz, grad_out, out_0,
                 weave("V", adj_key(q, 3), 7, 8)
             weave("V", adj_key(q, 2))
             if p == 0:
-                quant("a1_1")
-                turned("S", "dyT3", 1)
                 turned2("S", "w0")
             else:
                 dh_exit("S", p - 1, 0)
                 dh_exit("S", p - 1, 1)
             da(q, [1], False, False)
-            turn2("dpT%d" % p, 4)
+            turn2("dpT%d" % p, 6 if p == 0 else 4)
             if p == 0:
-                weave("V", "a1_3", 0, 4)
+                weave("V", "a1_3", 0, 2)
                 quant("a1_2")
-                weave("S", "a1_3", 4, 8)
+                weave("S", "a1_3", 2, 8)
                 weave("V", nxt[0])
                 quant("a1_3")
                 quant2("w0", "w1")
@@ -502,43 +498,52 @@ def tile_sage_re_pb_v_kernel(tc, h, adj, w, rw, b, y, dis, nnz, grad_out, out_0,
             else:
                 quant2(nxt[0], nxt[1])
 
-        dh4(2, (4, 5, 6, 7))
+        for t in range(J):
+            new_bank(("dh", 2, t), J + t)
+            mm(bank["dh", 2, t], "dyT2", t, "w1", True, False)
         for t in range(J):
             dp_exit("S", 3, t)
+        for t in range(2):
+            mm(bank["dh", 2, t], "dpT2", t, "w0", False, True)
         turn2("dpT3", 0)
+        for t in range(2, J):
+            mm(bank["dh", 2, t], "dpT2", t, "w0", False, True)
+
         weave("V", "dp2", 7, 8)
         weave_h("V", 0, 2, 4)
         quant("dp2", "h0")
-        dw(0, [0, 1, 2], 2)
-        for t in range(2):
+        dw(0, [0, 1, 2], 3)
+        for t in range(1):
             dh_exit("S", 2, t)
         turned2("S", "dpT3")
-        for t in range(2, J):
+        for t in range(1, J):
             dh_exit("S", 2, t)
         weave_h("V", 1)
         quant("dpT3")
-        dh4(3, (3, 4, 0, 1))
+        dh4(3, (4, 0, 1, 5))
         quant("h1")
-        dw(1, [0, 1, 2], 5)
-        weave_h("S", 2, 1, 4)
-        weave("V", "dp3")
-        weave_h("V", 2, 0, 1)
-        quant("dp3")
-        dw(0, [3], 2)
-        dw(1, [3], 5)
+        dw(1, [0, 1, 2], 6)
 
+        weave_h("S", 2, 2, 4)
+        weave("V", "dp3", 0, 8)
+        weave_h("V", 2, 0, 2)
+        quant("dp3")
+        dw(0, [3], 3)
+        dw(1, [3], 6)
         quant("h2")
-        dw(2, range(G), 6)
-        for t in range(0, J):
+        dw(2, range(G), 7)
+        for t in range(J):
             dh_exit("S", 3, t)
         weave_h("V", 3, 0, 2)
-
+        weave_h("S", 3, 3, 4)
         dw_exit("S", 0)
-        weave_h("V", 3, 2, 4)
+        weave_h("V", 3, 2, 3)
         quant_part("h3", 0, 2)
-        dw(3, [0, 1], 7)
-        quant_part("h3", 2, 4)
-        dw(3, [2, 3], 7)
+        dw(3, [0, 1], 2)
+        quant_part("h3", 2, 3)
+        dw(3, [2], 2)
+        quant_part("h3", 3, 4)
+        dw(3, [3], 2)
         dw_exit("S", 1)
         dw_exit("V", 2)
-        dw_exit("S", 3)
+        dw_exit("S", 3, 1)

@@ -17,7 +17,13 @@ P, J = 128, 4
 GROUP = P * J
 G = N // GROUP
 
-RAW_BUFS, WIDE_BUFS, CODE_BUFS, OUT_BUFS, ALIGN = 15, 10, 10, 8, 64
+RAW_BUFS, WIDE_BUFS, CODE_BUFS, OUT_BUFS, ALIGN = 15, 10, 10, 8, 256
+SIZE = {"raw": 4096, "wide": 8192, "code": 4096, "scale": 1024}
+START = {"raw": 16384}
+START["wide"] = START["raw"] + RAW_BUFS * SIZE["raw"]
+START["code"] = START["wide"] + WIDE_BUFS * SIZE["wide"]
+START["scale"] = START["code"] + CODE_BUFS * SIZE["code"]
+START["out"] = START["scale"] + CODE_BUFS * SIZE["scale"]
 
 WIDTH = J * GROUP
 SHARED = [("r_dy%d" % g, "r_dz%d" % g) for g in range(G)] + [("g_dz%d" % g, "g_a0_%d" % g) for g in range(G)]
@@ -59,35 +65,38 @@ def tile_sage_re_pb_v_kernel(tc, h, adj, w, rw, b, y, dis, nnz, grad_out, out_0,
         ident16 = keep.tile([P, P], BF16, name="ident16")
         make_identity(nc, ident16[:])
 
-        y_mid = work.tile([P, 2, J, F], F32, name="y_mid", tag="big", bufs=1)
+
         late = {}
         y_t, go_t, rows = {}, {}, {}
         grp, codes, bank = {}, {}, {}
         free = {"raw": list(range(RAW_BUFS)), "wide": list(range(WIDE_BUFS)), "code": list(range(CODE_BUFS))}
-        held, users, waiting, wide, pairs = {}, {"y_mid": 99}, [], {}, {}
+        held, users, waiting, wide, pairs = {}, {}, [], {}, {}
 
         def take(kind, name, n_users):
             i = free[kind].pop(0)
             held[name] = (kind, i)
             users[name] = n_users
-            return "%s%d" % (kind, i)
+            return i
+
+        def place(kind, i, name, shape, dtype):
+            return work.tile(shape, dtype, name=name, tag="%s%d" % (kind, i), bufs=1, align_bytes=ALIGN, offset=START[kind] + i * SIZE[kind])
 
         def take_raw(name, shape, dtype, n_users):
-            return work.tile(shape, dtype, name=name, tag=take("raw", name, n_users), bufs=1, align_bytes=ALIGN)
+            return place("raw", take("raw", name, n_users), name, shape, dtype)
 
         def half_of(key, n_users):
             name, i = PLACE[key]
             if name not in wide:
-                wide[name] = work.tile([P, 2 * WIDTH], BF16, name=name, tag=take("wide", name, 2), bufs=1, align_bytes=ALIGN)
+                wide[name] = place("wide", take("wide", name, 2), name, [P, 2 * WIDTH], BF16)
             users[key] = n_users
             return wide[name][:, i * WIDTH : (i + 1) * WIDTH]
 
         def code_pair(key):
             name, i = CODE_PLACE[key]
             if name not in pairs:
-                tag = take("code", name, 2)
-                c = work.tile([P, 2 * GROUP], U32, name=name, tag=tag, bufs=1, align_bytes=ALIGN)
-                s = work.tile([P, 2 * GROUP], U8, name=name + "s", tag=tag + "s", bufs=1, align_bytes=ALIGN)
+                slot = take("code", name, 2)
+                c = place("code", slot, name, [P, 2 * GROUP], U32)
+                s = place("scale", slot, name + "s", [P, 2 * GROUP], U8)
                 pairs[name] = (c, s)
             if key not in codes:
                 cols = slice(i * GROUP, (i + 1) * GROUP)
@@ -141,13 +150,9 @@ def tile_sage_re_pb_v_kernel(tc, h, adj, w, rw, b, y, dis, nnz, grad_out, out_0,
             nc.sync.dma_start(out=t[:], in_=src)
             rows[key] = t[:]
 
-        def load_y_whole(g):
-            nc.sync.dma_start(out=y_mid[:, g - 1], in_=y_v[g])
-            y_t[g, 0] = (y_mid[:, g - 1], "y_mid")
-
         def load_h(g):
             if g == 0:
-                late["h"] = work.tile([P, G, J, F], BF16, name="h_all", tag="big", bufs=1)
+                late["h"] = work.tile([P, G, J, F], BF16, name="h_all", bufs=1, align_bytes=ALIGN, offset=0)
             nc.sync.dma_start(out=late["h"][:, g], in_=h_v[g])
 
         def load_adj(q, g):
@@ -317,7 +322,7 @@ def tile_sage_re_pb_v_kernel(tc, h, adj, w, rw, b, y, dis, nnz, grad_out, out_0,
 
         def out_tile(name, early):
             if early:
-                return work.tile([P, F], F32, name=name, tag="out", bufs=OUT_BUFS)
+                return work.tile([P, F], F32, name=name, tag="out", bufs=OUT_BUFS, align_bytes=ALIGN, offset=START["out"])
             return take_raw(name, [P, F], F32, 1)
 
         def dh_exit(engine, q, t):

@@ -230,7 +230,9 @@ def tile_sage_re_pb_v_kernel(tc, h, adj, w, rw, b, y, dis, nnz, grad_out, out_0,
                 dst = grp[key].rearrange("p (c i t) -> p c t i", i=2, t=J)
                 src = rows[key].rearrange("p t (c i) -> p c t i", i=2)
             n = dst.shape[1]
-            copy_on(engine, dst[:, lo * n // 8 : hi * n // 8], src[:, lo * n // 8 : hi * n // 8])
+            cuts = (lo, hi - 2, hi) if engine == "V" and (hi - lo) % 4 == 0 else (lo, hi)
+            for x, z in zip(cuts, cuts[1:]):
+                copy_on(engine, dst[:, x * n // 8 : z * n // 8], src[:, x * n // 8 : z * n // 8])
             for i in range(lo, hi):
                 used("r_" + key)
 
@@ -240,7 +242,11 @@ def tile_sage_re_pb_v_kernel(tc, h, adj, w, rw, b, y, dis, nnz, grad_out, out_0,
                 new_group(key)
             dst = grp[key].rearrange("p (g c i t) -> p g c t i", g=G, i=2, t=J)
             src = late["h"][:, :, :, ft * P : (ft + 1) * P].rearrange("p g t (c i) -> p g c t i", i=2)
-            copy_on(engine, dst[:, lo:hi], src[:, lo:hi])
+            if engine == "V":
+                for g in range(lo, hi):
+                    copy_on(engine, dst[:, g], src[:, g])
+            else:
+                copy_on(engine, dst[:, lo:hi], src[:, lo:hi])
 
         def quant_part(key, lo, hi):
             code_pair(key)

@@ -227,8 +227,8 @@ def tile_sage_re_pb_v_kernel(tc, h, adj, w, rw, b, y, dis, nnz, grad_out, out_0,
                 dst = grp[key].rearrange("p (u w e t) -> p w u t e", u=2, e=2, t=J)
                 src = rows[key].rearrange("p t (w u e) -> p w u t e", u=2, e=2)
             else:
-                dst = grp[key].rearrange("p (c i t) -> p c t i", i=2, t=J)
-                src = rows[key].rearrange("p t (c i) -> p c t i", i=2)
+                dst = grp[key].rearrange("p (c i v f) -> p c v i f", i=8, v=2, f=2)
+                src = rows[key].rearrange("p (v f) (c i) -> p c v i f", i=8, v=2)
             n = dst.shape[1]
             cuts = (lo, hi - 2, hi) if engine == "V" and (hi - lo) % 4 == 0 else (lo, hi)
             for x, z in zip(cuts, cuts[1:]):
@@ -240,13 +240,10 @@ def tile_sage_re_pb_v_kernel(tc, h, adj, w, rw, b, y, dis, nnz, grad_out, out_0,
             key = "h%d" % ft
             if key not in grp:
                 new_group(key)
-            dst = grp[key].rearrange("p (g c i t) -> p g c t i", g=G, i=2, t=J)
-            src = late["h"][:, :, :, ft * P : (ft + 1) * P].rearrange("p g t (c i) -> p g c t i", i=2)
-            if engine == "V":
-                for g in range(lo, hi):
-                    copy_on(engine, dst[:, g], src[:, g])
-            else:
-                copy_on(engine, dst[:, lo:hi], src[:, lo:hi])
+            dst = grp[key].rearrange("p (g c i v f) -> p g c v i f", g=G, i=8, v=2, f=2)
+            src = late["h"][:, :, :, ft * P : (ft + 1) * P].rearrange("p g (v f) (c i) -> p g c v i f", i=8, v=2)
+            for g in range(lo, hi):
+                copy_on(engine, dst[:, g], src[:, g])
 
         def quant_part(key, lo, hi):
             code_pair(key)

@@ -17,7 +17,7 @@ P, J = 128, 4
 GROUP = P * J
 G = N // GROUP
 
-RAW_BUFS, WIDE_BUFS, CODE_BUFS, OUT_BUFS, ALIGN = 15, 10, 10, 8, 256
+RAW_BUFS, WIDE_BUFS, CODE_BUFS, OUT_BUFS, ALIGN = 15, 10, 10, 8, 1024
 SIZE = {"raw": 4096, "wide": 8192, "code": 4096, "scale": 1024}
 START = {"raw": 16384}
 START["wide"] = START["raw"] + RAW_BUFS * SIZE["raw"]
@@ -55,14 +55,14 @@ def tile_sage_re_pb_v_kernel(tc, h, adj, w, rw, b, y, dis, nnz, grad_out, out_0,
         psum = ctx.enter_context(tc.psum_pool(name="psum", bufs=1))
         ctx.enter_context(tc.manual_schedule())
 
-        dis_t = keep.tile([P, G, J], F32, name="dis_t")
-        flat = keep.tile([P, GROUP], F32, name="flat")
-        rinv = keep.tile([P, G, J], F32, name="rinv")
+        dis_t = keep.tile([P, G, J], F32, name="dis_t", align_bytes=256)
+        flat = keep.tile([P, GROUP], F32, name="flat", align_bytes=256)
+        rinv = keep.tile([P, G, J], F32, name="rinv", align_bytes=256)
         nc.gpsimd.memset(flat[:], 0.0)
-        ratio = keep.tile([P, G, J], F32, name="ratio")
-        ident = keep.tile([P, P], F32, name="ident")
+        ratio = keep.tile([P, G, J], F32, name="ratio", align_bytes=256)
+        ident = keep.tile([P, P], F32, name="ident", align_bytes=256)
         make_identity(nc, ident[:])
-        ident16 = keep.tile([P, P], BF16, name="ident16")
+        ident16 = keep.tile([P, P], BF16, name="ident16", align_bytes=256)
         make_identity(nc, ident16[:])
 
 
@@ -129,8 +129,12 @@ def tile_sage_re_pb_v_kernel(tc, h, adj, w, rw, b, y, dis, nnz, grad_out, out_0,
                 nc.tensor.transpose(bk[:, j * P : (j + 1) * P], flat[:, j:GROUP:J], ident[:])
             cols = bk[:].rearrange("p (j r) -> p r j", j=J)
             nc.vector.reciprocal(out=rinv[:], in_=cols[:, G : 2 * G, :])
+            turn("dyT0", 0, 4)
+            mask(0, 2, 2)
             nc.vector.tensor_tensor(out=ratio[:], in0=cols[:, 0:G, :], in1=rinv[:], op=ALU.mult)
-            nc.scalar.copy(out=dis_t[:], in_=cols[:, 0:G, :])
+
+        def node_dis():
+            nc.scalar.copy(out=dis_t[:], in_=bank["nodes"][:].rearrange("p (j r) -> p r j", j=J)[:, 0:G, :])
 
         def load_y(g, t0, n):
             name = "y_%d_%d" % (g, t0)
@@ -387,8 +391,8 @@ def tile_sage_re_pb_v_kernel(tc, h, adj, w, rw, b, y, dis, nnz, grad_out, out_0,
         later(load_adj, 0, 3)
         later(load_rows, "w1", w_v[1])
         later(load_adj, 1, 0)
-        later(load_rows, "w0", w_v[0])
         later(load_adj, 1, 1)
+        later(load_rows, "w0", w_v[0])
         later(load_adj, 1, 2)
         later(load_adj, 1, 3)
         for q in (2, 3):
@@ -400,64 +404,76 @@ def tile_sage_re_pb_v_kernel(tc, h, adj, w, rw, b, y, dis, nnz, grad_out, out_0,
 
         mask(0, 0, 2)
         node_factors()
-        turn("dyT0", 0, 4)
-        mask(0, 2, 2)
         scale(0, 0, 1)
 
         turned("S", "dyT0", 0)
         turn("dyT0", 1, 5)
         scale(0, 2, 3)
 
+        node_dis()
         turned("S", "dyT0", 1)
         weave("S", "dz0")
         for g in (1, 2):
             mask(g, 0, 2)
             turn("dyT%d" % g, 0, 4)
-            quant("dyT0" if g == 1 else "a0_0")
-            scale(g, 0, 1)
-            spread("dz%d" % g, 0, 6)
+            quant("dyT%d" % (g - 1))
+            if g == 2:
+                scale(g, 0, 1)
+                spread("dz%d" % g, 0, 6)
             turned("S", "dyT%d" % g, 0)
             mask(g, 2, 2)
             turn("dyT%d" % g, 1, 5)
-            quant("dz%d" % (g - 1))
+            if g == 2:
+                quant("dz1")
+            else:
+                scale(g, 0, 1)
+                spread("dz%d" % g, 0, 6)
             scale(g, 2, 3)
             spread("dz%d" % g, 1, 6)
-            weave("S", adj_key(0, g - 1))
+            if g == 1:
+                quant("dz0")
             if g == 2:
-                quant("dyT1")
+                weave("S", "a0_1", 2, 8)
+                quant("a0_0")
                 da(0, [0], True, False)
-            turned("V", "dyT%d" % g, 1)
+                weave("V", "a0_1", 0, 2)
+            else:
+                weave("S", "a0_0")
+            if g == 1:
+                turned("V", "dyT1", 1)
             spread_exit("dz%d" % g)
         mask(3, 0, 2)
+        turned("V", "dyT2", 1)
         turn("dyT3", 0, 4)
         quant("a0_1")
-        da(0, [1], False, False)
+        da(0, [1], False, False, [0, 1])
         scale(3, 0, 1)
+        quant("dyT2")
         weave("S", "a0_2")
         mask(3, 2, 2)
         turn("dyT3", 1, 5)
+        da(0, [1], False, False, [2, 3])
         quant("dz2")
         scale(3, 2, 3)
-        turned("S", "dyT3", 0)
-        weave("S", "a0_3", 0, 7)
+        weave("S", "a0_3")
         quant("a0_2")
         da(0, [2], False, False)
         turn2("w1", 6)
         weave("V", "dz3")
-        weave("V", "a0_3", 7, 8)
-        quant("dz3", "a0_3")
+        quant("a0_3", "dz3")
         da(0, [3], False, True)
 
 
-        turned("S", "dyT3", 1)
+        turned2("S", "dyT3")
         turn2("w0", 4)
-        weave("S", "a1_0", 4, 8)
+        weave("S", "a1_0", 5, 8)
         turned2("S", "w1")
-        weave("V", "a1_0", 0, 4)
+        weave("V", "a1_0", 0, 5)
         weave("V", "a1_1", 0, 4)
         quant("a1_0")
         weave("V", "a1_1", 4, 8)
-        quant("dyT2", "a1_1")
+        weave("V", "a1_2", 0, 2)
+        quant("a1_1")
         for q in range(1, G):
             p = q - 1
             last = q == G - 1
@@ -469,7 +485,7 @@ def tile_sage_re_pb_v_kernel(tc, h, adj, w, rw, b, y, dis, nnz, grad_out, out_0,
                 da(q, [0], True, False, [t])
             if p > 0:
                 weave("V", adj_key(q, 3), 7, 8)
-            weave("V", adj_key(q, 2))
+            weave("V", adj_key(q, 2), 2 if p == 0 else 0, 8)
             if p == 0:
                 turned2("S", "w0")
             else:
@@ -478,9 +494,9 @@ def tile_sage_re_pb_v_kernel(tc, h, adj, w, rw, b, y, dis, nnz, grad_out, out_0,
             da(q, [1], False, False)
             turn2("dpT%d" % p, 6 if p == 0 else 4)
             if p == 0:
-                weave("V", "a1_3", 0, 2)
+                weave("V", "a1_3", 0, 3)
                 quant("a1_2")
-                weave("S", "a1_3", 2, 8)
+                weave("S", "a1_3", 3, 8)
                 weave("V", nxt[0])
                 quant("a1_3")
                 quant2("w0", "w1")

@@ -435,7 +435,7 @@ def tile_sage_re_pb_v_kernel(tc, h, adj, w, rw, b, y, dis, nnz, grad_out, out_0,
             if g == 2:
                 weave("S", "a0_1", 2, 8)
                 quant("a0_0")
-                da(0, [0], True, False)
+                da(0, [0], True, False, [0, 1])
                 weave("V", "a0_1", 0, 2)
             else:
                 weave("S", "a0_0")
@@ -445,10 +445,10 @@ def tile_sage_re_pb_v_kernel(tc, h, adj, w, rw, b, y, dis, nnz, grad_out, out_0,
         mask(3, 0, 2)
         turned("V", "dyT2", 1)
         turn("dyT3", 0, 4)
+        da(0, [0], True, False, [2, 3])
         quant("a0_1")
         da(0, [1], False, False, [0, 1])
         scale(3, 0, 1)
-        quant("dyT2")
         weave("S", "a0_2")
         mask(3, 2, 2)
         turn("dyT3", 1, 5)
@@ -457,8 +457,9 @@ def tile_sage_re_pb_v_kernel(tc, h, adj, w, rw, b, y, dis, nnz, grad_out, out_0,
         scale(3, 2, 3)
         weave("S", "a0_3")
         quant("a0_2")
-        da(0, [2], False, False)
+        da(0, [2], False, False, [0, 1])
         turn2("w1", 6)
+        da(0, [2], False, False, [2, 3])
         weave("V", "dz3")
         quant("a0_3", "dz3")
         da(0, [3], False, True)
@@ -472,8 +473,7 @@ def tile_sage_re_pb_v_kernel(tc, h, adj, w, rw, b, y, dis, nnz, grad_out, out_0,
         weave("V", "a1_1", 0, 4)
         quant("a1_0")
         weave("V", "a1_1", 4, 8)
-        weave("V", "a1_2", 0, 2)
-        quant("a1_1")
+        quant("dyT2", "a1_1")
         for q in range(1, G):
             p = q - 1
             last = q == G - 1
@@ -485,7 +485,7 @@ def tile_sage_re_pb_v_kernel(tc, h, adj, w, rw, b, y, dis, nnz, grad_out, out_0,
                 da(q, [0], True, False, [t])
             if p > 0:
                 weave("V", adj_key(q, 3), 7, 8)
-            weave("V", adj_key(q, 2), 2 if p == 0 else 0, 8)
+            weave("V", adj_key(q, 2))
             if p == 0:
                 turned2("S", "w0")
             else:

from contextlib import ExitStack

import concourse.mybir as mybir
from concourse.masks import make_identity

F32 = mybir.dt.float32
BF16 = mybir.dt.bfloat16
U32 = mybir.dt.uint32
U8 = mybir.dt.uint8
E4M3 = mybir.dt.float8_e4m3fn_x4
E5M2 = mybir.dt.float8_e5m2_x4
ALU = mybir.AluOpType
COPY = mybir.ActivationFunctionType.Copy

N, F = 2048, 512
P, J = 128, 4
GROUP = P * J
G = N // GROUP

RAW_BUFS, WIDE_BUFS, CODE_BUFS, OUT_BUFS, ALIGN = 15, 10, 10, 8, 1024
SIZE = {"raw": 4096, "wide": 8192, "code": 4096, "scale": 1024}
START = {"raw": 16384}
START["wide"] = START["raw"] + RAW_BUFS * SIZE["raw"]
START["code"] = START["wide"] + WIDE_BUFS * SIZE["wide"]
START["scale"] = START["code"] + CODE_BUFS * SIZE["code"]
START["out"] = START["scale"] + CODE_BUFS * SIZE["scale"]

WIDTH = J * GROUP
SHARED = [("r_dy%d" % g, "r_dz%d" % g) for g in range(G)] + [("g_dz%d" % g, "g_a0_%d" % g) for g in range(G)]
SHARED = SHARED + [("r_dp0", "r_dp1"), ("r_dp2", "r_dp3")]
CODED = [("dyT0", "dyT1"), ("dyT2", "dyT3"), ("w0", "w1"), ("dpT0", "dpT1"), ("dpT2", "dpT3"), ("dp0", "dp1"), ("dp2", "dp3"), ("h0", "h1"), ("h2", "h3")]
CODED = CODED + [("a%d_%d" % (q, g), "a%d_%d" % (q, g + 1)) for q in range(1, G) for g in (0, 2)]
SHARED = SHARED + [("g_" + x, "g_" + z) for x, z in CODED]
CODED = CODED + [("dz0", "dz1"), ("dz2", "dz3"), ("a0_0", "a0_1"), ("a0_2", "a0_3")]
PLACE = {key: ("_".join(pair), i) for pair in SHARED for i, key in enumerate(pair)}
CODE_PLACE = {key: ("k_" + "_".join(pair), i) for pair in CODED for i, key in enumerate(pair)}

FLOPS = 2 * N * N * F + 2 * N * 2 * F * F + 2 * N * F * F
BYTES = 2 * (N * F + N * N + 2 * F * F + N * F) + 4 * (N * F + 2 * N) + 4 * (N * F + F * F)


def tile_sage_re_pb_v_kernel(tc, h, adj, w, rw, b, y, dis, nnz, grad_out, out_0, out_1):
    nc = tc.nc
    adj_v = adj.rearrange("(g p j) c -> g p j c", p=P, j=J)
    y_v = y.rearrange("(g p j) o -> g p j o", p=P, j=J)
    go_v = grad_out.rearrange("(g p j) o -> g p j o", p=P, j=J)
    h_v = h.rearrange("(g p j) o -> g p j o", p=P, j=J)
    w_v = [x.rearrange("(p b) o -> p b o", p=P) for x in (w, rw)]
    out0_v = out_0.rearrange("(g p j) f -> g p j f", p=P, j=J)
    out1_v = out_1.rearrange("(b p) f -> p b f", p=P)

    with ExitStack() as ctx:
        keep = ctx.enter_context(tc.tile_pool(name="keep", bufs=1))
        work = ctx.enter_context(tc.tile_pool(name="work", bufs=2))
        psum = ctx.enter_context(tc.psum_pool(name="psum", bufs=1))
        ctx.enter_context(tc.manual_schedule())

        dis_t = keep.tile([P, G, J], F32, name="dis_t", align_bytes=256)
        flat = keep.tile([P, GROUP], F32, name="flat", align_bytes=256)
        rinv = keep.tile([P, G, J], F32, name="rinv", align_bytes=256)
        nc.gpsimd.memset(flat[:], 0.0)
        ratio = keep.tile([P, G, J], F32, name="ratio", align_bytes=256)
        ident = keep.tile([P, P], F32, name="ident", align_bytes=256)
        make_identity(nc, ident[:])
        ident16 = keep.tile([P, P], BF16, name="ident16", align_bytes=256)
        make_identity(nc, ident16[:])


        late = {}
        y_t, go_t, rows = {}, {}, {}
        grp, codes, bank = {}, {}, {}
        free = {"raw": list(range(RAW_BUFS)), "wide": list(range(WIDE_BUFS)), "code": list(range(CODE_BUFS))}
        held, users, waiting, wide, pairs = {}, {}, [], {}, {}

        def take(kind, name, n_users):
            i = free[kind].pop(0)
            held[name] = (kind, i)
            users[name] = n_users
            return i

        def place(kind, i, name, shape, dtype):
            return work.tile(shape, dtype, name=name, tag="%s%d" % (kind, i), bufs=1, align_bytes=ALIGN, offset=START[kind] + i * SIZE[kind])

        def take_raw(name, shape, dtype, n_users):
            return place("raw", take("raw", name, n_users), name, shape, dtype)

        def half_of(key, n_users):
            name, i = PLACE[key]
            if name not in wide:
                wide[name] = place("wide", take("wide", name, 2), name, [P, 2 * WIDTH], BF16)
            users[key] = n_users
            return wide[name][:, i * WIDTH : (i + 1) * WIDTH]

        def code_pair(key):
            name, i = CODE_PLACE[key]
            if name not in pairs:
                slot = take("code", name, 2)
                c = place("code", slot, name, [P, 2 * GROUP], U32)
                s = place("scale", slot, name + "s", [P, 2 * GROUP], U8)
                pairs[name] = (c, s)
            if key not in codes:
                cols = slice(i * GROUP, (i + 1) * GROUP)
                codes[key] = (pairs[name][0][:, cols], pairs[name][1][:, cols], E4M3 if key[0] in "ahw" else E5M2)
                users["c_" + key] = J * G if key[:2] == "dz" or key[0] == "w" else J
            return pairs[name]

        def used(name):
            users[name] = users[name] - 1
            if users[name] > 0:
                return
            if name in held:
                kind, i = held[name]
                free[kind].append(i)
                issue_loads()
            else:
                used(CODE_PLACE[name[2:]][0] if name[:2] == "c_" else PLACE[name][0])

        def issue_loads():
            while waiting and free["raw"]:
                waiting.pop(0)()

        def new_bank(key, i):
            bank[key] = psum.tile([P, 512], F32, name="bank%d" % i, tag="bank%d" % i)
            return bank[key]

        def node_factors():
            bk = new_bank("nodes", 7)
            for j in range(J):
                nc.tensor.transpose(bk[:, j * P : (j + 1) * P], flat[:, j:GROUP:J], ident[:])
            cols = bk[:].rearrange("p (j r) -> p r j", j=J)
            nc.vector.reciprocal(out=rinv[:], in_=cols[:, G : 2 * G, :])
            turn("dyT0", 0, 4)
            mask(0, 2, 2)
            nc.vector.tensor_tensor(out=ratio[:], in0=cols[:, 0:G, :], in1=rinv[:], op=ALU.mult)

        def node_dis():
            nc.scalar.copy(out=dis_t[:], in_=bank["nodes"][:].rearrange("p (j r) -> p r j", j=J)[:, 0:G, :])

        def load_y(g, t0, n):
            name = "y_%d_%d" % (g, t0)
            t = take_raw(name, [P, n, F], F32, n)
            nc.sync.dma_start(out=t[:], in_=y_v[g][:, t0 : t0 + n, :])
            y_t[g, t0] = (t[:], name)

        def load_go(g, t0, n):
            name = "go_%d_%d" % (g, t0)
            t = take_raw(name, [P, n, F], BF16, n)
            nc.sync.dma_start(out=t[:], in_=go_v[g][:, t0 : t0 + n, :])
            for i in range(n):
                go_t[g, t0 + i] = (t, i, name)

        def load_rows(key, src):
            t = take_raw("r_" + key, [P, J, F], BF16, 2 if key[0] == "w" else 8)
            nc.sync.dma_start(out=t[:], in_=src)
            rows[key] = t[:]

        def load_h(g):
            if g == 0:
                late["h"] = work.tile([P, G, J, F], BF16, name="h_all", bufs=1, align_bytes=ALIGN, offset=0)
            nc.sync.dma_start(out=late["h"][:, g], in_=h_v[g])

        def load_adj(q, g):
            load_rows("a%d_%d" % (q, g), adj_v[g][:, :, q * GROUP : (q + 1) * GROUP])

        def mask(g, t0, n):
            if t0 == 0:
                rows["dy%d" % g] = half_of("r_dy%d" % g, 6).rearrange("p (j f) -> p j f", j=J)
            yt, yname = y_t[g, t0]
            gt, i, gname = go_t[g, t0]
            nc.vector.scalar_tensor_tensor(
                out=rows["dy%d" % g][:, t0 : t0 + n, :], in0=yt, scalar=0.0, in1=gt[:, i : i + n, :], op0=ALU.is_gt, op1=ALU.mult
            )
            for t in range(n):
                used(yname)
                used(gname)

        def scale(g, *ts):
            for t in ts:
                if t == 0:
                    rows["dz%d" % g] = half_of("r_dz%d" % g, 8).rearrange("p (j f) -> p j f", j=J)
                nc.vector.tensor_scalar(out=rows["dz%d" % g][:, t, :], in0=rows["dy%d" % g][:, t, :], scalar1=ratio[:, g, t : t + 1], scalar2=None, op0=ALU.mult)
                used("r_dy%d" % g)

        def spread(key, k, i, halves=(0, 1)):
            for half in halves:
                if k == 0:
                    bank[key, half] = psum.tile([P, 2 * GROUP], BF16, name="bank%d" % (i + half), tag="bank%d" % (i + half))
                slots = bank[key, half][:].rearrange("p (c t) -> p t c", t=J)
                cols = slice(half * GROUP // 2, (half + 1) * GROUP // 2)
                nc.tensor.matmul(slots[:, 2 * k : 2 * k + 2, :], lhsT=ident16[:], rhs=rows[key][:, 2 * k : 2 * k + 2, cols], start=True, stop=True)
            for i in range(2 * len(halves)):
                used("r_" + key)

        def spread4(key, i):
            for half in range(2):
                spread(key, 0, i, [half])
                spread(key, 1, i, [half])

        def spread_exit(key, engines="SS", halves=(0, 1)):
            if key not in grp:
                new_group(key)
            for half in halves:
                part = slice(half * P // 2, (half + 1) * P // 2)
                if key[0] == "a":
                    dst = grp[key].rearrange("p (t m j) -> p t m j", t=J, j=J)[:, :, part, :]
                    src = bank[key, half][:].rearrange("p (m t j) -> p t m j", t=J, j=J)
                elif key[:2] == "dp":
                    dst = grp[key][:, half * WIDTH // 2 : (half + 1) * WIDTH // 2]
                    src = bank[key, half][:]
                else:
                    dst = grp[key].rearrange("p (u w x) -> p u w x", u=2, x=2 * J)[:, :, part, :]
                    src = bank[key, half][:].rearrange("p (w u x) -> p u w x", u=2, x=2 * J)
                copy_on(engines[half], dst, src)

        def copy_on(engine, out, in_):
            if engine == "V":
                nc.vector.tensor_copy(out=out, in_=in_)
            else:
                nc.scalar.copy(out=out, in_=in_)

        def new_group(key):
            grp[key] = half_of("g_" + key, 1)

        def weave(engine, key, lo=0, hi=8):
            if key not in grp:
                new_group(key)
            if key[0] == "a":
                dst = grp[key].rearrange("p (t a b j) -> p a t j b", t=J, b=2, j=J)
                src = rows[key].rearrange("p j (a b t) -> p a t j b", b=2, t=J)
            elif key[:2] == "dz":
                dst = grp[key].rearrange("p (u w e t) -> p w u t e", u=2, e=2, t=J)
                src = rows[key].rearrange("p t (w u e) -> p w u t e", u=2, e=2)
            else:
                dst = grp[key].rearrange("p (c i v f) -> p c v i f", i=8, v=2, f=2)
                src = rows[key].rearrange("p (v f) (c i) -> p c v i f", i=8, v=2)
            n = dst.shape[1]
            cuts = (lo, hi - 2, hi) if engine == "V" and (hi - lo) % 4 == 0 else (lo, hi)
            for x, z in zip(cuts, cuts[1:]):
                copy_on(engine, dst[:, x * n // 8 : z * n // 8], src[:, x * n // 8 : z * n // 8])
            for i in range(lo, hi):
                used("r_" + key)

        def weave_h(engine, ft, lo=0, hi=G):
            key = "h%d" % ft
            if key not in grp:
                new_group(key)
            dst = grp[key].rearrange("p (g c i v f) -> p g c v i f", g=G, i=8, v=2, f=2)
            src = late["h"][:, :, :, ft * P : (ft + 1) * P].rearrange("p g (v f) (c i) -> p g c v i f", i=8, v=2)
            for g in range(lo, hi):
                copy_on(engine, dst[:, g], src[:, g])

        def quant_part(key, lo, hi):
            code_pair(key)
            c, s, fmt = codes[key]
            nc.vector.quantize_mx(out=c[:, lo * P : hi * P].bitcast(fmt), scales=s[:, lo * P : hi * P], in_=grp[key][:, lo * GROUP : hi * GROUP])
            if hi == J:
                used("g_" + key)

        def quant(*keys):
            for key in keys:
                code_pair(key)
                c, s, fmt = codes[key]
                nc.vector.quantize_mx(out=c.bitcast(fmt), scales=s, in_=grp[key])
                used("g_" + key)

        def quant2(key0, key1):
            code_pair(key0)
            c, s = code_pair(key1)
            nc.vector.quantize_mx(out=c[:].bitcast(codes[key0][2]), scales=s[:], in_=wide[PLACE["g_" + key0][0]][:])
            used("g_" + key0)
            used("g_" + key1)

        def words(key, t, u):
            row = rows[key.replace("T", "")].bitcast(F32)[:, t, :]
            return row[:, u * P : (u + 1) * P] if key[:2] == "dp" else row[:, u : 2 * P : 2]

        def turn(key, k, i):
            bk = new_bank((key, k), i)
            for s in range(2):
                for u in range(2):
                    nc.tensor.transpose(bk[:, (2 * s + u) * P : (2 * s + u + 1) * P], words(key, 2 * k + s, u), ident[:])
            used("r_" + key.replace("T", ""))

        def turned(engine, key, k):
            if k == 0:
                new_group(key)
            if key[0] == "w":
                dst = grp[key].bitcast(F32).rearrange("p (r b u) -> p r b u", b=J, u=2)[:, :, 2 * k : 2 * k + 2, :]
                copy_on(engine, dst, bank[key, k][:].rearrange("p (s u r) -> p r s u", s=2, u=2))
            else:
                dst = grp[key][:, k * 1024 : (k + 1) * 1024].bitcast(F32).rearrange("p (s r u) -> p s r u", s=2, u=2)
                copy_on(engine, dst, bank[key, k][:].rearrange("p (s u r) -> p s r u", s=2, u=2))

        def mm(out, lhs, t, rhs, start, stop):
            cols = slice(t * P, (t + 1) * P)
            lc, ls, lf = codes[lhs]
            rc, rs, rf = codes[rhs]
            nc.tensor.matmul_mx(out=out[:], lhsT=lc[:, cols].bitcast(lf), lhsT_scale=ls[:, cols], rhs=rc.bitcast(rf), rhs_scale=rs, start=start, stop=stop)
            used("c_" + lhs)
            used("c_" + rhs)

        def da(q, gs, first, last, tiles=range(J)):
            for t in tiles:
                if first:
                    new_bank(("da", q, t), t)
                for g in gs:
                    mm(bank["da", q, t], "a%d_%d" % (q, g), t, "dz%d" % g, first and g == gs[0], last and g == gs[-1])

        def dp_exit(engine, q, t):
            if t == 0:
                rows["dp%d" % q] = half_of("r_dp%d" % q, 10).rearrange("p (j f) -> p j f", j=J)
            out = rows["dp%d" % q][:, t, :]
            if engine == "V":
                nc.vector.tensor_scalar(out=out, in0=bank["da", q, t][:], scalar1=dis_t[:, q, t : t + 1], scalar2=None, op0=ALU.mult)
            else:
                nc.scalar.activation(out=out, in_=bank["da", q, t][:], func=COPY, scale=dis_t[:, q, t : t + 1])

        def dh(q, t, i):
            new_bank(("dh", q, t), i)
            mm(bank["dh", q, t], "dyT%d" % q, t, "w1", True, False)
            mm(bank["dh", q, t], "dpT%d" % q, t, "w0", False, True)

        def dh4(q, i):
            for t in range(J):
                new_bank(("dh", q, t), i[t])
                mm(bank["dh", q, t], "dyT%d" % q, t, "w1", True, False)
            for t in range(J):
                mm(bank["dh", q, t], "dpT%d" % q, t, "w0", False, True)

        def out_tile(name, early):
            if early:
                return work.tile([P, F], F32, name=name, tag="out", bufs=OUT_BUFS, align_bytes=ALIGN, offset=START["out"])
            return take_raw(name, [P, F], F32, 1)

        def dh_exit(engine, q, t):
            tile = out_tile("o0_%d_%d" % (q, t), q < 2)
            copy_on(engine, tile[:], bank["dh", q, t][:])
            nc.sync.dma_start(out=out0_v[q][:, t, :], in_=tile[:])

        def dh_exit2(engine, q, t):
            tile = take_raw("o0_%d_%d" % (q, t), [P, 2, F], F32, 1)
            for i in range(2):
                copy_on(engine, tile[:, i, :], bank["dh", q, t + i][:])
            nc.sync.dma_start(out=out0_v[q][:, t : t + 2, :], in_=tile[:])

        def dw(ft, qs, i):
            for q in qs:
                if q == 0:
                    new_bank(("dw", ft), i)
                mm(bank["dw", ft], "h%d" % ft, q, "dp%d" % q, q == 0, q == G - 1)

        def dw_exit(engine, ft, parts=1):
            t = out_tile("o1_%d" % ft, False)
            dst = t[:].rearrange("p (w u e) -> p w u e", u=2, e=2)
            src = bank["dw", ft][:].rearrange("p (u w e) -> p w u e", u=2, e=2)
            for i in range(parts):
                copy_on(engine, dst[:, i * P // parts : (i + 1) * P // parts], src[:, i * P // parts : (i + 1) * P // parts])
                nc.sync.dma_start(out=out1_v[:, ft, i * F // parts : (i + 1) * F // parts], in_=t[:, i * F // parts : (i + 1) * F // parts])

        def turn2(key, i):
            turn(key, 0, i)
            turn(key, 1, i + 1)

        def turned2(engine, key):
            turned(engine, key, 0)
            turned(engine, key, 1)

        def adj_key(q, g):
            return "a%d_%d" % (q, g)

        def small_loads():
            nc.sync.dma_start(out=flat[0:G, :], in_=dis.rearrange("(g c) -> g c", g=G))
            nc.sync.dma_start(out=flat[G : 2 * G, :], in_=nnz.rearrange("(g c) -> g c", g=G))

        def later(fn, *args):
            waiting.append(lambda: fn(*args))

        later(load_y, 0, 0, 2)
        later(load_go, 0, 0, 4)
        later(small_loads)
        later(load_y, 0, 2, 2)
        for g in (1, 2):
            later(load_y, g, 0, 2)
            later(load_go, g, 0, 4)
            later(load_y, g, 2, 2)
            later(load_adj, 0, g - 1)
        later(load_y, 3, 0, 2)
        later(load_go, 3, 0, 4)
        later(load_adj, 0, 2)
        later(load_y, 3, 2, 2)
        later(load_adj, 0, 3)
        later(load_rows, "w1", w_v[1])
        later(load_adj, 1, 0)
        later(load_adj, 1, 1)
        later(load_rows, "w0", w_v[0])
        later(load_adj, 1, 2)
        later(load_adj, 1, 3)
        for q in (2, 3):
            for g in (0, 3, 1, 2):
                later(load_adj, q, g)
        for g in range(G):
            later(load_h, g)
        issue_loads()

        mask(0, 0, 2)
        node_factors()
        scale(0, 0, 1)

        turned("S", "dyT0", 0)
        turn("dyT0", 1, 5)
        scale(0, 2, 3)

        node_dis()
        turned("S", "dyT0", 1)
        weave("S", "dz0")
        for g in (1, 2):
            mask(g, 0, 2)
            turn("dyT%d" % g, 0, 4)
            quant("dyT%d" % (g - 1))
            if g == 2:
                scale(g, 0, 1)
                spread("dz%d" % g, 0, 6)
            turned("S", "dyT%d" % g, 0)
            mask(g, 2, 2)
            turn("dyT%d" % g, 1, 5)
            if g == 2:
                quant("dz1")
            else:
                scale(g, 0, 1)
                spread("dz%d" % g, 0, 6)
            scale(g, 2, 3)
            spread("dz%d" % g, 1, 6)
            if g == 1:
                quant("dz0")
            if g == 2:
                weave("S", "a0_1", 2, 8)
                quant("a0_0")
                da(0, [0], True, False, [0, 1])
                weave("V", "a0_1", 0, 2)
            else:
                weave("S", "a0_0")
            if g == 1:
                turned("V", "dyT1", 1)
            spread_exit("dz%d" % g)
        mask(3, 0, 2)
        turned("V", "dyT2", 1)
        turn("dyT3", 0, 4)
        da(0, [0], True, False, [2, 3])
        quant("a0_1")
        da(0, [1], False, False, [0, 1])
        scale(3, 0, 1)
        weave("S", "a0_2")
        mask(3, 2, 2)
        turn("dyT3", 1, 5)
        da(0, [1], False, False, [2, 3])
        quant("dz2")
        scale(3, 2, 3)
        weave("S", "a0_3")
        quant("a0_2")
        da(0, [2], False, False, [0, 1])
        turn2("w1", 6)
        da(0, [2], False, False, [2, 3])
        weave("V", "dz3")
        quant("a0_3", "dz3")
        da(0, [3], False, True)


        turned2("S", "dyT3")
        turn2("w0", 4)
        weave("S", "a1_0", 5, 8)
        turned2("S", "w1")
        weave("V", "a1_0", 0, 5)
        weave("V", "a1_1", 0, 4)
        quant("a1_0")
        weave("V", "a1_1", 4, 8)
        quant("dyT2", "a1_1")
        for q in range(1, G):
            p = q - 1
            last = q == G - 1
            nxt = (adj_key(q + 1, 0), adj_key(q + 1, 1), adj_key(q + 1, 3)) if not last else ("dp0", "dp1", "dp2")
            if p > 0:
                dh4(p - 1, (4, 5, 6, 7))
            for t in range(J):
                dp_exit("S", p, t)
                da(q, [0], True, False, [t])
            if p > 0:
                weave("V", adj_key(q, 3), 7, 8)
            weave("V", adj_key(q, 2))
            if p == 0:
                turned2("S", "w0")
            else:
                dh_exit("S", p - 1, 0)
                dh_exit("S", p - 1, 1)
            da(q, [1], False, False)
            turn2("dpT%d" % p, 6 if p == 0 else 4)
            if p == 0:
                weave("V", "a1_3", 0, 3)
                quant("a1_2")
                weave("S", "a1_3", 3, 8)
                weave("V", nxt[0])
                quant("a1_3")
                quant2("w0", "w1")
            else:
                dh_exit("S", p - 1, 2)
                dh_exit("S", p - 1, 3)
                quant(adj_key(q, 3), adj_key(q, 2))
                weave("V", nxt[0])
                weave("V", nxt[1])
            weave("S", nxt[2], 0, 4 if p > 0 else 2)
            turned2("S", "dpT%d" % p)
            weave("S", nxt[2], 4 if p > 0 else 2, 7)
            da(q, [2 if p == 0 else 3], False, False)
            da(q, [3 if p == 0 else 2], False, True)
            if last:
                weave_h("V", 0, 0, 2)
            elif p > 0:
                quant("dyT3")
            quant("dpT%d" % p)
            if p == 0:
                weave("V", nxt[1])
                quant(nxt[0], nxt[1])
            else:
                quant2(nxt[0], nxt[1])

        for t in range(J):
            new_bank(("dh", 2, t), J + t)
            mm(bank["dh", 2, t], "dyT2", t, "w1", True, False)
        for t in range(J):
            dp_exit("S", 3, t)
        for t in range(2):
            mm(bank["dh", 2, t], "dpT2", t, "w0", False, True)
        turn2("dpT3", 0)
        for t in range(2, J):
            mm(bank["dh", 2, t], "dpT2", t, "w0", False, True)

        weave("V", "dp2", 7, 8)
        weave_h("V", 0, 2, 4)
        quant("dp2", "h0")
        dw(0, [0, 1, 2], 3)
        for t in range(1):
            dh_exit("S", 2, t)
        turned2("S", "dpT3")
        for t in range(1, J):
            dh_exit("S", 2, t)
        weave_h("V", 1)
        quant("dpT3")
        dh4(3, (4, 0, 1, 5))
        quant("h1")
        dw(1, [0, 1, 2], 6)

        weave_h("S", 2, 2, 4)
        weave("V", "dp3", 0, 8)
        weave_h("V", 2, 0, 2)
        quant("dp3")
        dw(0, [3], 3)
        dw(1, [3], 6)
        quant("h2")
        dw(2, range(G), 7)
        for t in range(J):
            dh_exit("S", 3, t)
        weave_h("V", 3, 0, 2)
        weave_h("S", 3, 3, 4)
        dw_exit("S", 0)
        weave_h("V", 3, 2, 3)
        quant_part("h3", 0, 2)
        dw(3, [0, 1], 2)
        quant_part("h3", 2, 3)
        dw(3, [2], 2)
        quant_part("h3", 3, 4)
        dw(3, [3], 2)
        dw_exit("S", 1)
        dw_exit("V", 2)
        dw_exit("S", 3, 1)
